import numpy as np
import ml_dtypes


def mxq(x, axis, fmt="e4m3"):
    dtype, down = {"e4m3": (ml_dtypes.float8_e4m3fn, 7), "e5m2": (ml_dtypes.float8_e5m2, 14)}[fmt]
    v = np.moveaxis(np.asarray(x, np.float32).astype(ml_dtypes.bfloat16).astype(np.float64), axis, -1)
    blocks = v.reshape(v.shape[:-1] + (-1, 32))
    amax = np.abs(blocks).max(-1, keepdims=True)
    byte = np.maximum(np.where(amax > 0, np.frexp(amax)[1] - 1 + 127, 0) - down, 1)
    scale = np.exp2(byte - 127.0)
    codes = (blocks / scale).astype(np.float32).astype(dtype).astype(np.float64)
    return np.moveaxis((codes * scale).reshape(v.shape), -1, axis)


WIDE = False


def mx_kscale(k):
    if not WIDE:
        return np.ones(k)
    levels = np.array([10, -10, 5, -5, 0])
    a = np.random.permutation(np.resize(levels, k // 512 * 4)).reshape(k // 512, 4)
    idx = np.arange(k)
    return np.exp2(a[idx // 512, idx % 128 // 32])


BF16 = ml_dtypes.bfloat16


def bf(x):
    return np.asarray(x, np.float32).astype(BF16)


def f64(x):
    return np.asarray(x).astype(np.float64)


B, SQ, SKV, DIN, Q_HEADS, KV_HEADS, DIMS = 2, 2048, 1024, 1024, 4, 1, 512
HEAD_DIM = DIMS // Q_HEADS
REP = Q_HEADS // KV_HEADS


def setup_inputs():
    s = mx_kscale(DIN)
    return {
        "xq": bf(np.random.standard_normal((B, SQ, DIMS)) * 2.0),
        "xk_rep": bf(np.repeat(np.random.standard_normal((B, SKV, KV_HEADS * HEAD_DIM)) * 1.5, REP, axis=-1)),
        "kv": bf(np.random.standard_normal((B, SKV, DIN)) * s),
        "mask": bf(np.random.uniform(0.25, 1.0, (1, 1, SQ, SKV))),
        "Wv": bf(np.random.standard_normal((DIN, KV_HEADS * HEAD_DIM)) / np.sqrt(DIN) / s[:, None]),
    }


def reference(xq, xk_rep, kv, mask, Wv):
    xv = mxq(f64(kv), 2, "e4m3") @ mxq(f64(Wv), 0, "e4m3")
    xv = np.repeat(xv, REP, axis=-1)
    qh = f64(xq).reshape(B, SQ, Q_HEADS, HEAD_DIM).transpose(0, 2, 1, 3)
    kh = f64(xk_rep).reshape(B, SKV, Q_HEADS, HEAD_DIM).transpose(0, 2, 3, 1)
    vh = xv.reshape(B, SKV, Q_HEADS, HEAD_DIM).transpose(0, 2, 1, 3)
    scores = (qh @ kh) * (HEAD_DIM ** -0.5)
    scores = scores - (1.0 / f64(mask) - 1.0)
    e = np.exp(scores - scores.max(-1, keepdims=True))
    out = (mxq(e, 3, "e4m3") @ mxq(vh, 2, "e4m3")) / e.sum(-1, keepdims=True)
    return out.transpose(0, 2, 1, 3).reshape(B, SQ, DIMS)

@@ -1,0 +1,234 @@
+from contextlib import ExitStack
+import math
+
+import concourse.bass as bass
+import concourse.mybir as mybir
+import concourse.tile as tile
+from concourse.masks import make_identity
+
+F32 = mybir.dt.float32
+BF16 = mybir.dt.bfloat16
+U32 = mybir.dt.uint32
+U8 = mybir.dt.uint8
+FP8X4 = mybir.dt.float8_e4m3fn_x4
+ALU = mybir.AluOpType
+ACT = mybir.ActivationFunctionType
+AX = mybir.AxisListType
+
+B, SQ, SKV, DIN, H, HD = 2, 2048, 1024, 1024, 4, 128
+P = 128
+NQT = SQ // P
+NKT = SKV // P
+REP = 4
+DIST = HD // REP
+SCALE = 1.0 / math.sqrt(HD)
+FLOPS = 2 * B * SKV * DIN * HD + 2 * 2 * B * H * SQ * SKV * HD
+
+
+def tile_groupedqueryattention_pa_t_kernel(tc, xq, xk_rep, kv, mask, Wv, out):
+    nc = tc.nc
+    with ExitStack() as ctx:
+        keep = ctx.enter_context(tc.tile_pool(name="keep", bufs=1))
+        ring = ctx.enter_context(tc.tile_pool(name="ring", bufs=2))
+        psum = ctx.enter_context(tc.psum_pool(name="psum", bufs=1))
+
+        mask_v = mask.rearrange("a c (t p) k -> p (a c t) k", p=P)
+        xq_v = xq.rearrange("b (t p) c -> p b t c", p=P)
+        xk_v = xk_rep.rearrange("b (j p) c -> p b j c", p=P)
+        kv_v = kv.rearrange("b (j p) c -> p b j c", p=P)
+
+        ident_bf = keep.tile([P, P], BF16, name="ident_bf")
+        make_identity(nc, ident_bf[:])
+        ident_f = keep.tile([P, P], F32, name="ident_f")
+        make_identity(nc, ident_f[:])
+
+        mask_sb = keep.tile([P, NQT, SKV], BF16, name="mask_sb")
+        y_all = keep.tile([P, NQT, SKV], F32, name="y_all")
+        kT = keep.tile([P, B, H, SKV], BF16, name="kT")
+
+        def load_mask(lo, hi):
+            nc.sync.dma_start(out=mask_sb[:, lo:hi, :], in_=mask_v[:, lo:hi, :])
+
+        def load_xk(b):
+            xk_sb = ring.tile([P, NKT, H * HD], BF16, tag="xk", bufs=1, name="xk_sb")
+            nc.sync.dma_start(out=xk_sb[:], in_=xk_v[:, b])
+            return xk_sb
+
+        def load_xq(qt):
+            xq_sb = ring.tile([P, B, H * HD], BF16, tag="xq", bufs=2, name="xq_sb")
+            nc.sync.dma_start(out=xq_sb[:], in_=xq_v[:, :, qt, :])
+            return xq_sb
+
+        def rsqrt_mask(qt):
+            nc.scalar.activation(out=y_all[:, qt, :], in_=mask_sb[:, qt, :], func=ACT.Abs_reciprocal_sqrt)
+
+        def newton(qt):
+            for c in range(2):
+                cols = slice(c * 512, (c + 1) * 512)
+                y = y_all[:, qt, cols]
+                nc.gpsimd.tensor_tensor(out=y, in0=y, in1=y, op=ALU.mult)
+                a = ring.tile([P, 512], F32, tag="nt", bufs=2, name="a")
+                nc.gpsimd.tensor_tensor(out=a[:], in0=y, in1=mask_sb[:, qt, cols], op=ALU.mult)
+                nc.gpsimd.tensor_scalar(out=a[:], in0=a[:], scalar1=-1.0, scalar2=2.0, op0=ALU.mult, op1=ALU.add)
+                nc.gpsimd.tensor_tensor(out=y, in0=y, in1=a[:], op=ALU.mult)
+
+        def build_kT(b, xk_sb):
+            for h in range(H):
+                ps = psum.tile([P, NKT, P], BF16, tag="et", bufs=2, name="kt_ps")
+                for j in range(NKT):
+                    nc.tensor.transpose(ps[:, j, :], xk_sb[:, j, h * HD:(h + 1) * HD], ident_bf[:])
+                nc.vector.tensor_copy(out=kT[:, b, h, :], in_=ps[:].rearrange("p j k -> p (j k)"))
+
+        def build_qT(xq_sb):
+            qT = ring.tile([P, B * H, P], BF16, tag="qT", bufs=2, name="qT")
+            ps = psum.tile([P, B * H, P], BF16, tag="q", bufs=1, name="qt_ps")
+            for b in range(B):
+                for h in range(H):
+                    nc.tensor.transpose(ps[:, b * H + h, :], xq_sb[:, b, h * HD:(h + 1) * HD], ident_bf[:])
+            nc.scalar.copy(out=qT[:], in_=ps[:])
+            return qT
+
+        load_mask(0, 1)
+        xk0 = load_xk(0)
+        xq0 = load_xq(0)
+        rsqrt_mask(0)
+        newton(0)
+        build_kT(0, xk0)
+        qT_cur = build_qT(xq0)
+        for lo in (1, 4, 8, 12):
+            load_mask(lo, min(lo + 4, NQT) if lo > 1 else 4)
+        for qt in range(1, NQT):
+            rsqrt_mask(qt)
+        for qt in range(1, NQT):
+            newton(qt)
+
+        wv_raw = keep.tile([P, 2, 2, 2, HD], BF16, name="wv_raw")
+        nc.sync.dma_start(out=wv_raw[:], in_=Wv.rearrange("(g u p e) f -> p g u e f", g=2, u=2, e=2))
+        wv_grp = keep.tile([P, 2, HD, 4], BF16, name="wv_grp", align_bytes=64)
+        nc.vector.tensor_copy(out=wv_grp[:], in_=wv_raw[:].rearrange("p g u e f -> p g f (u e)"))
+        wv_codes = keep.tile([P, 2 * HD], U32, name="wv_codes", align_bytes=64)
+        wv_scales = keep.tile([P, 2 * HD], U8, name="wv_scales", align_bytes=64)
+        nc.vector.quantize_mx(
+            out=wv_codes[:].bitcast(FP8X4),
+            scales=wv_scales[:],
+            in_=wv_grp[:].rearrange("p g f t -> p (g f t)"),
+        )
+
+        v_codes = []
+        v_scales = []
+
+        def value_chain(b):
+            v_grp = ring.tile([P, 2, HD, 4], BF16, tag="vg", bufs=1, name="v_grp", align_bytes=64)
+            for g in range(2):
+                kv_sb = ring.tile([P, 4, DIN], BF16, tag="kv", bufs=2, name="kv_sb")
+                nc.sync.dma_start(out=kv_sb[:], in_=kv_v[:, b, 4 * g:4 * g + 4, :])
+                kv_grp = ring.tile([P, 4 * 1024], BF16, tag="kvg", bufs=1, name="kv_grp", align_bytes=64)
+                grp_w = kv_grp[:].bitcast(F32).rearrange("p (t g k u) -> p t g k u", t=4, g=2, u=2)
+                for t in range(4):
+                    xt = psum.tile([P, 4, P], F32, tag="s", bufs=4, name="xt")
+                    kw = kv_sb[:, t, :].bitcast(F32)
+                    for w in range(4):
+                        nc.tensor.transpose(xt[:, w, :], kw[:, w * P:(w + 1) * P], ident_f[:])
+                    nc.scalar.copy(out=grp_w[:, t], in_=xt[:].rearrange("p (g u) k -> p g k u", u=2))
+                kv_codes = ring.tile([P, 1024], U32, tag="kvc", bufs=2, name="kv_codes", align_bytes=64)
+                kv_scales = ring.tile([P, 1024], U8, tag="kvs", bufs=2, name="kv_scales", align_bytes=64)
+                nc.vector.quantize_mx(out=kv_codes[:].bitcast(FP8X4), scales=kv_scales[:], in_=kv_grp[:])
+                xv_ps = psum.tile([P, 4, HD], F32, tag="o", bufs=1, name="xv_ps")
+                for t in range(4):
+                    for gg in range(2):
+                        cols = slice((t * 2 + gg) * P, (t * 2 + gg + 1) * P)
+                        wcols = slice(gg * HD, (gg + 1) * HD)
+                        nc.tensor.matmul_mx(
+                            out=xv_ps[:, t, :],
+                            lhsT=kv_codes[:, cols].bitcast(FP8X4),
+                            lhsT_scale=kv_scales[:, cols],
+                            rhs=wv_codes[:, wcols].bitcast(FP8X4),
+                            rhs_scale=wv_scales[:, wcols],
+                            start=(gg == 0),
+                            stop=(gg == 1),
+                        )
+                nc.scalar.copy(out=v_grp[:, g], in_=xv_ps[:].rearrange("p t f -> p f t"))
+            vc = keep.tile([P, 2 * HD], U32, name="v_codes%d" % b, align_bytes=64)
+            vs = keep.tile([P, 2 * HD], U8, name="v_scales%d" % b, align_bytes=64)
+            nc.vector.quantize_mx(
+                out=vc[:].bitcast(FP8X4), scales=vs[:], in_=v_grp[:].rearrange("p g f t -> p (g f t)")
+            )
+            v_codes.append(vc)
+            v_scales.append(vs)
+
+        def stage1(qt, b, qT):
+            et_grp = ring.tile([P, H, 2, P, 4], BF16, tag="etg", bufs=2, name="et_grp", align_bytes=64)
+            rowsum = ring.tile([P, H], F32, tag="rs", bufs=3, name="rowsum")
+            for h in range(H):
+                t = ring.tile([P, SKV], F32, tag="t", bufs=4, name="t")
+                for c in range(2):
+                    cols = slice(c * 512, (c + 1) * 512)
+                    s_ps = psum.tile([P, 512], F32, tag="s", bufs=4, name="s_ps")
+                    nc.tensor.matmul(s_ps[:], lhsT=qT[:, b * H + h, :], rhs=kT[:, b, h, cols], start=True, stop=True)
+                    nc.vector.scalar_tensor_tensor(
+                        out=t[:, cols], in0=s_ps[:], scalar=-SCALE, in1=y_all[:, qt, cols], op0=ALU.mult, op1=ALU.add
+                    )
+                m = ring.tile([P, 1], F32, tag="m", bufs=4, name="m")
+                nc.vector.tensor_reduce(out=m[:], in_=t[:], axis=AX.X, op=ALU.min)
+                e = ring.tile([P, SKV], BF16, tag="e", bufs=3, name="e")
+                nc.scalar.activation(
+                    out=e[:], in_=t[:], func=ACT.Exp, bias=m[:, 0:1], scale=-1.0, accum_out=rowsum[:, h:h + 1]
+                )
+                et_ps = psum.tile([P, NKT, P], BF16, tag="et", bufs=2, name="et_ps")
+                for j in range(NKT):
+                    nc.tensor.transpose(et_ps[:, j, :], e[:, j * P:(j + 1) * P], ident_bf[:])
+                nc.scalar.copy(out=et_grp[:, h], in_=et_ps[:].rearrange("p (g t) q -> p g q t", t=4))
+            e_codes = ring.tile([P, H * 2 * P], U32, tag="ec", bufs=2, name="e_codes", align_bytes=64)
+            e_scales = ring.tile([P, H * 2 * P], U8, tag="es", bufs=2, name="e_scales", align_bytes=64)
+            nc.vector.quantize_mx(
+                out=e_codes[:].bitcast(FP8X4), scales=e_scales[:], in_=et_grp[:].rearrange("p h g q t -> p (h g q t)")
+            )
+            return e_codes, e_scales, rowsum
+
+        def stage2(qt, b, st):
+            e_codes, e_scales, rowsum = st
+            o_ps = psum.tile([P, H, HD], F32, tag="o", bufs=1, name="o_ps")
+            for h in range(H):
+                for g in range(2):
+                    cols = slice((h * 2 + g) * P, (h * 2 + g + 1) * P)
+                    vcols = slice(g * HD, (g + 1) * HD)
+                    nc.tensor.matmul_mx(
+                        out=o_ps[:, h, :],
+                        lhsT=e_codes[:, cols].bitcast(FP8X4),
+                        lhsT_scale=e_scales[:, cols],
+                        rhs=v_codes[b][:, vcols].bitcast(FP8X4),
+                        rhs_scale=v_scales[b][:, vcols],
+                        start=(g == 0),
+                        stop=(g == 1),
+                    )
+            rinv = ring.tile([P, H], F32, tag="ri", bufs=2, name="rinv")
+            nc.vector.reciprocal(rinv[:], rowsum[:])
+            o_sb = ring.tile([P, H, DIST, REP], F32, tag="osb", bufs=2, name="o_sb")
+            for h in range(H):
+                nc.vector.tensor_scalar(
+                    out=o_sb[:, h],
+                    in0=o_ps[:, h, h * DIST:(h + 1) * DIST].unsqueeze(2).to_broadcast([P, DIST, REP]),
+                    scalar1=rinv[:, h:h + 1],
+                    scalar2=None,
+                    op0=ALU.mult,
+                )
+            nc.sync.dma_start(out=out[b, qt * P:(qt + 1) * P, :], in_=o_sb[:].rearrange("p h j r -> p (h j r)"))
+
+        groups = [(qt, b) for qt in range(NQT) for b in range(B)]
+        prev = stage1(0, 0, qT_cur)
+        xk1 = load_xk(1)
+        build_kT(1, xk1)
+        value_chain(0)
+        value_chain(1)
+        qT_next = None
+        for i in range(1, len(groups)):
+            qt, b = groups[i]
+            if b == 1 and qt + 1 < NQT:
+                qT_next = build_qT(load_xq(qt + 1))
+            if b == 0:
+                qT_cur = qT_next
+            cur = stage1(qt, b, qT_cur)
+            pq, pb = groups[i - 1]
+            stage2(pq, pb, prev)
+            prev = cur
+        stage2(groups[-1][0], groups[-1][1], prev)

@@ -22,7 +22,10 @@ NKT = SKV // P
 REP = 4
 DIST = HD // REP
 SCALE = 1.0 / math.sqrt(HD)
+ROOT = math.sqrt(HD)
 FLOPS = 2 * B * SKV * DIN * HD + 2 * 2 * B * H * SQ * SKV * HD
+MANUAL = True
+REGROUP_ON_VECTOR = (3,)
 
 
 def tile_groupedqueryattention_pa_t_kernel(tc, xq, xk_rep, kv, mask, Wv, out):
@@ -31,6 +34,8 @@ def tile_groupedqueryattention_pa_t_kernel(tc, xq, xk_rep, kv, mask, Wv, out):
         keep = ctx.enter_context(tc.tile_pool(name="keep", bufs=1))
         ring = ctx.enter_context(tc.tile_pool(name="ring", bufs=2))
         psum = ctx.enter_context(tc.psum_pool(name="psum", bufs=1))
+        if MANUAL:
+            ctx.enter_context(tc.manual_schedule())
 
         mask_v = mask.rearrange("a c (t p) k -> p (a c t) k", p=P)
         xq_v = xq.rearrange("b (t p) c -> p b t c", p=P)
@@ -42,12 +47,14 @@ def tile_groupedqueryattention_pa_t_kernel(tc, xq, xk_rep, kv, mask, Wv, out):
         ident_f = keep.tile([P, P], F32, name="ident_f")
         make_identity(nc, ident_f[:])
 
-        mask_sb = keep.tile([P, NQT, SKV], BF16, name="mask_sb")
-        y_all = keep.tile([P, NQT, SKV], F32, name="y_all")
+        xT = keep.tile([P, NQT, NKT, P], BF16, name="xT")
+        yT = keep.tile([P, NQT, NKT, P], F32, name="yT")
         kT = keep.tile([P, B, H, SKV], BF16, name="kT")
 
-        def load_mask(lo, hi):
-            nc.sync.dma_start(out=mask_sb[:, lo:hi, :], in_=mask_v[:, lo:hi, :])
+        def load_mask(qt):
+            m_sb = ring.tile([P, SKV], BF16, tag="mraw", bufs=4, name="m_sb")
+            nc.sync.dma_start(out=m_sb[:], in_=mask_v[:, qt, :])
+            return m_sb
 
         def load_xk(b):
             xk_sb = ring.tile([P, NKT, H * HD], BF16, tag="xk", bufs=1, name="xk_sb")
@@ -59,18 +66,20 @@ def tile_groupedqueryattention_pa_t_kernel(tc, xq, xk_rep, kv, mask, Wv, out):
             nc.sync.dma_start(out=xq_sb[:], in_=xq_v[:, :, qt, :])
             return xq_sb
 
-        def rsqrt_mask(qt):
-            nc.scalar.activation(out=y_all[:, qt, :], in_=mask_sb[:, qt, :], func=ACT.Abs_reciprocal_sqrt)
+        def mask_seed(qt, m_sb):
+            ps = psum.tile([P, NKT, P], BF16, tag="et", bufs=2, name="mt_ps")
+            for j in range(NKT):
+                nc.tensor.transpose(ps[:, j, :], m_sb[:, j * P:(j + 1) * P], ident_bf[:])
+            nc.vector.tensor_copy(out=xT[:, qt], in_=ps[:])
+            nc.scalar.activation(out=yT[:, qt], in_=xT[:, qt], func=ACT.Abs_reciprocal_sqrt)
 
-        def newton(qt):
-            for c in range(2):
-                cols = slice(c * 512, (c + 1) * 512)
-                y = y_all[:, qt, cols]
-                nc.gpsimd.tensor_tensor(out=y, in0=y, in1=y, op=ALU.mult)
-                a = ring.tile([P, 512], F32, tag="nt", bufs=2, name="a")
-                nc.gpsimd.tensor_tensor(out=a[:], in0=y, in1=mask_sb[:, qt, cols], op=ALU.mult)
-                nc.gpsimd.tensor_scalar(out=a[:], in0=a[:], scalar1=-1.0, scalar2=2.0, op0=ALU.mult, op1=ALU.add)
-                nc.gpsimd.tensor_tensor(out=y, in0=y, in1=a[:], op=ALU.mult)
+        def newton(qt, c, eng):
+            y = yT[:, qt, 4 * c:4 * c + 4, :]
+            eng.tensor_tensor(out=y, in0=y, in1=y, op=ALU.mult)
+            a = ring.tile([P, 4, P], F32, tag="nt", bufs=2, name="a")
+            eng.tensor_tensor(out=a[:], in0=y, in1=xT[:, qt, 4 * c:4 * c + 4, :], op=ALU.mult)
+            eng.tensor_scalar(out=a[:], in0=a[:], scalar1=ROOT, scalar2=-2.0 * ROOT, op0=ALU.mult, op1=ALU.add)
+            eng.tensor_tensor(out=y, in0=y, in1=a[:], op=ALU.mult)
 
         def build_kT(b, xk_sb):
             for h in range(H):
@@ -88,121 +97,210 @@ def tile_groupedqueryattention_pa_t_kernel(tc, xq, xk_rep, kv, mask, Wv, out):
             nc.scalar.copy(out=qT[:], in_=ps[:])
             return qT
 
-        load_mask(0, 1)
+        raw = {0: load_mask(0)}
         xk0 = load_xk(0)
         xq0 = load_xq(0)
-        rsqrt_mask(0)
-        newton(0)
+        for qt in range(1, 4):
+            raw[qt] = load_mask(qt)
+
+        def seed(qt):
+            mask_seed(qt, raw[qt])
+            if qt + 4 < NQT:
+                raw[qt + 4] = load_mask(qt + 4)
+            if qt > 0:
+                newton(qt, 0, nc.gpsimd)
+                newton(qt, 1, nc.gpsimd)
+
+        seed(0)
+        newton(0, 0, nc.vector)
+        newton(0, 1, nc.gpsimd)
         build_kT(0, xk0)
-        qT_cur = build_qT(xq0)
-        for lo in (1, 4, 8, 12):
-            load_mask(lo, min(lo + 4, NQT) if lo > 1 else 4)
-        for qt in range(1, NQT):
-            rsqrt_mask(qt)
-        for qt in range(1, NQT):
-            newton(qt)
+        qTs = {0: build_qT(xq0)}
+        for qt in range(1, 12):
+            seed(qt)
+        xk1 = load_xk(1)
 
         wv_raw = keep.tile([P, 2, 2, 2, HD], BF16, name="wv_raw")
         nc.sync.dma_start(out=wv_raw[:], in_=Wv.rearrange("(g u p e) f -> p g u e f", g=2, u=2, e=2))
         wv_grp = keep.tile([P, 2, HD, 4], BF16, name="wv_grp", align_bytes=64)
-        nc.vector.tensor_copy(out=wv_grp[:], in_=wv_raw[:].rearrange("p g u e f -> p g f (u e)"))
         wv_codes = keep.tile([P, 2 * HD], U32, name="wv_codes", align_bytes=64)
         wv_scales = keep.tile([P, 2 * HD], U8, name="wv_scales", align_bytes=64)
-        nc.vector.quantize_mx(
-            out=wv_codes[:].bitcast(FP8X4),
-            scales=wv_scales[:],
-            in_=wv_grp[:].rearrange("p g f t -> p (g f t)"),
-        )
+
+        def wv_regroup():
+            nc.vector.tensor_copy(out=wv_grp[:], in_=wv_raw[:].rearrange("p g u e f -> p g f (u e)"))
+
+        def wv_quantise():
+            nc.vector.quantize_mx(
+                out=wv_codes[:].bitcast(FP8X4),
+                scales=wv_scales[:],
+                in_=wv_grp[:].rearrange("p g f t -> p (g f t)"),
+            )
 
         v_codes = []
         v_scales = []
 
-        def value_chain(b):
-            v_grp = ring.tile([P, 2, HD, 4], BF16, tag="vg", bufs=1, name="v_grp", align_bytes=64)
-            for g in range(2):
-                kv_sb = ring.tile([P, 4, DIN], BF16, tag="kv", bufs=2, name="kv_sb")
-                nc.sync.dma_start(out=kv_sb[:], in_=kv_v[:, b, 4 * g:4 * g + 4, :])
-                kv_grp = ring.tile([P, 4 * 1024], BF16, tag="kvg", bufs=1, name="kv_grp", align_bytes=64)
-                grp_w = kv_grp[:].bitcast(F32).rearrange("p (t g k u) -> p t g k u", t=4, g=2, u=2)
-                for t in range(4):
-                    xt = psum.tile([P, 4, P], F32, tag="s", bufs=4, name="xt")
-                    kw = kv_sb[:, t, :].bitcast(F32)
-                    for w in range(4):
-                        nc.tensor.transpose(xt[:, w, :], kw[:, w * P:(w + 1) * P], ident_f[:])
-                    nc.scalar.copy(out=grp_w[:, t], in_=xt[:].rearrange("p (g u) k -> p g k u", u=2))
-                kv_codes = ring.tile([P, 1024], U32, tag="kvc", bufs=2, name="kv_codes", align_bytes=64)
-                kv_scales = ring.tile([P, 1024], U8, tag="kvs", bufs=2, name="kv_scales", align_bytes=64)
-                nc.vector.quantize_mx(out=kv_codes[:].bitcast(FP8X4), scales=kv_scales[:], in_=kv_grp[:])
-                xv_ps = psum.tile([P, 4, HD], F32, tag="o", bufs=1, name="xv_ps")
-                for t in range(4):
-                    for gg in range(2):
-                        cols = slice((t * 2 + gg) * P, (t * 2 + gg + 1) * P)
-                        wcols = slice(gg * HD, (gg + 1) * HD)
-                        nc.tensor.matmul_mx(
-                            out=xv_ps[:, t, :],
-                            lhsT=kv_codes[:, cols].bitcast(FP8X4),
-                            lhsT_scale=kv_scales[:, cols],
-                            rhs=wv_codes[:, wcols].bitcast(FP8X4),
-                            rhs_scale=wv_scales[:, wcols],
-                            start=(gg == 0),
-                            stop=(gg == 1),
-                        )
-                nc.scalar.copy(out=v_grp[:, g], in_=xv_ps[:].rearrange("p t f -> p f t"))
+        vst = {}
+
+        def kv_load(c):
+            kv_sb = ring.tile([P, 4, DIN], BF16, tag="kv", bufs=2, name="kv_sb")
+            nc.sync.dma_start(out=kv_sb[:], in_=kv_v[:, c // 2, 4 * (c % 2):4 * (c % 2) + 4, :])
+            vst[("kv", c)] = kv_sb
+
+        def kv_transpose(c, half):
+            if half == 0:
+                vst[("grp", c)] = ring.tile([P, 4 * 1024], BF16, tag="kvg", bufs=1, name="kv_grp", align_bytes=64)
+            grp_w = vst[("grp", c)][:].bitcast(F32).rearrange("p (t g k u) -> p t g k u", t=4, g=2, u=2)
+            for t in (2 * half, 2 * half + 1):
+                xt = psum.tile([P, 4, P], F32, tag="s", bufs=4, name="xt")
+                kw = vst[("kv", c)][:, t, :].bitcast(F32)
+                for w in range(4):
+                    nc.tensor.transpose(xt[:, w, :], kw[:, w * P:(w + 1) * P], ident_f[:])
+                nc.vector.tensor_copy(out=grp_w[:, t], in_=xt[:].rearrange("p (g u) k -> p g k u", u=2))
+
+        def kv_quantise(c):
+            kv_codes = ring.tile([P, 1024], U32, tag="kvc", bufs=1, name="kv_codes", align_bytes=64)
+            kv_scales = ring.tile([P, 1024], U8, tag="kvs", bufs=1, name="kv_scales", align_bytes=64)
+            nc.vector.quantize_mx(out=kv_codes[:].bitcast(FP8X4), scales=kv_scales[:], in_=vst[("grp", c)][:])
+            vst[("codes", c)] = (kv_codes, kv_scales)
+
+        def xv_matmul(c):
+            kv_codes, kv_scales = vst[("codes", c)]
+            xv_ps = psum.tile([P, 4, HD], F32, tag="o", bufs=1, name="xv_ps")
+            for t in range(4):
+                for gg in range(2):
+                    cols = slice((t * 2 + gg) * P, (t * 2 + gg + 1) * P)
+                    wcols = slice(gg * HD, (gg + 1) * HD)
+                    nc.tensor.matmul_mx(
+                        out=xv_ps[:, t, :],
+                        lhsT=kv_codes[:, cols].bitcast(FP8X4),
+                        lhsT_scale=kv_scales[:, cols],
+                        rhs=wv_codes[:, wcols].bitcast(FP8X4),
+                        rhs_scale=wv_scales[:, wcols],
+                        start=(gg == 0),
+                        stop=(gg == 1),
+                    )
+            vst[("xv", c)] = xv_ps
+
+        def xv_leave(c):
+            if c % 2 == 0:
+                vst[("vg", c // 2)] = ring.tile([P, 2, HD, 4], BF16, tag="vg", bufs=1, name="v_grp", align_bytes=64)
+            nc.vector.tensor_copy(
+                out=vst[("vg", c // 2)][:, c % 2], in_=vst[("xv", c)][:].rearrange("p t f -> p f t")
+            )
+
+        def v_quantise(b):
             vc = keep.tile([P, 2 * HD], U32, name="v_codes%d" % b, align_bytes=64)
             vs = keep.tile([P, 2 * HD], U8, name="v_scales%d" % b, align_bytes=64)
             nc.vector.quantize_mx(
-                out=vc[:].bitcast(FP8X4), scales=vs[:], in_=v_grp[:].rearrange("p g f t -> p (g f t)")
+                out=vc[:].bitcast(FP8X4), scales=vs[:], in_=vst[("vg", b)][:].rearrange("p g f t -> p (g f t)")
             )
             v_codes.append(vc)
             v_scales.append(vs)
 
-        def stage1(qt, b, qT):
-            et_grp = ring.tile([P, H, 2, P, 4], BF16, tag="etg", bufs=2, name="et_grp", align_bytes=64)
-            rowsum = ring.tile([P, H], F32, tag="rs", bufs=3, name="rowsum")
-            for h in range(H):
-                t = ring.tile([P, SKV], F32, tag="t", bufs=4, name="t")
-                for c in range(2):
-                    cols = slice(c * 512, (c + 1) * 512)
-                    s_ps = psum.tile([P, 512], F32, tag="s", bufs=4, name="s_ps")
-                    nc.tensor.matmul(s_ps[:], lhsT=qT[:, b * H + h, :], rhs=kT[:, b, h, cols], start=True, stop=True)
-                    nc.vector.scalar_tensor_tensor(
-                        out=t[:, cols], in0=s_ps[:], scalar=-SCALE, in1=y_all[:, qt, cols], op0=ALU.mult, op1=ALU.add
-                    )
-                m = ring.tile([P, 1], F32, tag="m", bufs=4, name="m")
-                nc.vector.tensor_reduce(out=m[:], in_=t[:], axis=AX.X, op=ALU.min)
-                e = ring.tile([P, SKV], BF16, tag="e", bufs=3, name="e")
-                nc.scalar.activation(
-                    out=e[:], in_=t[:], func=ACT.Exp, bias=m[:, 0:1], scale=-1.0, accum_out=rowsum[:, h:h + 1]
-                )
-                et_ps = psum.tile([P, NKT, P], BF16, tag="et", bufs=2, name="et_ps")
-                for j in range(NKT):
-                    nc.tensor.transpose(et_ps[:, j, :], e[:, j * P:(j + 1) * P], ident_bf[:])
-                nc.scalar.copy(out=et_grp[:, h], in_=et_ps[:].rearrange("p (g t) q -> p g q t", t=4))
-            e_codes = ring.tile([P, H * 2 * P], U32, tag="ec", bufs=2, name="e_codes", align_bytes=64)
-            e_scales = ring.tile([P, H * 2 * P], U8, tag="es", bufs=2, name="e_scales", align_bytes=64)
-            nc.vector.quantize_mx(
-                out=e_codes[:].bitcast(FP8X4), scales=e_scales[:], in_=et_grp[:].rearrange("p h g q t -> p (h g q t)")
-            )
-            return e_codes, e_scales, rowsum
+        units = [(qt, b, h) for qt in range(NQT) for b in range(B) for h in range(H)]
+        NU = len(units)
+        NG = NU // H
+        st = {}
 
-        def stage2(qt, b, st):
-            e_codes, e_scales, rowsum = st
+        def scores(u):
+            qt, b, h = units[u]
+            banks = []
+            for c in range(2):
+                s_ps = psum.tile([P, 512], F32, tag="s", bufs=4, name="s_ps")
+                nc.tensor.matmul(
+                    s_ps[:], lhsT=qTs[qt][:, b * H + h, :], rhs=kT[:, b, h, c * 512:(c + 1) * 512],
+                    start=True, stop=False,
+                )
+                banks.append(s_ps)
+            for c in range(2):
+                for jj in range(4):
+                    nc.tensor.matmul(
+                        banks[c][:, jj * P:(jj + 1) * P], lhsT=yT[:, qt, 4 * c + jj, :], rhs=ident_f[:],
+                        is_transpose=True, start=False, stop=(jj == 3),
+                    )
+            st[("s", u)] = banks
+
+        def leave_psum(u, c):
+            if c == 0:
+                st[("t", u)] = ring.tile([P, SKV], F32, tag="t", bufs=4, name="t")
+                st[("m0", u)] = ring.tile([P, 1], F32, tag="m0", bufs=3, name="m0")
+                st[("m", u)] = ring.tile([P, 1], F32, tag="m", bufs=4, name="m")
+            t = st[("t", u)]
+            nc.vector.tensor_scalar(
+                out=t[:, c * 512:(c + 1) * 512],
+                in0=st[("s", u)][c][:],
+                scalar1=-SCALE,
+                scalar2=(None if c == 0 else st[("m0", u)][:, 0:1]),
+                op0=ALU.mult,
+                op1=ALU.min,
+                accum_out=(st[("m0", u)][:] if c == 0 else st[("m", u)][:]),
+            )
+
+        def exponent(u):
+            qt, b, h = units[u]
+            g = u // H
+            if h == 0:
+                st[("rs", g)] = ring.tile([P, H], F32, tag="rs", bufs=5, name="rowsum")
+            e = ring.tile([P, SKV], BF16, tag="e", bufs=3, name="e")
+            nc.scalar.activation(
+                out=e[:], in_=st[("t", u)][:], func=ACT.Exp, bias=st[("m", u)][:, 0:1], scale=-1.0,
+                accum_out=st[("rs", g)][:, h:h + 1],
+            )
+            st[("e", u)] = e
+
+        def transposes(u):
+            e = st[("e", u)]
+            et_ps = psum.tile([P, NKT, P], BF16, tag="et", bufs=2, name="et_ps")
+            for j in range(NKT):
+                nc.tensor.transpose(et_ps[:, j, :], e[:, j * P:(j + 1) * P], ident_bf[:])
+            st[("et", u)] = et_ps
+
+        def regroup(u):
+            h = u % H
+            et_grp = ring.tile([P, 2, P, 4], BF16, tag="etg", bufs=3, name="et_grp", align_bytes=64)
+            src = st[("et", u)][:].rearrange("p (g t) q -> p g q t", t=4)
+            if h in REGROUP_ON_VECTOR:
+                nc.vector.tensor_copy(out=et_grp[:], in_=src)
+            else:
+                nc.scalar.copy(out=et_grp[:], in_=src)
+            st[("etg", u)] = et_grp
+
+        def quantise(u):
+            h = u % H
+            g = u // H
+            if h == 0:
+                st[("ec", g)] = ring.tile([P, H * 2 * P], U32, tag="ec", bufs=3, name="e_codes", align_bytes=64)
+                st[("es", g)] = ring.tile([P, H * 2 * P], U8, tag="es", bufs=3, name="e_scales", align_bytes=64)
+            cols = slice(h * 2 * P, (h + 1) * 2 * P)
+            nc.vector.quantize_mx(
+                out=st[("ec", g)][:, cols].bitcast(FP8X4),
+                scales=st[("es", g)][:, cols],
+                in_=st[("etg", u)][:].rearrange("p g q t -> p (g q t)"),
+            )
+
+        def weighted_sum(g):
+            qt, b, h0 = units[g * H]
             o_ps = psum.tile([P, H, HD], F32, tag="o", bufs=1, name="o_ps")
             for h in range(H):
-                for g in range(2):
-                    cols = slice((h * 2 + g) * P, (h * 2 + g + 1) * P)
-                    vcols = slice(g * HD, (g + 1) * HD)
+                for gg in range(2):
+                    cols = slice((h * 2 + gg) * P, (h * 2 + gg + 1) * P)
+                    vcols = slice(gg * HD, (gg + 1) * HD)
                     nc.tensor.matmul_mx(
                         out=o_ps[:, h, :],
-                        lhsT=e_codes[:, cols].bitcast(FP8X4),
-                        lhsT_scale=e_scales[:, cols],
+                        lhsT=st[("ec", g)][:, cols].bitcast(FP8X4),
+                        lhsT_scale=st[("es", g)][:, cols],
                         rhs=v_codes[b][:, vcols].bitcast(FP8X4),
                         rhs_scale=v_scales[b][:, vcols],
-                        start=(g == 0),
-                        stop=(g == 1),
+                        start=(gg == 0),
+                        stop=(gg == 1),
                     )
+            st[("o", g)] = o_ps
+
+        def normalise(g):
+            qt, b, h0 = units[g * H]
+            o_ps = st[("o", g)]
             rinv = ring.tile([P, H], F32, tag="ri", bufs=2, name="rinv")
-            nc.vector.reciprocal(rinv[:], rowsum[:])
+            nc.vector.reciprocal(rinv[:], st[("rs", g)][:])
             o_sb = ring.tile([P, H, DIST, REP], F32, tag="osb", bufs=2, name="o_sb")
             for h in range(H):
                 nc.vector.tensor_scalar(
@@ -214,21 +312,56 @@ def tile_groupedqueryattention_pa_t_kernel(tc, xq, xk_rep, kv, mask, Wv, out):
                 )
             nc.sync.dma_start(out=out[b, qt * P:(qt + 1) * P, :], in_=o_sb[:].rearrange("p h j r -> p (h j r)"))
 
-        groups = [(qt, b) for qt in range(NQT) for b in range(B)]
-        prev = stage1(0, 0, qT_cur)
-        xk1 = load_xk(1)
-        build_kT(1, xk1)
-        value_chain(0)
-        value_chain(1)
-        qT_next = None
-        for i in range(1, len(groups)):
-            qt, b = groups[i]
-            if b == 1 and qt + 1 < NQT:
-                qT_next = build_qT(load_xq(qt + 1))
-            if b == 0:
-                qT_cur = qT_next
-            cur = stage1(qt, b, qT_cur)
-            pq, pb = groups[i - 1]
-            stage2(pq, pb, prev)
-            prev = cur
-        stage2(groups[-1][0], groups[-1][1], prev)
+        LAG_PV = 15
+        KV_AT = (4, 6, 8, 10)
+        kv_load(0)
+        kv_load(1)
+        for tk in range(NU + LAG_PV + 2):
+            if tk % 8 == 0 and tk // 8 + 1 < NQT:
+                st[("xq", tk // 8 + 1)] = load_xq(tk // 8 + 1)
+            for c in (2, 3):
+                if tk == KV_AT[c - 2] + 2:
+                    kv_load(c)
+            if 0 <= tk - 3 < NU:
+                transposes(tk - 3)
+            if tk < NU:
+                scores(tk)
+            if tk >= LAG_PV and (tk - LAG_PV) % H == 0 and (tk - LAG_PV) // H < NG:
+                weighted_sum((tk - LAG_PV) // H)
+            if tk == 0:
+                for qt in range(12, NQT):
+                    seed(qt)
+            if tk == 2:
+                build_kT(1, xk1)
+            if tk % 8 == 4 and tk // 8 + 1 < NQT:
+                qTs[tk // 8 + 1] = build_qT(st[("xq", tk // 8 + 1)])
+            if 0 <= tk - 1 < NU:
+                leave_psum(tk - 1, 0)
+            if 0 <= tk - 5 < NU:
+                quantise(tk - 5)
+            if 0 <= tk - 1 < NU:
+                leave_psum(tk - 1, 1)
+            if 0 <= tk - 2 < NU:
+                exponent(tk - 2)
+            if 0 <= tk - 4 < NU:
+                regroup(tk - 4)
+            if tk >= LAG_PV + 1 and (tk - LAG_PV - 1) % H == 0 and (tk - LAG_PV - 1) // H < NG:
+                normalise((tk - LAG_PV - 1) // H)
+            if tk == 3:
+                wv_regroup()
+            if tk == 4:
+                wv_quantise()
+            for c in range(4):
+                if tk == KV_AT[c] + 2:
+                    kv_quantise(c)
+                if tk == KV_AT[c] + 3:
+                    xv_matmul(c)
+                if tk == KV_AT[c] + 4:
+                    xv_leave(c)
+                if tk == KV_AT[c] + 5 and c % 2 == 1:
+                    v_quantise(c // 2)
+            for c in range(4):
+                if tk == KV_AT[c]:
+                    kv_transpose(c, 0)
+                if tk == KV_AT[c] + 1:
+                    kv_transpose(c, 1)

@@ -13,7 +13,6 @@ U8 = mybir.dt.uint8
 FP8X4 = mybir.dt.float8_e4m3fn_x4
 ALU = mybir.AluOpType
 ACT = mybir.ActivationFunctionType
-AX = mybir.AxisListType
 
 B, SQ, SKV, DIN, H, HD = 2, 2048, 1024, 1024, 4, 128
 P = 128
@@ -24,8 +23,16 @@ DIST = HD // REP
 SCALE = 1.0 / math.sqrt(HD)
 ROOT = math.sqrt(HD)
 FLOPS = 2 * B * SKV * DIN * HD + 2 * 2 * B * H * SQ * SKV * HD
-MANUAL = True
 REGROUP_ON_VECTOR = (3,)
+
+LAG_LEAVE = 1
+LAG_EXP = 3
+LAG_TR = 5
+LAG_REGROUP = 6
+LAG_QUANT = 8
+LAG_PV = 16
+LAG_NORM = 18
+KV_AT = (3, 7, 11, 15)
 
 
 def tile_groupedqueryattention_pa_t_kernel(tc, xq, xk_rep, kv, mask, Wv, out):
@@ -34,8 +41,7 @@ def tile_groupedqueryattention_pa_t_kernel(tc, xq, xk_rep, kv, mask, Wv, out):
         keep = ctx.enter_context(tc.tile_pool(name="keep", bufs=1))
         ring = ctx.enter_context(tc.tile_pool(name="ring", bufs=2))
         psum = ctx.enter_context(tc.psum_pool(name="psum", bufs=1))
-        if MANUAL:
-            ctx.enter_context(tc.manual_schedule())
+        ctx.enter_context(tc.manual_schedule())
 
         mask_v = mask.rearrange("a c (t p) k -> p (a c t) k", p=P)
         xq_v = xq.rearrange("b (t p) c -> p b t c", p=P)
@@ -51,27 +57,25 @@ def tile_groupedqueryattention_pa_t_kernel(tc, xq, xk_rep, kv, mask, Wv, out):
         yT = keep.tile([P, NQT, NKT, P], F32, name="yT")
         kT = keep.tile([P, B, H, SKV], BF16, name="kT")
 
+        st = {}
+
+        def et_bank(dtype, shape, name):
+            return psum.tile(shape, dtype, tag="et", bufs=3, name=name)
+
         def load_mask(qt):
-            m_sb = ring.tile([P, SKV], BF16, tag="mraw", bufs=4, name="m_sb")
+            m_sb = ring.tile([P, SKV], BF16, tag="mraw", bufs=6, name="m_sb")
             nc.sync.dma_start(out=m_sb[:], in_=mask_v[:, qt, :])
-            return m_sb
+            st[("mraw", qt)] = m_sb
 
         def load_xk(b):
             xk_sb = ring.tile([P, NKT, H * HD], BF16, tag="xk", bufs=1, name="xk_sb")
             nc.sync.dma_start(out=xk_sb[:], in_=xk_v[:, b])
-            return xk_sb
+            st[("xk", b)] = xk_sb
 
         def load_xq(qt):
             xq_sb = ring.tile([P, B, H * HD], BF16, tag="xq", bufs=2, name="xq_sb")
             nc.sync.dma_start(out=xq_sb[:], in_=xq_v[:, :, qt, :])
-            return xq_sb
-
-        def mask_seed(qt, m_sb):
-            ps = psum.tile([P, NKT, P], BF16, tag="et", bufs=2, name="mt_ps")
-            for j in range(NKT):
-                nc.tensor.transpose(ps[:, j, :], m_sb[:, j * P:(j + 1) * P], ident_bf[:])
-            nc.vector.tensor_copy(out=xT[:, qt], in_=ps[:])
-            nc.scalar.activation(out=yT[:, qt], in_=xT[:, qt], func=ACT.Abs_reciprocal_sqrt)
+            st[("xq", qt)] = xq_sb
 
         def newton(qt, c, eng):
             y = yT[:, qt, 4 * c:4 * c + 4, :]
@@ -81,50 +85,49 @@ def tile_groupedqueryattention_pa_t_kernel(tc, xq, xk_rep, kv, mask, Wv, out):
             eng.tensor_scalar(out=a[:], in0=a[:], scalar1=ROOT, scalar2=-2.0 * ROOT, op0=ALU.mult, op1=ALU.add)
             eng.tensor_tensor(out=y, in0=y, in1=a[:], op=ALU.mult)
 
-        def build_kT(b, xk_sb):
-            for h in range(H):
-                ps = psum.tile([P, NKT, P], BF16, tag="et", bufs=2, name="kt_ps")
-                for j in range(NKT):
-                    nc.tensor.transpose(ps[:, j, :], xk_sb[:, j, h * HD:(h + 1) * HD], ident_bf[:])
-                nc.vector.tensor_copy(out=kT[:, b, h, :], in_=ps[:].rearrange("p j k -> p (j k)"))
+        def seed(qt):
+            m_sb = st[("mraw", qt)]
+            ps = et_bank(BF16, [P, NKT, P], "mt_ps")
+            for j in range(NKT):
+                nc.tensor.transpose(ps[:, j, :], m_sb[:, j * P:(j + 1) * P], ident_bf[:])
+            nc.vector.tensor_copy(out=xT[:, qt], in_=ps[:])
+            nc.scalar.activation(out=yT[:, qt], in_=xT[:, qt], func=ACT.Abs_reciprocal_sqrt)
+            if qt + 6 < NQT:
+                load_mask(qt + 6)
+            if qt == 0:
+                newton(0, 0, nc.vector)
+            else:
+                newton(qt, 0, nc.gpsimd)
+            newton(qt, 1, nc.gpsimd)
 
-        def build_qT(xq_sb):
-            qT = ring.tile([P, B * H, P], BF16, tag="qT", bufs=2, name="qT")
-            ps = psum.tile([P, B * H, P], BF16, tag="q", bufs=1, name="qt_ps")
+        def kT_transposes(b, h):
+            ps = et_bank(BF16, [P, NKT, P], "kt_ps")
+            for j in range(NKT):
+                nc.tensor.transpose(ps[:, j, :], st[("xk", b)][:, j, h * HD:(h + 1) * HD], ident_bf[:])
+            st[("ktps", b, h)] = ps
+
+        def kT_leave(b, h):
+            nc.vector.tensor_copy(out=kT[:, b, h, :], in_=st[("ktps", b, h)][:].rearrange("p j k -> p (j k)"))
+
+        def qT_transposes(qt):
+            ps = et_bank(BF16, [P, B * H, P], "qt_ps")
             for b in range(B):
                 for h in range(H):
-                    nc.tensor.transpose(ps[:, b * H + h, :], xq_sb[:, b, h * HD:(h + 1) * HD], ident_bf[:])
-            nc.scalar.copy(out=qT[:], in_=ps[:])
-            return qT
+                    nc.tensor.transpose(ps[:, b * H + h, :], st[("xq", qt)][:, b, h * HD:(h + 1) * HD], ident_bf[:])
+            st[("qtps", qt)] = ps
 
-        raw = {0: load_mask(0)}
-        xk0 = load_xk(0)
-        xq0 = load_xq(0)
-        for qt in range(1, 4):
-            raw[qt] = load_mask(qt)
-
-        def seed(qt):
-            mask_seed(qt, raw[qt])
-            if qt + 4 < NQT:
-                raw[qt + 4] = load_mask(qt + 4)
-            if qt > 0:
-                newton(qt, 0, nc.gpsimd)
-                newton(qt, 1, nc.gpsimd)
-
-        seed(0)
-        newton(0, 0, nc.vector)
-        newton(0, 1, nc.gpsimd)
-        build_kT(0, xk0)
-        qTs = {0: build_qT(xq0)}
-        for qt in range(1, 12):
-            seed(qt)
-        xk1 = load_xk(1)
+        def qT_leave(qt):
+            qT = ring.tile([P, B * H, P], BF16, tag="qT", bufs=2, name="qT")
+            nc.scalar.copy(out=qT[:], in_=st[("qtps", qt)][:])
+            st[("qT", qt)] = qT
 
         wv_raw = keep.tile([P, 2, 2, 2, HD], BF16, name="wv_raw")
-        nc.sync.dma_start(out=wv_raw[:], in_=Wv.rearrange("(g u p e) f -> p g u e f", g=2, u=2, e=2))
         wv_grp = keep.tile([P, 2, HD, 4], BF16, name="wv_grp", align_bytes=64)
         wv_codes = keep.tile([P, 2 * HD], U32, name="wv_codes", align_bytes=64)
         wv_scales = keep.tile([P, 2 * HD], U8, name="wv_scales", align_bytes=64)
+
+        def wv_load():
+            nc.sync.dma_start(out=wv_raw[:], in_=Wv.rearrange("(g u p e) f -> p g u e f", g=2, u=2, e=2))
 
         def wv_regroup():
             nc.vector.tensor_copy(out=wv_grp[:], in_=wv_raw[:].rearrange("p g u e f -> p g f (u e)"))
@@ -136,23 +139,18 @@ def tile_groupedqueryattention_pa_t_kernel(tc, xq, xk_rep, kv, mask, Wv, out):
                 in_=wv_grp[:].rearrange("p g f t -> p (g f t)"),
             )
 
-        v_codes = []
-        v_scales = []
-
-        vst = {}
-
         def kv_load(c):
-            kv_sb = ring.tile([P, 4, DIN], BF16, tag="kv", bufs=2, name="kv_sb")
+            kv_sb = ring.tile([P, 4, DIN], BF16, tag="kv", bufs=1, name="kv_sb")
             nc.sync.dma_start(out=kv_sb[:], in_=kv_v[:, c // 2, 4 * (c % 2):4 * (c % 2) + 4, :])
-            vst[("kv", c)] = kv_sb
+            st[("kv", c)] = kv_sb
 
         def kv_transpose(c, half):
             if half == 0:
-                vst[("grp", c)] = ring.tile([P, 4 * 1024], BF16, tag="kvg", bufs=1, name="kv_grp", align_bytes=64)
-            grp_w = vst[("grp", c)][:].bitcast(F32).rearrange("p (t g k u) -> p t g k u", t=4, g=2, u=2)
+                st[("kvg", c)] = ring.tile([P, 4 * 1024], BF16, tag="kvg", bufs=1, name="kv_grp", align_bytes=64)
+            grp_w = st[("kvg", c)][:].bitcast(F32).rearrange("p (t g k u) -> p t g k u", t=4, g=2, u=2)
             for t in (2 * half, 2 * half + 1):
                 xt = psum.tile([P, 4, P], F32, tag="s", bufs=4, name="xt")
-                kw = vst[("kv", c)][:, t, :].bitcast(F32)
+                kw = st[("kv", c)][:, t, :].bitcast(F32)
                 for w in range(4):
                     nc.tensor.transpose(xt[:, w, :], kw[:, w * P:(w + 1) * P], ident_f[:])
                 nc.vector.tensor_copy(out=grp_w[:, t], in_=xt[:].rearrange("p (g u) k -> p g k u", u=2))
@@ -160,12 +158,12 @@ def tile_groupedqueryattention_pa_t_kernel(tc, xq, xk_rep, kv, mask, Wv, out):
         def kv_quantise(c):
             kv_codes = ring.tile([P, 1024], U32, tag="kvc", bufs=1, name="kv_codes", align_bytes=64)
             kv_scales = ring.tile([P, 1024], U8, tag="kvs", bufs=1, name="kv_scales", align_bytes=64)
-            nc.vector.quantize_mx(out=kv_codes[:].bitcast(FP8X4), scales=kv_scales[:], in_=vst[("grp", c)][:])
-            vst[("codes", c)] = (kv_codes, kv_scales)
+            nc.vector.quantize_mx(out=kv_codes[:].bitcast(FP8X4), scales=kv_scales[:], in_=st[("kvg", c)][:])
+            st[("kvc", c)] = (kv_codes, kv_scales)
 
         def xv_matmul(c):
-            kv_codes, kv_scales = vst[("codes", c)]
-            xv_ps = psum.tile([P, 4, HD], F32, tag="o", bufs=1, name="xv_ps")
+            kv_codes, kv_scales = st[("kvc", c)]
+            xv_ps = et_bank(F32, [P, 4, HD], "xv_ps")
             for t in range(4):
                 for gg in range(2):
                     cols = slice((t * 2 + gg) * P, (t * 2 + gg + 1) * P)
@@ -179,28 +177,25 @@ def tile_groupedqueryattention_pa_t_kernel(tc, xq, xk_rep, kv, mask, Wv, out):
                         start=(gg == 0),
                         stop=(gg == 1),
                     )
-            vst[("xv", c)] = xv_ps
+            st[("xv", c)] = xv_ps
 
         def xv_leave(c):
             if c % 2 == 0:
-                vst[("vg", c // 2)] = ring.tile([P, 2, HD, 4], BF16, tag="vg", bufs=1, name="v_grp", align_bytes=64)
-            nc.vector.tensor_copy(
-                out=vst[("vg", c // 2)][:, c % 2], in_=vst[("xv", c)][:].rearrange("p t f -> p f t")
-            )
+                st[("vg", c // 2)] = ring.tile([P, 2, HD, 4], BF16, tag="vg", bufs=1, name="v_grp", align_bytes=64)
+            nc.vector.tensor_copy(out=st[("vg", c // 2)][:, c % 2], in_=st[("xv", c)][:].rearrange("p t f -> p f t"))
 
         def v_quantise(b):
             vc = keep.tile([P, 2 * HD], U32, name="v_codes%d" % b, align_bytes=64)
             vs = keep.tile([P, 2 * HD], U8, name="v_scales%d" % b, align_bytes=64)
             nc.vector.quantize_mx(
-                out=vc[:].bitcast(FP8X4), scales=vs[:], in_=vst[("vg", b)][:].rearrange("p g f t -> p (g f t)")
+                out=vc[:].bitcast(FP8X4), scales=vs[:], in_=st[("vg", b)][:].rearrange("p g f t -> p (g f t)")
             )
-            v_codes.append(vc)
-            v_scales.append(vs)
+            st[("v", b)] = (vc, vs)
 
-        units = [(qt, b, h) for qt in range(NQT) for b in range(B) for h in range(H)]
+        groups = [(0, 0), (1, 0), (0, 1), (1, 1)] + [(qt, b) for qt in range(2, NQT) for b in range(B)]
+        units = [(qt, b, h) for (qt, b) in groups for h in range(H)]
         NU = len(units)
-        NG = NU // H
-        st = {}
+        NG = len(groups)
 
         def scores(u):
             qt, b, h = units[u]
@@ -208,26 +203,24 @@ def tile_groupedqueryattention_pa_t_kernel(tc, xq, xk_rep, kv, mask, Wv, out):
             for c in range(2):
                 s_ps = psum.tile([P, 512], F32, tag="s", bufs=4, name="s_ps")
                 nc.tensor.matmul(
-                    s_ps[:], lhsT=qTs[qt][:, b * H + h, :], rhs=kT[:, b, h, c * 512:(c + 1) * 512],
+                    s_ps[:], lhsT=st[("qT", qt)][:, b * H + h, :], rhs=kT[:, b, h, c * 512:(c + 1) * 512],
                     start=True, stop=False,
                 )
-                banks.append(s_ps)
-            for c in range(2):
                 for jj in range(4):
                     nc.tensor.matmul(
-                        banks[c][:, jj * P:(jj + 1) * P], lhsT=yT[:, qt, 4 * c + jj, :], rhs=ident_f[:],
+                        s_ps[:, jj * P:(jj + 1) * P], lhsT=yT[:, qt, 4 * c + jj, :], rhs=ident_f[:],
                         is_transpose=True, start=False, stop=(jj == 3),
                     )
+                banks.append(s_ps)
             st[("s", u)] = banks
 
         def leave_psum(u, c):
             if c == 0:
                 st[("t", u)] = ring.tile([P, SKV], F32, tag="t", bufs=4, name="t")
                 st[("m0", u)] = ring.tile([P, 1], F32, tag="m0", bufs=3, name="m0")
-                st[("m", u)] = ring.tile([P, 1], F32, tag="m", bufs=4, name="m")
-            t = st[("t", u)]
+                st[("m", u)] = ring.tile([P, 1], F32, tag="m", bufs=5, name="m")
             nc.vector.tensor_scalar(
-                out=t[:, c * 512:(c + 1) * 512],
+                out=st[("t", u)][:, c * 512:(c + 1) * 512],
                 in0=st[("s", u)][c][:],
                 scalar1=-SCALE,
                 scalar2=(None if c == 0 else st[("m0", u)][:, 0:1]),
@@ -237,10 +230,10 @@ def tile_groupedqueryattention_pa_t_kernel(tc, xq, xk_rep, kv, mask, Wv, out):
             )
 
         def exponent(u):
-            qt, b, h = units[u]
+            h = u % H
             g = u // H
             if h == 0:
-                st[("rs", g)] = ring.tile([P, H], F32, tag="rs", bufs=5, name="rowsum")
+                st[("rs", g)] = ring.tile([P, H], F32, tag="rs", bufs=6, name="rowsum")
             e = ring.tile([P, SKV], BF16, tag="e", bufs=3, name="e")
             nc.scalar.activation(
                 out=e[:], in_=st[("t", u)][:], func=ACT.Exp, bias=st[("m", u)][:, 0:1], scale=-1.0,
@@ -250,7 +243,7 @@ def tile_groupedqueryattention_pa_t_kernel(tc, xq, xk_rep, kv, mask, Wv, out):
 
         def transposes(u):
             e = st[("e", u)]
-            et_ps = psum.tile([P, NKT, P], BF16, tag="et", bufs=2, name="et_ps")
+            et_ps = et_bank(BF16, [P, NKT, P], "et_ps")
             for j in range(NKT):
                 nc.tensor.transpose(et_ps[:, j, :], e[:, j * P:(j + 1) * P], ident_bf[:])
             st[("et", u)] = et_ps
@@ -279,7 +272,8 @@ def tile_groupedqueryattention_pa_t_kernel(tc, xq, xk_rep, kv, mask, Wv, out):
             )
 
         def weighted_sum(g):
-            qt, b, h0 = units[g * H]
+            qt, b = groups[g]
+            vc, vs = st[("v", b)]
             o_ps = psum.tile([P, H, HD], F32, tag="o", bufs=1, name="o_ps")
             for h in range(H):
                 for gg in range(2):
@@ -289,15 +283,15 @@ def tile_groupedqueryattention_pa_t_kernel(tc, xq, xk_rep, kv, mask, Wv, out):
                         out=o_ps[:, h, :],
                         lhsT=st[("ec", g)][:, cols].bitcast(FP8X4),
                         lhsT_scale=st[("es", g)][:, cols],
-                        rhs=v_codes[b][:, vcols].bitcast(FP8X4),
-                        rhs_scale=v_scales[b][:, vcols],
+                        rhs=vc[:, vcols].bitcast(FP8X4),
+                        rhs_scale=vs[:, vcols],
                         start=(gg == 0),
                         stop=(gg == 1),
                     )
             st[("o", g)] = o_ps
 
         def normalise(g):
-            qt, b, h0 = units[g * H]
+            qt, b = groups[g]
             o_ps = st[("o", g)]
             rinv = ring.tile([P, H], F32, tag="ri", bufs=2, name="rinv")
             nc.vector.reciprocal(rinv[:], st[("rs", g)][:])
@@ -312,18 +306,40 @@ def tile_groupedqueryattention_pa_t_kernel(tc, xq, xk_rep, kv, mask, Wv, out):
                 )
             nc.sync.dma_start(out=out[b, qt * P:(qt + 1) * P, :], in_=o_sb[:].rearrange("p h j r -> p (h j r)"))
 
-        LAG_PV = 15
-        KV_AT = (4, 6, 8, 10)
+        load_mask(0)
+        load_xk(0)
+        load_xq(0)
+        load_mask(1)
+        load_xq(1)
+        for qt in range(2, 6):
+            load_mask(qt)
+        seed(0)
+        for h in range(H):
+            kT_transposes(0, h)
+            kT_leave(0, h)
+        for qt in range(2):
+            qT_transposes(qt)
+            qT_leave(qt)
+        for qt in range(1, 12):
+            seed(qt)
+        load_xk(1)
+        wv_load()
         kv_load(0)
-        kv_load(1)
-        for tk in range(NU + LAG_PV + 2):
-            if tk % 8 == 0 and tk // 8 + 1 < NQT:
-                st[("xq", tk // 8 + 1)] = load_xq(tk // 8 + 1)
-            for c in (2, 3):
-                if tk == KV_AT[c - 2] + 2:
+
+        first_use = {}
+        for u in range(NU):
+            if units[u][0] not in first_use:
+                first_use[units[u][0]] = u
+
+        for tk in range(NU + LAG_NORM + 1):
+            for qt in range(2, NQT):
+                if tk == first_use[qt] - 10:
+                    load_xq(qt)
+            for c in (1, 2, 3):
+                if tk == KV_AT[c - 1] + 2:
                     kv_load(c)
-            if 0 <= tk - 3 < NU:
-                transposes(tk - 3)
+            if 0 <= tk - LAG_TR < NU:
+                transposes(tk - LAG_TR)
             if tk < NU:
                 scores(tk)
             if tk >= LAG_PV and (tk - LAG_PV) % H == 0 and (tk - LAG_PV) // H < NG:
@@ -331,34 +347,41 @@ def tile_groupedqueryattention_pa_t_kernel(tc, xq, xk_rep, kv, mask, Wv, out):
             if tk == 0:
                 for qt in range(12, NQT):
                     seed(qt)
+            if 2 <= tk < 2 + H:
+                kT_transposes(1, tk - 2)
+            for qt in range(2, NQT):
+                if tk == first_use[qt] - 6:
+                    qT_transposes(qt)
+            for c in range(4):
+                if tk == KV_AT[c] + 4:
+                    xv_matmul(c)
+            if 0 <= tk - LAG_LEAVE < NU:
+                leave_psum(tk - LAG_LEAVE, 0)
+            if 0 <= tk - LAG_QUANT < NU:
+                quantise(tk - LAG_QUANT)
+            if 0 <= tk - LAG_LEAVE < NU:
+                leave_psum(tk - LAG_LEAVE, 1)
+            if 0 <= tk - LAG_EXP < NU:
+                exponent(tk - LAG_EXP)
+            if 0 <= tk - LAG_REGROUP < NU:
+                regroup(tk - LAG_REGROUP)
+            for qt in range(2, NQT):
+                if tk == first_use[qt] - 4:
+                    qT_leave(qt)
+            if tk >= LAG_NORM and (tk - LAG_NORM) % H == 0 and (tk - LAG_NORM) // H < NG:
+                normalise((tk - LAG_NORM) // H)
+            if 4 <= tk < 4 + H:
+                kT_leave(1, tk - 4)
             if tk == 2:
-                build_kT(1, xk1)
-            if tk % 8 == 4 and tk // 8 + 1 < NQT:
-                qTs[tk // 8 + 1] = build_qT(st[("xq", tk // 8 + 1)])
-            if 0 <= tk - 1 < NU:
-                leave_psum(tk - 1, 0)
-            if 0 <= tk - 5 < NU:
-                quantise(tk - 5)
-            if 0 <= tk - 1 < NU:
-                leave_psum(tk - 1, 1)
-            if 0 <= tk - 2 < NU:
-                exponent(tk - 2)
-            if 0 <= tk - 4 < NU:
-                regroup(tk - 4)
-            if tk >= LAG_PV + 1 and (tk - LAG_PV - 1) % H == 0 and (tk - LAG_PV - 1) // H < NG:
-                normalise((tk - LAG_PV - 1) // H)
-            if tk == 3:
                 wv_regroup()
-            if tk == 4:
+            if tk == 3:
                 wv_quantise()
             for c in range(4):
                 if tk == KV_AT[c] + 2:
                     kv_quantise(c)
-                if tk == KV_AT[c] + 3:
-                    xv_matmul(c)
-                if tk == KV_AT[c] + 4:
+                if tk == KV_AT[c] + 6:
                     xv_leave(c)
-                if tk == KV_AT[c] + 5 and c % 2 == 1:
+                if tk == KV_AT[c] + 7 and c % 2 == 1:
                     v_quantise(c // 2)
             for c in range(4):
                 if tk == KV_AT[c]:

@@ -46,7 +46,7 @@ def tile_groupedqueryattention_pa_t_kernel(tc, xq, xk_rep, kv, mask, Wv, out):
         mask_v = mask.rearrange("a c (t p) k -> p (a c t) k", p=P)
         xq_v = xq.rearrange("b (t p) c -> p b t c", p=P)
         xk_v = xk_rep.rearrange("b (j p) c -> p b j c", p=P)
-        kv_v = kv.rearrange("b (j p) c -> p b j c", p=P)
+        kv_v = kv.rearrange("b (g u p e) c -> p b g u e c", g=2, u=2, e=2)
 
         ident_bf = keep.tile([P, P], BF16, name="ident_bf")
         make_identity(nc, ident_bf[:])
@@ -141,7 +141,9 @@ def tile_groupedqueryattention_pa_t_kernel(tc, xq, xk_rep, kv, mask, Wv, out):
 
         def kv_load(c):
             kv_sb = ring.tile([P, 4, DIN], BF16, tag="kv", bufs=1, name="kv_sb")
-            nc.sync.dma_start(out=kv_sb[:], in_=kv_v[:, c // 2, 4 * (c % 2):4 * (c % 2) + 4, :])
+            nc.sync.dma_start(
+                out=kv_sb[:].rearrange("p (u e) c -> p u e c", e=2), in_=kv_v[:, c // 2, c % 2]
+            )
             st[("kv", c)] = kv_sb
 
         def kv_transpose(c, half):
@@ -243,19 +245,21 @@ def tile_groupedqueryattention_pa_t_kernel(tc, xq, xk_rep, kv, mask, Wv, out):
 
         def transposes(u):
             e = st[("e", u)]
-            et_ps = et_bank(BF16, [P, NKT, P], "et_ps")
-            for j in range(NKT):
-                nc.tensor.transpose(et_ps[:, j, :], e[:, j * P:(j + 1) * P], ident_bf[:])
+            et_ps = et_bank(F32, [P, 4, P], "et_ps")
+            ew = e[:].bitcast(F32)
+            for w in range(4):
+                nc.tensor.transpose(et_ps[:, w, :], ew[:, w * P:(w + 1) * P], ident_f[:])
             st[("et", u)] = et_ps
 
         def regroup(u):
             h = u % H
-            et_grp = ring.tile([P, 2, P, 4], BF16, tag="etg", bufs=3, name="et_grp", align_bytes=64)
-            src = st[("et", u)][:].rearrange("p (g t) q -> p g q t", t=4)
+            et_grp = ring.tile([P, 2 * P * 4], BF16, tag="etg", bufs=3, name="et_grp", align_bytes=64)
+            src = st[("et", u)][:].rearrange("p (g u) q -> p g q u", u=2)
+            dst = et_grp[:].bitcast(F32).rearrange("p (g q u) -> p g q u", g=2, u=2)
             if h in REGROUP_ON_VECTOR:
-                nc.vector.tensor_copy(out=et_grp[:], in_=src)
+                nc.vector.tensor_copy(out=dst, in_=src)
             else:
-                nc.scalar.copy(out=et_grp[:], in_=src)
+                nc.scalar.copy(out=dst, in_=src)
             st[("etg", u)] = et_grp
 
         def quantise(u):
@@ -268,7 +272,7 @@ def tile_groupedqueryattention_pa_t_kernel(tc, xq, xk_rep, kv, mask, Wv, out):
             nc.vector.quantize_mx(
                 out=st[("ec", g)][:, cols].bitcast(FP8X4),
                 scales=st[("es", g)][:, cols],
-                in_=st[("etg", u)][:].rearrange("p g q t -> p (g q t)"),
+                in_=st[("etg", u)][:],
             )
 
         def weighted_sum(g):

@@ -204,14 +204,15 @@ def tile_groupedqueryattention_pa_t_kernel(tc, xq, xk_rep, kv, mask, Wv, out):
             banks = []
             for c in range(2):
                 s_ps = psum.tile([P, 512], F32, tag="s", bufs=4, name="s_ps")
-                nc.tensor.matmul(
-                    s_ps[:], lhsT=st[("qT", qt)][:, b * H + h, :], rhs=kT[:, b, h, c * 512:(c + 1) * 512],
-                    start=True, stop=False,
-                )
                 for jj in range(4):
+                    j = 4 * c + jj
                     nc.tensor.matmul(
-                        s_ps[:, jj * P:(jj + 1) * P], lhsT=yT[:, qt, 4 * c + jj, :], rhs=ident_f[:],
-                        is_transpose=True, start=False, stop=(jj == 3),
+                        s_ps[:, jj * P:(jj + 1) * P], lhsT=yT[:, qt, j, :], rhs=ident_f[:],
+                        is_transpose=True, start=True, stop=False,
+                    )
+                    nc.tensor.matmul(
+                        s_ps[:, jj * P:(jj + 1) * P], lhsT=st[("qT", qt)][:, b * H + h, :],
+                        rhs=kT[:, b, h, j * P:(j + 1) * P], start=False, stop=True,
                     )
                 banks.append(s_ps)
             st[("s", u)] = banks

@@ -23,7 +23,7 @@ DIST = HD // REP
 SCALE = 1.0 / math.sqrt(HD)
 ROOT = math.sqrt(HD)
 FLOPS = 2 * B * SKV * DIN * HD + 2 * 2 * B * H * SQ * SKV * HD
-REGROUP_ON_VECTOR = (3,)
+REGROUP_ON_VECTOR = ()
 
 LAG_LEAVE = 1
 LAG_EXP = 3
@@ -53,8 +53,10 @@ def tile_groupedqueryattention_pa_t_kernel(tc, xq, xk_rep, kv, mask, Wv, out):
         ident_f = keep.tile([P, P], F32, name="ident_f")
         make_identity(nc, ident_f[:])
 
-        xT = keep.tile([P, NQT, NKT, P], BF16, name="xT")
-        yT = keep.tile([P, NQT, NKT, P], F32, name="yT")
+        xT = keep.tile([P, NQT, 4, P], BF16, name="xT")
+        yT = keep.tile([P, NQT, 4, P], F32, name="yT")
+        mN = keep.tile([P, NQT, 512], BF16, name="mN")
+        yN = keep.tile([P, NQT, 512], F32, name="yN")
         kT = keep.tile([P, B, H, SKV], BF16, name="kT")
 
         st = {}
@@ -62,10 +64,11 @@ def tile_groupedqueryattention_pa_t_kernel(tc, xq, xk_rep, kv, mask, Wv, out):
         def et_bank(dtype, shape, name):
             return psum.tile(shape, dtype, tag="et", bufs=3, name=name)
 
-        def load_mask(qt):
-            m_sb = ring.tile([P, SKV], BF16, tag="mraw", bufs=6, name="m_sb")
-            nc.sync.dma_start(out=m_sb[:], in_=mask_v[:, qt, :])
-            st[("mraw", qt)] = m_sb
+        def load_mask(i):
+            m_sb = ring.tile([P, 2, 512], BF16, tag="mraw", bufs=4, name="m_sb")
+            nc.sync.dma_start(out=m_sb[:], in_=mask_v[:, 2 * i:2 * i + 2, 0:512])
+            nc.sync.dma_start(out=mN[:, 2 * i:2 * i + 2, :], in_=mask_v[:, 2 * i:2 * i + 2, 512:1024])
+            st[("mraw", i)] = m_sb
 
         def load_xk(b):
             xk_sb = ring.tile([P, NKT, H * HD], BF16, tag="xk", bufs=1, name="xk_sb")
@@ -77,28 +80,30 @@ def tile_groupedqueryattention_pa_t_kernel(tc, xq, xk_rep, kv, mask, Wv, out):
             nc.sync.dma_start(out=xq_sb[:], in_=xq_v[:, :, qt, :])
             st[("xq", qt)] = xq_sb
 
-        def newton(qt, c, eng):
-            y = yT[:, qt, 4 * c:4 * c + 4, :]
+        def newton(y, x, c1, c2, eng):
             eng.tensor_tensor(out=y, in0=y, in1=y, op=ALU.mult)
-            a = ring.tile([P, 4, P], F32, tag="nt", bufs=2, name="a")
-            eng.tensor_tensor(out=a[:], in0=y, in1=xT[:, qt, 4 * c:4 * c + 4, :], op=ALU.mult)
-            eng.tensor_scalar(out=a[:], in0=a[:], scalar1=ROOT, scalar2=-2.0 * ROOT, op0=ALU.mult, op1=ALU.add)
+            a = ring.tile([P, 512], F32, tag="nt", bufs=2, name="a")
+            eng.tensor_tensor(out=a[:], in0=y, in1=x, op=ALU.mult)
+            eng.tensor_scalar(out=a[:], in0=a[:], scalar1=c1, scalar2=c2, op0=ALU.mult, op1=ALU.add)
             eng.tensor_tensor(out=y, in0=y, in1=a[:], op=ALU.mult)
 
-        def seed(qt):
-            m_sb = st[("mraw", qt)]
-            ps = et_bank(BF16, [P, NKT, P], "mt_ps")
-            for j in range(NKT):
-                nc.tensor.transpose(ps[:, j, :], m_sb[:, j * P:(j + 1) * P], ident_bf[:])
-            nc.vector.tensor_copy(out=xT[:, qt], in_=ps[:])
-            nc.scalar.activation(out=yT[:, qt], in_=xT[:, qt], func=ACT.Abs_reciprocal_sqrt)
-            if qt + 6 < NQT:
-                load_mask(qt + 6)
-            if qt == 0:
-                newton(0, 0, nc.vector)
-            else:
-                newton(qt, 0, nc.gpsimd)
-            newton(qt, 1, nc.gpsimd)
+        def seed(i):
+            m_sb = st[("mraw", i)]
+            ps = et_bank(BF16, [P, 2, 4, P], "mt_ps")
+            for a2 in range(2):
+                for j in range(4):
+                    nc.tensor.transpose(ps[:, a2, j, :], m_sb[:, a2, j * P:(j + 1) * P], ident_bf[:])
+            nc.vector.tensor_copy(out=xT[:, 2 * i:2 * i + 2], in_=ps[:])
+            nc.scalar.activation(out=yT[:, 2 * i:2 * i + 2], in_=xT[:, 2 * i:2 * i + 2], func=ACT.Abs_reciprocal_sqrt)
+            nc.scalar.activation(out=yN[:, 2 * i:2 * i + 2], in_=mN[:, 2 * i:2 * i + 2], func=ACT.Abs_reciprocal_sqrt)
+            if i + 4 < NQT // 2:
+                load_mask(i + 4)
+            for qt in (2 * i, 2 * i + 1):
+                newton(
+                    yT[:, qt].rearrange("p j q -> p (j q)"), xT[:, qt].rearrange("p j q -> p (j q)"),
+                    ROOT, -2.0 * ROOT, nc.vector if qt == 0 else nc.gpsimd,
+                )
+                newton(yN[:, qt], mN[:, qt], -1.0, 2.0, nc.gpsimd)
 
         def kT_transposes(b, h):
             ps = et_bank(BF16, [P, NKT, P], "kt_ps")
@@ -107,7 +112,11 @@ def tile_groupedqueryattention_pa_t_kernel(tc, xq, xk_rep, kv, mask, Wv, out):
             st[("ktps", b, h)] = ps
 
         def kT_leave(b, h):
-            nc.vector.tensor_copy(out=kT[:, b, h, :], in_=st[("ktps", b, h)][:].rearrange("p j k -> p (j k)"))
+            src = st[("ktps", b, h)][:].rearrange("p j k -> p (j k)")
+            if b == 0:
+                nc.vector.tensor_copy(out=kT[:, b, h, :], in_=src)
+            else:
+                nc.scalar.copy(out=kT[:, b, h, :], in_=src)
 
         def qT_transposes(qt):
             ps = et_bank(BF16, [P, B * H, P], "qt_ps")
@@ -155,7 +164,7 @@ def tile_groupedqueryattention_pa_t_kernel(tc, xq, xk_rep, kv, mask, Wv, out):
                 kw = st[("kv", c)][:, t, :].bitcast(F32)
                 for w in range(4):
                     nc.tensor.transpose(xt[:, w, :], kw[:, w * P:(w + 1) * P], ident_f[:])
-                nc.vector.tensor_copy(out=grp_w[:, t], in_=xt[:].rearrange("p (g u) k -> p g k u", u=2))
+                nc.scalar.copy(out=grp_w[:, t], in_=xt[:].rearrange("p (g u) k -> p g k u", u=2))
 
         def kv_quantise(c):
             kv_codes = ring.tile([P, 1024], U32, tag="kvc", bufs=1, name="kv_codes", align_bytes=64)
@@ -184,7 +193,7 @@ def tile_groupedqueryattention_pa_t_kernel(tc, xq, xk_rep, kv, mask, Wv, out):
         def xv_leave(c):
             if c % 2 == 0:
                 st[("vg", c // 2)] = ring.tile([P, 2, HD, 4], BF16, tag="vg", bufs=1, name="v_grp", align_bytes=64)
-            nc.vector.tensor_copy(out=st[("vg", c // 2)][:, c % 2], in_=st[("xv", c)][:].rearrange("p t f -> p f t"))
+            nc.scalar.copy(out=st[("vg", c // 2)][:, c % 2], in_=st[("xv", c)][:].rearrange("p t f -> p f t"))
 
         def v_quantise(b):
             vc = keep.tile([P, 2 * HD], U32, name="v_codes%d" % b, align_bytes=64)
@@ -204,16 +213,16 @@ def tile_groupedqueryattention_pa_t_kernel(tc, xq, xk_rep, kv, mask, Wv, out):
             banks = []
             for c in range(2):
                 s_ps = psum.tile([P, 512], F32, tag="s", bufs=4, name="s_ps")
-                for jj in range(4):
-                    j = 4 * c + jj
-                    nc.tensor.matmul(
-                        s_ps[:, jj * P:(jj + 1) * P], lhsT=yT[:, qt, j, :], rhs=ident_f[:],
-                        is_transpose=True, start=True, stop=False,
-                    )
-                    nc.tensor.matmul(
-                        s_ps[:, jj * P:(jj + 1) * P], lhsT=st[("qT", qt)][:, b * H + h, :],
-                        rhs=kT[:, b, h, j * P:(j + 1) * P], start=False, stop=True,
-                    )
+                nc.tensor.matmul(
+                    s_ps[:], lhsT=st[("qT", qt)][:, b * H + h, :], rhs=kT[:, b, h, c * 512:(c + 1) * 512],
+                    start=True, stop=(c == 1),
+                )
+                if c == 0:
+                    for jj in range(4):
+                        nc.tensor.matmul(
+                            s_ps[:, jj * P:(jj + 1) * P], lhsT=yT[:, qt, jj, :], rhs=ident_f[:],
+                            is_transpose=True, start=False, stop=(jj == 3),
+                        )
                 banks.append(s_ps)
             st[("s", u)] = banks
 
@@ -222,15 +231,22 @@ def tile_groupedqueryattention_pa_t_kernel(tc, xq, xk_rep, kv, mask, Wv, out):
                 st[("t", u)] = ring.tile([P, SKV], F32, tag="t", bufs=4, name="t")
                 st[("m0", u)] = ring.tile([P, 1], F32, tag="m0", bufs=3, name="m0")
                 st[("m", u)] = ring.tile([P, 1], F32, tag="m", bufs=5, name="m")
-            nc.vector.tensor_scalar(
-                out=st[("t", u)][:, c * 512:(c + 1) * 512],
-                in0=st[("s", u)][c][:],
-                scalar1=-SCALE,
-                scalar2=(None if c == 0 else st[("m0", u)][:, 0:1]),
-                op0=ALU.mult,
-                op1=ALU.min,
-                accum_out=(st[("m0", u)][:] if c == 0 else st[("m", u)][:]),
-            )
+            t = st[("t", u)]
+            if c == 0:
+                nc.vector.tensor_scalar(
+                    out=t[:, 0:512], in0=st[("s", u)][0][:], scalar1=-SCALE, scalar2=None,
+                    op0=ALU.mult, op1=ALU.min, accum_out=st[("m0", u)][:],
+                )
+            if c == 1:
+                nc.vector.scalar_tensor_tensor(
+                    out=t[:, 512:1024], in0=st[("s", u)][1][:], scalar=-SCALE, in1=yN[:, units[u][0], :],
+                    op0=ALU.mult, op1=ALU.add,
+                )
+            if c == 2:
+                nc.vector.tensor_scalar(
+                    out=t[:, 512:1024], in0=t[:, 512:1024], scalar1=1.0, scalar2=st[("m0", u)][:, 0:1],
+                    op0=ALU.mult, op1=ALU.min, accum_out=st[("m", u)][:],
+                )
 
         def exponent(u):
             h = u % H
@@ -314,10 +330,9 @@ def tile_groupedqueryattention_pa_t_kernel(tc, xq, xk_rep, kv, mask, Wv, out):
         load_mask(0)
         load_xk(0)
         load_xq(0)
-        load_mask(1)
         load_xq(1)
-        for qt in range(2, 6):
-            load_mask(qt)
+        for i in range(1, 4):
+            load_mask(i)
         seed(0)
         for h in range(H):
             kT_transposes(0, h)
@@ -325,8 +340,8 @@ def tile_groupedqueryattention_pa_t_kernel(tc, xq, xk_rep, kv, mask, Wv, out):
         for qt in range(2):
             qT_transposes(qt)
             qT_leave(qt)
-        for qt in range(1, 12):
-            seed(qt)
+        for i in range(1, 6):
+            seed(i)
         load_xk(1)
         wv_load()
         kv_load(0)
@@ -350,8 +365,8 @@ def tile_groupedqueryattention_pa_t_kernel(tc, xq, xk_rep, kv, mask, Wv, out):
             if tk >= LAG_PV and (tk - LAG_PV) % H == 0 and (tk - LAG_PV) // H < NG:
                 weighted_sum((tk - LAG_PV) // H)
             if tk == 0:
-                for qt in range(12, NQT):
-                    seed(qt)
+                for i in range(6, NQT // 2):
+                    seed(i)
             if 2 <= tk < 2 + H:
                 kT_transposes(1, tk - 2)
             for qt in range(2, NQT):
@@ -362,10 +377,11 @@ def tile_groupedqueryattention_pa_t_kernel(tc, xq, xk_rep, kv, mask, Wv, out):
                     xv_matmul(c)
             if 0 <= tk - LAG_LEAVE < NU:
                 leave_psum(tk - LAG_LEAVE, 0)
+                leave_psum(tk - LAG_LEAVE, 1)
             if 0 <= tk - LAG_QUANT < NU:
                 quantise(tk - LAG_QUANT)
             if 0 <= tk - LAG_LEAVE < NU:
-                leave_psum(tk - LAG_LEAVE, 1)
+                leave_psum(tk - LAG_LEAVE, 2)
             if 0 <= tk - LAG_EXP < NU:
                 exponent(tk - LAG_EXP)
             if 0 <= tk - LAG_REGROUP < NU:

@@ -26,11 +26,13 @@ FLOPS = 2 * B * SKV * DIN * HD + 2 * 2 * B * H * SQ * SKV * HD
 REGROUP_ON_VECTOR = ()
 
 LAG_LEAVE = 1
-LAG_EXP = 3
-LAG_TR = 5
-LAG_REGROUP = 6
-LAG_QUANT = 8
+LAG_MIN = 2
+LAG_EXP = 4
+LAG_TR = 6
+LAG_REGROUP = 7
+LAG_QUANT = 9
 LAG_PV = 16
+LAG_RECIP = 14
 LAG_NORM = 18
 KV_AT = (3, 7, 11, 15)
 
@@ -53,10 +55,8 @@ def tile_groupedqueryattention_pa_t_kernel(tc, xq, xk_rep, kv, mask, Wv, out):
         ident_f = keep.tile([P, P], F32, name="ident_f")
         make_identity(nc, ident_f[:])
 
-        xT = keep.tile([P, NQT, 4, P], BF16, name="xT")
-        yT = keep.tile([P, NQT, 4, P], F32, name="yT")
-        mN = keep.tile([P, NQT, 512], BF16, name="mN")
-        yN = keep.tile([P, NQT, 512], F32, name="yN")
+        xT = keep.tile([P, NQT, NKT, P], BF16, name="xT")
+        yT = keep.tile([P, NQT, NKT, P], F32, name="yT")
         kT = keep.tile([P, B, H, SKV], BF16, name="kT")
 
         st = {}
@@ -64,11 +64,10 @@ def tile_groupedqueryattention_pa_t_kernel(tc, xq, xk_rep, kv, mask, Wv, out):
         def et_bank(dtype, shape, name):
             return psum.tile(shape, dtype, tag="et", bufs=3, name=name)
 
-        def load_mask(i):
-            m_sb = ring.tile([P, 2, 512], BF16, tag="mraw", bufs=4, name="m_sb")
-            nc.sync.dma_start(out=m_sb[:], in_=mask_v[:, 2 * i:2 * i + 2, 0:512])
-            nc.sync.dma_start(out=mN[:, 2 * i:2 * i + 2, :], in_=mask_v[:, 2 * i:2 * i + 2, 512:1024])
-            st[("mraw", i)] = m_sb
+        def load_mask(qt):
+            m_sb = ring.tile([P, SKV], BF16, tag="mraw", bufs=4, name="m_sb")
+            nc.sync.dma_start(out=m_sb[:], in_=mask_v[:, qt, :])
+            st[("mraw", qt)] = m_sb
 
         def load_xk(b):
             xk_sb = ring.tile([P, NKT, H * HD], BF16, tag="xk", bufs=1, name="xk_sb")
@@ -80,30 +79,42 @@ def tile_groupedqueryattention_pa_t_kernel(tc, xq, xk_rep, kv, mask, Wv, out):
             nc.sync.dma_start(out=xq_sb[:], in_=xq_v[:, :, qt, :])
             st[("xq", qt)] = xq_sb
 
-        def newton(y, x, c1, c2, eng):
-            eng.tensor_tensor(out=y, in0=y, in1=y, op=ALU.mult)
-            a = ring.tile([P, 512], F32, tag="nt", bufs=2, name="a")
-            eng.tensor_tensor(out=a[:], in0=y, in1=x, op=ALU.mult)
-            eng.tensor_scalar(out=a[:], in0=a[:], scalar1=c1, scalar2=c2, op0=ALU.mult, op1=ALU.add)
-            eng.tensor_tensor(out=y, in0=y, in1=a[:], op=ALU.mult)
+        def newton(pieces, eng):
+            tmp = []
+            for y, x in pieces:
+                eng.tensor_tensor(out=y, in0=y, in1=y, op=ALU.mult)
+            for y, x in pieces:
+                a = ring.tile([P, NKT * P], F32, tag="nt", bufs=2, name="a")
+                a = a[:, 0:y.shape[1]]
+                eng.tensor_tensor(out=a, in0=y, in1=x, op=ALU.mult)
+                tmp.append(a)
+            for a in tmp:
+                eng.tensor_scalar(out=a, in0=a, scalar1=ROOT, scalar2=-2.0 * ROOT, op0=ALU.mult, op1=ALU.add)
+            for (y, x), a in zip(pieces, tmp):
+                eng.tensor_tensor(out=y, in0=y, in1=a, op=ALU.mult)
 
-        def seed(i):
-            m_sb = st[("mraw", i)]
-            ps = et_bank(BF16, [P, 2, 4, P], "mt_ps")
-            for a2 in range(2):
-                for j in range(4):
-                    nc.tensor.transpose(ps[:, a2, j, :], m_sb[:, a2, j * P:(j + 1) * P], ident_bf[:])
-            nc.vector.tensor_copy(out=xT[:, 2 * i:2 * i + 2], in_=ps[:])
-            nc.scalar.activation(out=yT[:, 2 * i:2 * i + 2], in_=xT[:, 2 * i:2 * i + 2], func=ACT.Abs_reciprocal_sqrt)
-            nc.scalar.activation(out=yN[:, 2 * i:2 * i + 2], in_=mN[:, 2 * i:2 * i + 2], func=ACT.Abs_reciprocal_sqrt)
-            if i + 4 < NQT // 2:
-                load_mask(i + 4)
-            for qt in (2 * i, 2 * i + 1):
-                newton(
-                    yT[:, qt].rearrange("p j q -> p (j q)"), xT[:, qt].rearrange("p j q -> p (j q)"),
-                    ROOT, -2.0 * ROOT, nc.vector if qt == 0 else nc.gpsimd,
-                )
-                newton(yN[:, qt], mN[:, qt], -1.0, 2.0, nc.gpsimd)
+        def piece(qt, lo, hi):
+            return (
+                yT[:, qt, lo:hi, :].rearrange("p j q -> p (j q)"),
+                xT[:, qt, lo:hi, :].rearrange("p j q -> p (j q)"),
+            )
+
+        def seed(qt):
+            m_sb = st[("mraw", qt)]
+            ps = et_bank(BF16, [P, NKT, P], "mt_ps")
+            for j in range(NKT):
+                nc.tensor.transpose(ps[:, j, :], m_sb[:, j * P:(j + 1) * P], ident_bf[:])
+            nc.vector.tensor_copy(out=xT[:, qt], in_=ps[:])
+            nc.scalar.activation(out=yT[:, qt], in_=xT[:, qt], func=ACT.Abs_reciprocal_sqrt)
+            if qt + 4 < NQT:
+                load_mask(qt + 4)
+            if qt == 0:
+                newton([piece(0, 0, 2), piece(0, 2, 4)], nc.vector)
+                newton([piece(0, 4, 6), piece(0, 6, 8)], nc.gpsimd)
+            elif qt == 1:
+                newton([piece(1, 0, 4), piece(1, 4, 8)], nc.gpsimd)
+            elif qt % 2 == 1:
+                newton([piece(qt - 1, 0, 8), piece(qt, 0, 8)], nc.gpsimd)
 
         def kT_transposes(b, h):
             ps = et_bank(BF16, [P, NKT, P], "kt_ps")
@@ -208,52 +219,46 @@ def tile_groupedqueryattention_pa_t_kernel(tc, xq, xk_rep, kv, mask, Wv, out):
         NU = len(units)
         NG = len(groups)
 
-        def scores(u):
+        def scores(u, c):
             qt, b, h = units[u]
-            banks = []
-            for c in range(2):
-                s_ps = psum.tile([P, 512], F32, tag="s", bufs=4, name="s_ps")
+            s_ps = psum.tile([P, 512], F32, tag="s", bufs=4, name="s_ps")
+            nc.tensor.matmul(
+                s_ps[:], lhsT=st[("qT", qt)][:, b * H + h, :], rhs=kT[:, b, h, c * 512:(c + 1) * 512],
+                start=True, stop=False,
+            )
+            for jj in range(4):
                 nc.tensor.matmul(
-                    s_ps[:], lhsT=st[("qT", qt)][:, b * H + h, :], rhs=kT[:, b, h, c * 512:(c + 1) * 512],
-                    start=True, stop=(c == 1),
+                    s_ps[:, jj * P:(jj + 1) * P], lhsT=yT[:, qt, 4 * c + jj, :], rhs=ident_f[:],
+                    is_transpose=True, start=False, stop=(jj == 3),
                 )
-                if c == 0:
-                    for jj in range(4):
-                        nc.tensor.matmul(
-                            s_ps[:, jj * P:(jj + 1) * P], lhsT=yT[:, qt, jj, :], rhs=ident_f[:],
-                            is_transpose=True, start=False, stop=(jj == 3),
-                        )
-                banks.append(s_ps)
-            st[("s", u)] = banks
+            st[("s", u, c)] = s_ps
 
         def leave_psum(u, c):
             if c == 0:
-                st[("t", u)] = ring.tile([P, SKV], F32, tag="t", bufs=4, name="t")
-                st[("m0", u)] = ring.tile([P, 1], F32, tag="m0", bufs=3, name="m0")
-                st[("m", u)] = ring.tile([P, 1], F32, tag="m", bufs=5, name="m")
-            t = st[("t", u)]
-            if c == 0:
-                nc.vector.tensor_scalar(
-                    out=t[:, 0:512], in0=st[("s", u)][0][:], scalar1=-SCALE, scalar2=None,
-                    op0=ALU.mult, op1=ALU.min, accum_out=st[("m0", u)][:],
-                )
-            if c == 1:
-                nc.vector.scalar_tensor_tensor(
-                    out=t[:, 512:1024], in0=st[("s", u)][1][:], scalar=-SCALE, in1=yN[:, units[u][0], :],
-                    op0=ALU.mult, op1=ALU.add,
-                )
-            if c == 2:
-                nc.vector.tensor_scalar(
-                    out=t[:, 512:1024], in0=t[:, 512:1024], scalar1=1.0, scalar2=st[("m0", u)][:, 0:1],
-                    op0=ALU.mult, op1=ALU.min, accum_out=st[("m", u)][:],
-                )
+                st[("t", u)] = ring.tile([P, SKV], F32, tag="t", bufs=5, name="t")
+                st[("mm", u)] = ring.tile([P, 2], F32, tag="mm", bufs=5, name="mm")
+            nc.vector.tensor_scalar(
+                out=st[("t", u)][:, c * 512:(c + 1) * 512],
+                in0=st[("s", u, c)][:],
+                scalar1=-SCALE,
+                scalar2=None,
+                op0=ALU.mult,
+                op1=ALU.min,
+                accum_out=st[("mm", u)][:, c:c + 1],
+            )
+
+        def row_min(u):
+            m = ring.tile([P, 1], F32, tag="m", bufs=5, name="m")
+            mm = st[("mm", u)]
+            nc.vector.tensor_tensor(out=m[:], in0=mm[:, 0:1], in1=mm[:, 1:2], op=ALU.min)
+            st[("m", u)] = m
 
         def exponent(u):
             h = u % H
             g = u // H
             if h == 0:
                 st[("rs", g)] = ring.tile([P, H], F32, tag="rs", bufs=6, name="rowsum")
-            e = ring.tile([P, SKV], BF16, tag="e", bufs=3, name="e")
+            e = ring.tile([P, SKV], BF16, tag="e", bufs=4, name="e")
             nc.scalar.activation(
                 out=e[:], in_=st[("t", u)][:], func=ACT.Exp, bias=st[("m", u)][:, 0:1], scale=-1.0,
                 accum_out=st[("rs", g)][:, h:h + 1],
@@ -270,7 +275,7 @@ def tile_groupedqueryattention_pa_t_kernel(tc, xq, xk_rep, kv, mask, Wv, out):
 
         def regroup(u):
             h = u % H
-            et_grp = ring.tile([P, 2 * P * 4], BF16, tag="etg", bufs=3, name="et_grp", align_bytes=64)
+            et_grp = ring.tile([P, 2 * P * 4], BF16, tag="etg", bufs=4, name="et_grp", align_bytes=64)
             src = st[("et", u)][:].rearrange("p (g u) q -> p g q u", u=2)
             dst = et_grp[:].bitcast(F32).rearrange("p (g q u) -> p g q u", g=2, u=2)
             if h in REGROUP_ON_VECTOR:
@@ -311,11 +316,15 @@ def tile_groupedqueryattention_pa_t_kernel(tc, xq, xk_rep, kv, mask, Wv, out):
                     )
             st[("o", g)] = o_ps
 
+        def reciprocal(g):
+            rinv = ring.tile([P, H], F32, tag="ri", bufs=3, name="rinv")
+            nc.vector.reciprocal(rinv[:], st[("rs", g)][:])
+            st[("ri", g)] = rinv
+
         def normalise(g):
             qt, b = groups[g]
             o_ps = st[("o", g)]
-            rinv = ring.tile([P, H], F32, tag="ri", bufs=2, name="rinv")
-            nc.vector.reciprocal(rinv[:], st[("rs", g)][:])
+            rinv = st[("ri", g)]
             o_sb = ring.tile([P, H, DIST, REP], F32, tag="osb", bufs=2, name="o_sb")
             for h in range(H):
                 nc.vector.tensor_scalar(
@@ -330,9 +339,10 @@ def tile_groupedqueryattention_pa_t_kernel(tc, xq, xk_rep, kv, mask, Wv, out):
         load_mask(0)
         load_xk(0)
         load_xq(0)
+        load_mask(1)
         load_xq(1)
-        for i in range(1, 4):
-            load_mask(i)
+        for qt in range(2, 4):
+            load_mask(qt)
         seed(0)
         for h in range(H):
             kT_transposes(0, h)
@@ -340,8 +350,8 @@ def tile_groupedqueryattention_pa_t_kernel(tc, xq, xk_rep, kv, mask, Wv, out):
         for qt in range(2):
             qT_transposes(qt)
             qT_leave(qt)
-        for i in range(1, 6):
-            seed(i)
+        for qt in range(1, 12):
+            seed(qt)
         load_xk(1)
         wv_load()
         kv_load(0)
@@ -358,15 +368,17 @@ def tile_groupedqueryattention_pa_t_kernel(tc, xq, xk_rep, kv, mask, Wv, out):
             for c in (1, 2, 3):
                 if tk == KV_AT[c - 1] + 2:
                     kv_load(c)
+            if tk < NU:
+                scores(tk, 0)
             if 0 <= tk - LAG_TR < NU:
                 transposes(tk - LAG_TR)
             if tk < NU:
-                scores(tk)
+                scores(tk, 1)
             if tk >= LAG_PV and (tk - LAG_PV) % H == 0 and (tk - LAG_PV) // H < NG:
                 weighted_sum((tk - LAG_PV) // H)
             if tk == 0:
-                for i in range(6, NQT // 2):
-                    seed(i)
+                for qt in range(12, NQT):
+                    seed(qt)
             if 2 <= tk < 2 + H:
                 kT_transposes(1, tk - 2)
             for qt in range(2, NQT):
@@ -380,8 +392,10 @@ def tile_groupedqueryattention_pa_t_kernel(tc, xq, xk_rep, kv, mask, Wv, out):
                 leave_psum(tk - LAG_LEAVE, 1)
             if 0 <= tk - LAG_QUANT < NU:
                 quantise(tk - LAG_QUANT)
-            if 0 <= tk - LAG_LEAVE < NU:
-                leave_psum(tk - LAG_LEAVE, 2)
+            if 0 <= tk - LAG_MIN < NU:
+                row_min(tk - LAG_MIN)
+            if tk >= LAG_RECIP and (tk - LAG_RECIP) % H == 0 and (tk - LAG_RECIP) // H < NG:
+                reciprocal((tk - LAG_RECIP) // H)
             if 0 <= tk - LAG_EXP < NU:
                 exponent(tk - LAG_EXP)
             if 0 <= tk - LAG_REGROUP < NU:

@@ -55,7 +55,6 @@ def tile_groupedqueryattention_pa_t_kernel(tc, xq, xk_rep, kv, mask, Wv, out):
         ident_f = keep.tile([P, P], F32, name="ident_f")
         make_identity(nc, ident_f[:])
 
-        xT = keep.tile([P, NQT, NKT, P], BF16, name="xT")
         yT = keep.tile([P, NQT, NKT, P], F32, name="yT")
         kT = keep.tile([P, B, H, SKV], BF16, name="kT")
 
@@ -79,42 +78,18 @@ def tile_groupedqueryattention_pa_t_kernel(tc, xq, xk_rep, kv, mask, Wv, out):
             nc.sync.dma_start(out=xq_sb[:], in_=xq_v[:, :, qt, :])
             st[("xq", qt)] = xq_sb
 
-        def newton(pieces, eng):
-            tmp = []
-            for y, x in pieces:
-                eng.tensor_tensor(out=y, in0=y, in1=y, op=ALU.mult)
-            for y, x in pieces:
-                a = ring.tile([P, NKT * P], F32, tag="nt", bufs=2, name="a")
-                a = a[:, 0:y.shape[1]]
-                eng.tensor_tensor(out=a, in0=y, in1=x, op=ALU.mult)
-                tmp.append(a)
-            for a in tmp:
-                eng.tensor_scalar(out=a, in0=a, scalar1=ROOT, scalar2=-2.0 * ROOT, op0=ALU.mult, op1=ALU.add)
-            for (y, x), a in zip(pieces, tmp):
-                eng.tensor_tensor(out=y, in0=y, in1=a, op=ALU.mult)
-
-        def piece(qt, lo, hi):
-            return (
-                yT[:, qt, lo:hi, :].rearrange("p j q -> p (j q)"),
-                xT[:, qt, lo:hi, :].rearrange("p j q -> p (j q)"),
-            )
-
         def seed(qt):
             m_sb = st[("mraw", qt)]
             ps = et_bank(BF16, [P, NKT, P], "mt_ps")
             for j in range(NKT):
                 nc.tensor.transpose(ps[:, j, :], m_sb[:, j * P:(j + 1) * P], ident_bf[:])
-            nc.vector.tensor_copy(out=xT[:, qt], in_=ps[:])
-            nc.scalar.activation(out=yT[:, qt], in_=xT[:, qt], func=ACT.Abs_reciprocal_sqrt)
+            nc.scalar.activation(out=yT[:, qt], in_=ps[:], func=ACT.Abs_reciprocal_sqrt, scale=1.0 / ROOT)
             if qt + 4 < NQT:
                 load_mask(qt + 4)
-            if qt == 0:
-                newton([piece(0, 0, 2), piece(0, 2, 4)], nc.vector)
-                newton([piece(0, 4, 6), piece(0, 6, 8)], nc.gpsimd)
-            elif qt == 1:
-                newton([piece(1, 0, 4), piece(1, 4, 8)], nc.gpsimd)
-            elif qt % 2 == 1:
-                newton([piece(qt - 1, 0, 8), piece(qt, 0, 8)], nc.gpsimd)
+            eng = nc.vector if qt < 2 else nc.gpsimd
+            for i in range(4):
+                y = yT[:, qt, 2 * i:2 * i + 2, :]
+                eng.tensor_tensor(out=y, in0=y, in1=y, op=ALU.mult)
 
         def kT_transposes(b, h):
             ps = et_bank(BF16, [P, NKT, P], "kt_ps")
@@ -124,10 +99,7 @@ def tile_groupedqueryattention_pa_t_kernel(tc, xq, xk_rep, kv, mask, Wv, out):
 
         def kT_leave(b, h):
             src = st[("ktps", b, h)][:].rearrange("p j k -> p (j k)")
-            if b == 0:
-                nc.vector.tensor_copy(out=kT[:, b, h, :], in_=src)
-            else:
-                nc.scalar.copy(out=kT[:, b, h, :], in_=src)
+            nc.vector.tensor_scalar(out=kT[:, b, h, :], in0=src, scalar1=-1.0, scalar2=None, op0=ALU.mult)
 
         def qT_transposes(qt):
             ps = et_bank(BF16, [P, B * H, P], "qt_ps")
@@ -240,7 +212,7 @@ def tile_groupedqueryattention_pa_t_kernel(tc, xq, xk_rep, kv, mask, Wv, out):
             nc.vector.tensor_scalar(
                 out=st[("t", u)][:, c * 512:(c + 1) * 512],
                 in0=st[("s", u, c)][:],
-                scalar1=-SCALE,
+                scalar1=SCALE,
                 scalar2=None,
                 op0=ALU.mult,
                 op1=ALU.min,

@@ -26,7 +26,6 @@ FLOPS = 2 * B * SKV * DIN * HD + 2 * 2 * B * H * SQ * SKV * HD
 REGROUP_ON_VECTOR = ()
 
 LAG_LEAVE = 1
-LAG_MIN = 2
 LAG_EXP = 4
 LAG_TR = 6
 LAG_REGROUP = 7
@@ -122,7 +121,11 @@ def tile_groupedqueryattention_pa_t_kernel(tc, xq, xk_rep, kv, mask, Wv, out):
             nc.sync.dma_start(out=wv_raw[:], in_=Wv.rearrange("(g u p e) f -> p g u e f", g=2, u=2, e=2))
 
         def wv_regroup():
-            nc.vector.tensor_copy(out=wv_grp[:], in_=wv_raw[:].rearrange("p g u e f -> p g f (u e)"))
+            for h in range(H):
+                nc.vector.tensor_copy(
+                    out=wv_grp[:, :, (H - 1 - h) * DIST:(H - h) * DIST, :],
+                    in_=wv_raw[:, :, :, :, h * DIST:(h + 1) * DIST].rearrange("p g u e f -> p g f (u e)"),
+                )
 
         def wv_quantise():
             nc.vector.quantize_mx(
@@ -208,22 +211,17 @@ def tile_groupedqueryattention_pa_t_kernel(tc, xq, xk_rep, kv, mask, Wv, out):
         def leave_psum(u, c):
             if c == 0:
                 st[("t", u)] = ring.tile([P, SKV], F32, tag="t", bufs=5, name="t")
-                st[("mm", u)] = ring.tile([P, 2], F32, tag="mm", bufs=5, name="mm")
+                st[("m0", u)] = ring.tile([P, 1], F32, tag="m0", bufs=3, name="m0")
+                st[("m", u)] = ring.tile([P, 1], F32, tag="m", bufs=5, name="m")
             nc.vector.tensor_scalar(
                 out=st[("t", u)][:, c * 512:(c + 1) * 512],
                 in0=st[("s", u, c)][:],
                 scalar1=SCALE,
-                scalar2=None,
+                scalar2=None if c == 0 else st[("m0", u)][:],
                 op0=ALU.mult,
                 op1=ALU.min,
-                accum_out=st[("mm", u)][:, c:c + 1],
+                accum_out=st[("m0", u)][:] if c == 0 else st[("m", u)][:],
             )
-
-        def row_min(u):
-            m = ring.tile([P, 1], F32, tag="m", bufs=5, name="m")
-            mm = st[("mm", u)]
-            nc.vector.tensor_tensor(out=m[:], in0=mm[:, 0:1], in1=mm[:, 1:2], op=ALU.min)
-            st[("m", u)] = m
 
         def exponent(u):
             h = u % H
@@ -297,16 +295,24 @@ def tile_groupedqueryattention_pa_t_kernel(tc, xq, xk_rep, kv, mask, Wv, out):
             qt, b = groups[g]
             o_ps = st[("o", g)]
             rinv = st[("ri", g)]
-            o_sb = ring.tile([P, H, DIST, REP], F32, tag="osb", bufs=2, name="o_sb")
-            for h in range(H):
-                nc.vector.tensor_scalar(
-                    out=o_sb[:, h],
-                    in0=o_ps[:, h, h * DIST:(h + 1) * DIST].unsqueeze(2).to_broadcast([P, DIST, REP]),
-                    scalar1=rinv[:, h:h + 1],
-                    scalar2=None,
-                    op0=ALU.mult,
-                )
-            nc.sync.dma_start(out=out[b, qt * P:(qt + 1) * P, :], in_=o_sb[:].rearrange("p h j r -> p (h j r)"))
+            own = o_ps[:].rearrange("p h f -> p (h f)")[:, HD - DIST:HD - DIST + H * (HD - DIST)]
+            o_n = ring.tile([P, H, DIST], F32, tag="on", bufs=2, name="o_n")
+            nc.vector.tensor_tensor(
+                out=o_n[:],
+                in0=own.rearrange("p (h x) -> p h x", h=H)[:, :, 0:DIST],
+                in1=rinv[:].unsqueeze(2).to_broadcast([P, H, DIST]),
+                op=ALU.mult,
+            )
+            o_sb = ring.tile([P, H * DIST, REP], F32, tag="osb", bufs=2, name="o_sb")
+            nc.gpsimd.tensor_scalar(
+                out=o_sb[:],
+                in0=o_n[:].rearrange("p h j -> p (h j)").unsqueeze(2).to_broadcast([P, H * DIST, REP]),
+                scalar1=1.0,
+                scalar2=0.0,
+                op0=ALU.mult,
+                op1=ALU.add,
+            )
+            nc.sync.dma_start(out=out[b, qt * P:(qt + 1) * P, :], in_=o_sb[:].rearrange("p j r -> p (j r)"))
 
         load_mask(0)
         load_xk(0)
@@ -361,11 +367,10 @@ def tile_groupedqueryattention_pa_t_kernel(tc, xq, xk_rep, kv, mask, Wv, out):
                     xv_matmul(c)
             if 0 <= tk - LAG_LEAVE < NU:
                 leave_psum(tk - LAG_LEAVE, 0)
-                leave_psum(tk - LAG_LEAVE, 1)
             if 0 <= tk - LAG_QUANT < NU:
                 quantise(tk - LAG_QUANT)
-            if 0 <= tk - LAG_MIN < NU:
-                row_min(tk - LAG_MIN)
+            if 0 <= tk - LAG_LEAVE < NU:
+                leave_psum(tk - LAG_LEAVE, 1)
             if tk >= LAG_RECIP and (tk - LAG_RECIP) % H == 0 and (tk - LAG_RECIP) // H < NG:
                 reciprocal((tk - LAG_RECIP) // H)
             if 0 <= tk - LAG_EXP < NU:

@@ -23,7 +23,7 @@ DIST = HD // REP
 SCALE = 1.0 / math.sqrt(HD)
 ROOT = math.sqrt(HD)
 FLOPS = 2 * B * SKV * DIN * HD + 2 * 2 * B * H * SQ * SKV * HD
-REGROUP_ON_VECTOR = ()
+REGROUP_ON_VECTOR = (3,)
 
 LAG_LEAVE = 1
 LAG_EXP = 4
@@ -109,7 +109,7 @@ def tile_groupedqueryattention_pa_t_kernel(tc, xq, xk_rep, kv, mask, Wv, out):
 
         def qT_leave(qt):
             qT = ring.tile([P, B * H, P], BF16, tag="qT", bufs=2, name="qT")
-            nc.scalar.copy(out=qT[:], in_=st[("qtps", qt)][:])
+            nc.vector.tensor_copy(out=qT[:], in_=st[("qtps", qt)][:])
             st[("qT", qt)] = qT
 
         wv_raw = keep.tile([P, 2, 2, 2, HD], BF16, name="wv_raw")
@@ -150,7 +150,7 @@ def tile_groupedqueryattention_pa_t_kernel(tc, xq, xk_rep, kv, mask, Wv, out):
                 kw = st[("kv", c)][:, t, :].bitcast(F32)
                 for w in range(4):
                     nc.tensor.transpose(xt[:, w, :], kw[:, w * P:(w + 1) * P], ident_f[:])
-                nc.scalar.copy(out=grp_w[:, t], in_=xt[:].rearrange("p (g u) k -> p g k u", u=2))
+                nc.vector.tensor_copy(out=grp_w[:, t], in_=xt[:].rearrange("p (g u) k -> p g k u", u=2))
 
         def kv_quantise(c):
             kv_codes = ring.tile([P, 1024], U32, tag="kvc", bufs=1, name="kv_codes", align_bytes=64)

@@ -197,15 +197,15 @@ def tile_groupedqueryattention_pa_t_kernel(tc, xq, xk_rep, kv, mask, Wv, out):
         def scores(u, c):
             qt, b, h = units[u]
             s_ps = psum.tile([P, 512], F32, tag="s", bufs=4, name="s_ps")
-            nc.tensor.matmul(
-                s_ps[:], lhsT=st[("qT", qt)][:, b * H + h, :], rhs=kT[:, b, h, c * 512:(c + 1) * 512],
-                start=True, stop=False,
-            )
             for jj in range(4):
                 nc.tensor.matmul(
                     s_ps[:, jj * P:(jj + 1) * P], lhsT=yT[:, qt, 4 * c + jj, :], rhs=ident_f[:],
-                    is_transpose=True, start=False, stop=(jj == 3),
+                    is_transpose=True, start=(jj == 0), stop=False,
                 )
+            nc.tensor.matmul(
+                s_ps[:], lhsT=st[("qT", qt)][:, b * H + h, :], rhs=kT[:, b, h, c * 512:(c + 1) * 512],
+                start=False, stop=True,
+            )
             st[("s", u, c)] = s_ps
 
         def leave_psum(u, c):

@@ -23,7 +23,7 @@ DIST = HD // REP
 SCALE = 1.0 / math.sqrt(HD)
 ROOT = math.sqrt(HD)
 FLOPS = 2 * B * SKV * DIN * HD + 2 * 2 * B * H * SQ * SKV * HD
-REGROUP_ON_VECTOR = (3,)
+REGROUP_ON_VECTOR = ()
 
 LAG_LEAVE = 1
 LAG_EXP = 4

@@ -23,17 +23,20 @@ DIST = HD // REP
 SCALE = 1.0 / math.sqrt(HD)
 ROOT = math.sqrt(HD)
 FLOPS = 2 * B * SKV * DIN * HD + 2 * 2 * B * H * SQ * SKV * HD
-REGROUP_ON_VECTOR = ()
 
-LAG_LEAVE = 1
-LAG_EXP = 4
+MASK_BUFS = 8
+S_BANKS = 5
+ET_BANKS = 2
+LAG_EXP = 3
 LAG_TR = 6
 LAG_REGROUP = 7
 LAG_QUANT = 9
-LAG_PV = 16
-LAG_RECIP = 14
-LAG_NORM = 18
-KV_AT = (3, 7, 11, 15)
+LAG_PV = 14
+LAG_RECIP = 13
+LAG_NORM = 15
+SEEDS_FIRST = 12
+KT_AT = 4
+KV_AT = 2
 
 
 def tile_groupedqueryattention_pa_t_kernel(tc, xq, xk_rep, kv, mask, Wv, out):
@@ -46,8 +49,8 @@ def tile_groupedqueryattention_pa_t_kernel(tc, xq, xk_rep, kv, mask, Wv, out):
 
         mask_v = mask.rearrange("a c (t p) k -> p (a c t) k", p=P)
         xq_v = xq.rearrange("b (t p) c -> p b t c", p=P)
-        xk_v = xk_rep.rearrange("b (j p) c -> p b j c", p=P)
-        kv_v = kv.rearrange("b (g u p e) c -> p b g u e c", g=2, u=2, e=2)
+        xk_v = xk_rep.rearrange("b (w p e) c -> p b w e c", p=P, e=2)
+        kv_v = kv.rearrange("b (g u q i h) c -> h q b g u i c", g=2, u=2, i=2, h=2)
 
         ident_bf = keep.tile([P, P], BF16, name="ident_bf")
         make_identity(nc, ident_bf[:])
@@ -57,19 +60,30 @@ def tile_groupedqueryattention_pa_t_kernel(tc, xq, xk_rep, kv, mask, Wv, out):
         yT = keep.tile([P, NQT, NKT, P], F32, name="yT")
         kT = keep.tile([P, B, H, SKV], BF16, name="kT")
 
+        zeros = keep.tile([P, 512], BF16, name="zeros")
+        nc.vector.memset(zeros[:], 0.0)
+
         st = {}
 
+        def keep_clock(n):
+            for i in range(n):
+                nothing = s_bank(F32, [P, 512], "nothing")
+                nc.tensor.matmul(nothing[:], lhsT=zeros[:, 0:P], rhs=zeros[:], start=True, stop=True)
+
         def et_bank(dtype, shape, name):
-            return psum.tile(shape, dtype, tag="et", bufs=3, name=name)
+            return psum.tile(shape, dtype, tag="et", bufs=ET_BANKS, name=name)
+
+        def s_bank(dtype, shape, name):
+            return psum.tile(shape, dtype, tag="s", bufs=S_BANKS, name=name)
 
         def load_mask(qt):
-            m_sb = ring.tile([P, SKV], BF16, tag="mraw", bufs=4, name="m_sb")
+            m_sb = ring.tile([P, SKV], BF16, tag="mraw", bufs=MASK_BUFS, name="m_sb")
             nc.sync.dma_start(out=m_sb[:], in_=mask_v[:, qt, :])
             st[("mraw", qt)] = m_sb
 
         def load_xk(b):
-            xk_sb = ring.tile([P, NKT, H * HD], BF16, tag="xk", bufs=1, name="xk_sb")
-            nc.sync.dma_start(out=xk_sb[:], in_=xk_v[:, b])
+            xk_sb = ring.tile([P, NKT, H * HD], BF16, tag="xk", bufs=2, name="xk_sb")
+            nc.sync.dma_start(out=xk_sb[:].rearrange("p (w e) c -> p w e c", e=2), in_=xk_v[:, b])
             st[("xk", b)] = xk_sb
 
         def load_xq(qt):
@@ -79,19 +93,28 @@ def tile_groupedqueryattention_pa_t_kernel(tc, xq, xk_rep, kv, mask, Wv, out):
 
         def seed(qt):
             m_sb = st[("mraw", qt)]
-            ps = et_bank(BF16, [P, NKT, P], "mt_ps")
-            for j in range(NKT):
-                nc.tensor.transpose(ps[:, j, :], m_sb[:, j * P:(j + 1) * P], ident_bf[:])
-            nc.scalar.activation(out=yT[:, qt], in_=ps[:], func=ACT.Abs_reciprocal_sqrt, scale=1.0 / ROOT)
-            if qt + 4 < NQT:
-                load_mask(qt + 4)
+            if qt < SEEDS_FIRST:
+                ps = s_bank(F32, [P, NKT // 2, P], "mt_ps")
+            else:
+                ps = et_bank(F32, [P, NKT // 2, P], "mt_ps")
+            words = m_sb[:].bitcast(F32)
+            for w in range(NKT // 2):
+                nc.tensor.transpose(ps[:, w, :], words[:, w * P:(w + 1) * P], ident_f[:])
+            nc.scalar.activation(
+                out=yT[:, qt].rearrange("p (w e) q -> p w e q", e=2),
+                in_=ps[:].rearrange("p w q -> p (w q)").bitcast(BF16).rearrange("p (w q e) -> p w e q", e=2, q=P),
+                func=ACT.Abs_reciprocal_sqrt,
+                scale=1.0 / ROOT,
+            )
+            if qt + MASK_BUFS < NQT:
+                load_mask(qt + MASK_BUFS)
             eng = nc.vector if qt < 2 else nc.gpsimd
             for i in range(4):
                 y = yT[:, qt, 2 * i:2 * i + 2, :]
                 eng.tensor_tensor(out=y, in0=y, in1=y, op=ALU.mult)
 
         def kT_transposes(b, h):
-            ps = et_bank(BF16, [P, NKT, P], "kt_ps")
+            ps = s_bank(BF16, [P, NKT, P], "kt_ps")
             for j in range(NKT):
                 nc.tensor.transpose(ps[:, j, :], st[("xk", b)][:, j, h * HD:(h + 1) * HD], ident_bf[:])
             st[("ktps", b, h)] = ps
@@ -101,7 +124,7 @@ def tile_groupedqueryattention_pa_t_kernel(tc, xq, xk_rep, kv, mask, Wv, out):
             nc.vector.tensor_scalar(out=kT[:, b, h, :], in0=src, scalar1=-1.0, scalar2=None, op0=ALU.mult)
 
         def qT_transposes(qt):
-            ps = et_bank(BF16, [P, B * H, P], "qt_ps")
+            ps = s_bank(BF16, [P, B * H, P], "qt_ps")
             for b in range(B):
                 for h in range(H):
                     nc.tensor.transpose(ps[:, b * H + h, :], st[("xq", qt)][:, b, h * HD:(h + 1) * HD], ident_bf[:])
@@ -135,22 +158,26 @@ def tile_groupedqueryattention_pa_t_kernel(tc, xq, xk_rep, kv, mask, Wv, out):
             )
 
         def kv_load(c):
-            kv_sb = ring.tile([P, 4, DIN], BF16, tag="kv", bufs=1, name="kv_sb")
-            nc.sync.dma_start(
-                out=kv_sb[:].rearrange("p (u e) c -> p u e c", e=2), in_=kv_v[:, c // 2, c % 2]
-            )
+            kv_sb = ring.tile([P, 4, DIN], BF16, tag="kv", bufs=2, name="kv_sb")
+            for h in range(2):
+                for u in range(2):
+                    nc.sync.dma_start(
+                        out=kv_sb[h * P // 2:(h + 1) * P // 2, 2 * u:2 * u + 2, :], in_=kv_v[h, :, c // 2, c % 2, u]
+                    )
             st[("kv", c)] = kv_sb
 
-        def kv_transpose(c, half):
-            if half == 0:
+        def kv_transpose(c, t):
+            xt = s_bank(F32, [P, 4, P], "xt")
+            kw = st[("kv", c)][:, t, :].bitcast(F32)
+            for w in range(4):
+                nc.tensor.transpose(xt[:, w, :], kw[:, w * P:(w + 1) * P], ident_f[:])
+            st[("xt", c, t)] = xt
+
+        def kv_leave(c, t):
+            if t == 0:
                 st[("kvg", c)] = ring.tile([P, 4 * 1024], BF16, tag="kvg", bufs=1, name="kv_grp", align_bytes=64)
             grp_w = st[("kvg", c)][:].bitcast(F32).rearrange("p (t g k u) -> p t g k u", t=4, g=2, u=2)
-            for t in (2 * half, 2 * half + 1):
-                xt = psum.tile([P, 4, P], F32, tag="s", bufs=4, name="xt")
-                kw = st[("kv", c)][:, t, :].bitcast(F32)
-                for w in range(4):
-                    nc.tensor.transpose(xt[:, w, :], kw[:, w * P:(w + 1) * P], ident_f[:])
-                nc.vector.tensor_copy(out=grp_w[:, t], in_=xt[:].rearrange("p (g u) k -> p g k u", u=2))
+            nc.vector.tensor_copy(out=grp_w[:, t], in_=st[("xt", c, t)][:].rearrange("p (g u) k -> p g k u", u=2))
 
         def kv_quantise(c):
             kv_codes = ring.tile([P, 1024], U32, tag="kvc", bufs=1, name="kv_codes", align_bytes=64)
@@ -160,7 +187,7 @@ def tile_groupedqueryattention_pa_t_kernel(tc, xq, xk_rep, kv, mask, Wv, out):
 
         def xv_matmul(c):
             kv_codes, kv_scales = st[("kvc", c)]
-            xv_ps = et_bank(F32, [P, 4, HD], "xv_ps")
+            xv_ps = s_bank(F32, [P, 4, HD], "xv_ps")
             for t in range(4):
                 for gg in range(2):
                     cols = slice((t * 2 + gg) * P, (t * 2 + gg + 1) * P)
@@ -179,7 +206,7 @@ def tile_groupedqueryattention_pa_t_kernel(tc, xq, xk_rep, kv, mask, Wv, out):
         def xv_leave(c):
             if c % 2 == 0:
                 st[("vg", c // 2)] = ring.tile([P, 2, HD, 4], BF16, tag="vg", bufs=1, name="v_grp", align_bytes=64)
-            nc.scalar.copy(out=st[("vg", c // 2)][:, c % 2], in_=st[("xv", c)][:].rearrange("p t f -> p f t"))
+            nc.vector.tensor_copy(out=st[("vg", c // 2)][:, c % 2], in_=st[("xv", c)][:].rearrange("p t f -> p f t"))
 
         def v_quantise(b):
             vc = keep.tile([P, 2 * HD], U32, name="v_codes%d" % b, align_bytes=64)
@@ -194,25 +221,28 @@ def tile_groupedqueryattention_pa_t_kernel(tc, xq, xk_rep, kv, mask, Wv, out):
         NU = len(units)
         NG = len(groups)
 
-        def scores(u, c):
+        def penalties(u, c):
             qt, b, h = units[u]
-            s_ps = psum.tile([P, 512], F32, tag="s", bufs=4, name="s_ps")
+            s_ps = s_bank(F32, [P, 512], "s_ps")
             for jj in range(4):
                 nc.tensor.matmul(
                     s_ps[:, jj * P:(jj + 1) * P], lhsT=yT[:, qt, 4 * c + jj, :], rhs=ident_f[:],
                     is_transpose=True, start=(jj == 0), stop=False,
                 )
+            st[("s", u, c)] = s_ps
+
+        def scores(u, c):
+            qt, b, h = units[u]
             nc.tensor.matmul(
-                s_ps[:], lhsT=st[("qT", qt)][:, b * H + h, :], rhs=kT[:, b, h, c * 512:(c + 1) * 512],
+                st[("s", u, c)][:], lhsT=st[("qT", qt)][:, b * H + h, :], rhs=kT[:, b, h, c * 512:(c + 1) * 512],
                 start=False, stop=True,
             )
-            st[("s", u, c)] = s_ps
 
         def leave_psum(u, c):
             if c == 0:
-                st[("t", u)] = ring.tile([P, SKV], F32, tag="t", bufs=5, name="t")
+                st[("t", u)] = ring.tile([P, SKV], F32, tag="t", bufs=7, name="t")
                 st[("m0", u)] = ring.tile([P, 1], F32, tag="m0", bufs=3, name="m0")
-                st[("m", u)] = ring.tile([P, 1], F32, tag="m", bufs=5, name="m")
+                st[("m", u)] = ring.tile([P, 1], F32, tag="m", bufs=7, name="m")
             nc.vector.tensor_scalar(
                 out=st[("t", u)][:, c * 512:(c + 1) * 512],
                 in0=st[("s", u, c)][:],
@@ -228,7 +258,7 @@ def tile_groupedqueryattention_pa_t_kernel(tc, xq, xk_rep, kv, mask, Wv, out):
             g = u // H
             if h == 0:
                 st[("rs", g)] = ring.tile([P, H], F32, tag="rs", bufs=6, name="rowsum")
-            e = ring.tile([P, SKV], BF16, tag="e", bufs=4, name="e")
+            e = ring.tile([P, SKV], BF16, tag="e", bufs=5, name="e")
             nc.scalar.activation(
                 out=e[:], in_=st[("t", u)][:], func=ACT.Exp, bias=st[("m", u)][:, 0:1], scale=-1.0,
                 accum_out=st[("rs", g)][:, h:h + 1],
@@ -244,14 +274,10 @@ def tile_groupedqueryattention_pa_t_kernel(tc, xq, xk_rep, kv, mask, Wv, out):
             st[("et", u)] = et_ps
 
         def regroup(u):
-            h = u % H
             et_grp = ring.tile([P, 2 * P * 4], BF16, tag="etg", bufs=4, name="et_grp", align_bytes=64)
             src = st[("et", u)][:].rearrange("p (g u) q -> p g q u", u=2)
             dst = et_grp[:].bitcast(F32).rearrange("p (g q u) -> p g q u", g=2, u=2)
-            if h in REGROUP_ON_VECTOR:
-                nc.vector.tensor_copy(out=dst, in_=src)
-            else:
-                nc.scalar.copy(out=dst, in_=src)
+            nc.scalar.copy(out=dst, in_=src)
             st[("etg", u)] = et_grp
 
         def quantise(u):
@@ -315,88 +341,101 @@ def tile_groupedqueryattention_pa_t_kernel(tc, xq, xk_rep, kv, mask, Wv, out):
             nc.sync.dma_start(out=out[b, qt * P:(qt + 1) * P, :], in_=o_sb[:].rearrange("p j r -> p (j r)"))
 
         load_mask(0)
-        load_xk(0)
-        load_xq(0)
         load_mask(1)
+        load_mask(2)
+        load_mask(3)
+        load_xk(0)
+        load_mask(4)
+        load_mask(5)
+        load_xq(0)
         load_xq(1)
-        for qt in range(2, 4):
+        for qt in range(6, MASK_BUFS):
             load_mask(qt)
-        seed(0)
+        keep_clock(5)
+        for qt in range(4):
+            seed(qt)
+        kv_load(0)
         for h in range(H):
+            keep_clock(2)
             kT_transposes(0, h)
             kT_leave(0, h)
+            seed(4 + h)
+            if h == 1:
+                load_xk(1)
+        wv_load()
+        kv_load(1)
         for qt in range(2):
+            keep_clock(2)
             qT_transposes(qt)
             qT_leave(qt)
-        for qt in range(1, 12):
+            seed(4 + H + qt)
+        for qt in range(6 + H, SEEDS_FIRST):
+            keep_clock(1)
             seed(qt)
-        load_xk(1)
-        wv_load()
-        kv_load(0)
 
         first_use = {}
         for u in range(NU):
             if units[u][0] not in first_use:
                 first_use[units[u][0]] = u
 
+        extras = {}
+
+        def extra(tick, fill, leave, *args):
+            extras.setdefault(tick, []).append((lambda: fill(*args), lambda: leave(*args)))
+
+        for h in range(H):
+            extra(KT_AT + h, kT_transposes, kT_leave, 1, h)
+        for qt in range(2, NQT):
+            extra(first_use[qt] - 4, qT_transposes, qT_leave, qt)
+        for c in range(4):
+            for t in range(4):
+                extra(KV_AT + 4 * c + t, kv_transpose, kv_leave, c, t)
+            extra(KV_AT + 4 * c + 5, xv_matmul, xv_leave, c)
+
         for tk in range(NU + LAG_NORM + 1):
             for qt in range(2, NQT):
                 if tk == first_use[qt] - 10:
                     load_xq(qt)
-            for c in (1, 2, 3):
-                if tk == KV_AT[c - 1] + 2:
+            for c in (2, 3):
+                if tk == KV_AT + 4 * (c - 1):
                     kv_load(c)
-            if tk < NU:
-                scores(tk, 0)
             if 0 <= tk - LAG_TR < NU:
                 transposes(tk - LAG_TR)
             if tk < NU:
+                penalties(tk, 0)
+                penalties(tk, 1)
+                scores(tk, 0)
                 scores(tk, 1)
             if tk >= LAG_PV and (tk - LAG_PV) % H == 0 and (tk - LAG_PV) // H < NG:
                 weighted_sum((tk - LAG_PV) // H)
-            if tk == 0:
-                for qt in range(12, NQT):
-                    seed(qt)
-            if 2 <= tk < 2 + H:
-                kT_transposes(1, tk - 2)
-            for qt in range(2, NQT):
-                if tk == first_use[qt] - 6:
-                    qT_transposes(qt)
-            for c in range(4):
-                if tk == KV_AT[c] + 4:
-                    xv_matmul(c)
-            if 0 <= tk - LAG_LEAVE < NU:
-                leave_psum(tk - LAG_LEAVE, 0)
+            if SEEDS_FIRST + tk < NQT:
+                seed(SEEDS_FIRST + tk)
+                keep_clock(1)
+            for fill, leave in extras.get(tk, []):
+                fill()
+            if tk < NU:
+                leave_psum(tk, 0)
             if 0 <= tk - LAG_QUANT < NU:
                 quantise(tk - LAG_QUANT)
-            if 0 <= tk - LAG_LEAVE < NU:
-                leave_psum(tk - LAG_LEAVE, 1)
+            if tk < NU:
+                leave_psum(tk, 1)
+            for c in range(4):
+                if tk == KV_AT + 4 * c + 4:
+                    kv_quantise(c)
+            for fill, leave in extras.get(tk, []):
+                leave()
+            if tk == KV_AT + 1:
+                wv_regroup()
+            if tk == KV_AT + 2:
+                wv_quantise()
+            for c in range(4):
+                if tk == KV_AT + 4 * c + 6 and c % 2 == 1:
+                    v_quantise(c // 2)
+            if tk >= LAG_NORM and (tk - LAG_NORM) % H == 0 and (tk - LAG_NORM) // H < NG:
+                normalise((tk - LAG_NORM) // H)
             if tk >= LAG_RECIP and (tk - LAG_RECIP) % H == 0 and (tk - LAG_RECIP) // H < NG:
                 reciprocal((tk - LAG_RECIP) // H)
             if 0 <= tk - LAG_EXP < NU:
                 exponent(tk - LAG_EXP)
             if 0 <= tk - LAG_REGROUP < NU:
                 regroup(tk - LAG_REGROUP)
-            for qt in range(2, NQT):
-                if tk == first_use[qt] - 4:
-                    qT_leave(qt)
-            if tk >= LAG_NORM and (tk - LAG_NORM) % H == 0 and (tk - LAG_NORM) // H < NG:
-                normalise((tk - LAG_NORM) // H)
-            if 4 <= tk < 4 + H:
-                kT_leave(1, tk - 4)
-            if tk == 2:
-                wv_regroup()
-            if tk == 3:
-                wv_quantise()
-            for c in range(4):
-                if tk == KV_AT[c] + 2:
-                    kv_quantise(c)
-                if tk == KV_AT[c] + 6:
-                    xv_leave(c)
-                if tk == KV_AT[c] + 7 and c % 2 == 1:
-                    v_quantise(c // 2)
-            for c in range(4):
-                if tk == KV_AT[c]:
-                    kv_transpose(c, 0)
-                if tk == KV_AT[c] + 1:
-                    kv_transpose(c, 1)

@@ -26,17 +26,20 @@ FLOPS = 2 * B * SKV * DIN * HD + 2 * 2 * B * H * SQ * SKV * HD
 
 MASK_BUFS = 8
 S_BANKS = 5
-ET_BANKS = 2
-LAG_EXP = 3
-LAG_TR = 6
-LAG_REGROUP = 7
-LAG_QUANT = 9
-LAG_PV = 14
-LAG_RECIP = 13
-LAG_NORM = 15
-SEEDS_FIRST = 12
+ET_BANKS = 3
+EXP_LAG_FIRST = 5
+EXP_LAG_LAST = 3
+TR_AFTER_EXP = 3
+REGROUP_AFTER_TR = 1
+QUANT_AFTER_REGROUP = 2
+PV_AFTER_QUANT = 2
+T_BUFS = EXP_LAG_FIRST + 2
+SEEDS_FIRST = 5
+CLOCK_TICKS = 12
+SEEDS_A_TICK = 3
+SQUARE_LAG = 6
 KT_AT = 4
-KV_AT = 2
+KV_AT = (6, 10, 14, 18)
 
 
 def tile_groupedqueryattention_pa_t_kernel(tc, xq, xk_rep, kv, mask, Wv, out):
@@ -82,7 +85,7 @@ def tile_groupedqueryattention_pa_t_kernel(tc, xq, xk_rep, kv, mask, Wv, out):
             st[("mraw", qt)] = m_sb
 
         def load_xk(b):
-            xk_sb = ring.tile([P, NKT, H * HD], BF16, tag="xk", bufs=2, name="xk_sb")
+            xk_sb = ring.tile([P, NKT, H * HD], BF16, tag="xk", bufs=1, name="xk_sb")
             nc.sync.dma_start(out=xk_sb[:].rearrange("p (w e) c -> p w e c", e=2), in_=xk_v[:, b])
             st[("xk", b)] = xk_sb
 
@@ -108,7 +111,8 @@ def tile_groupedqueryattention_pa_t_kernel(tc, xq, xk_rep, kv, mask, Wv, out):
             )
             if qt + MASK_BUFS < NQT:
                 load_mask(qt + MASK_BUFS)
-            eng = nc.vector if qt < 2 else nc.gpsimd
+
+        def square(qt, eng):
             for i in range(4):
                 y = yT[:, qt, 2 * i:2 * i + 2, :]
                 eng.tensor_tensor(out=y, in0=y, in1=y, op=ALU.mult)
@@ -240,18 +244,25 @@ def tile_groupedqueryattention_pa_t_kernel(tc, xq, xk_rep, kv, mask, Wv, out):
 
         def leave_psum(u, c):
             if c == 0:
-                st[("t", u)] = ring.tile([P, SKV], F32, tag="t", bufs=7, name="t")
-                st[("m0", u)] = ring.tile([P, 1], F32, tag="m0", bufs=3, name="m0")
-                st[("m", u)] = ring.tile([P, 1], F32, tag="m", bufs=7, name="m")
+                st[("t", u)] = ring.tile([P, SKV], F32, tag="t", bufs=T_BUFS, name="t")
+                st[("mm", u)] = ring.tile([P, 2], F32, tag="mm", bufs=T_BUFS, name="mm")
             nc.vector.tensor_scalar(
                 out=st[("t", u)][:, c * 512:(c + 1) * 512],
                 in0=st[("s", u, c)][:],
                 scalar1=SCALE,
-                scalar2=None if c == 0 else st[("m0", u)][:],
+                scalar2=None,
                 op0=ALU.mult,
                 op1=ALU.min,
-                accum_out=st[("m0", u)][:] if c == 0 else st[("m", u)][:],
+                accum_out=st[("mm", u)][:, c:c + 1],
             )
+
+        def row_min(u):
+            m = ring.tile([P, 1], F32, tag="m", bufs=T_BUFS, name="m")
+            mm = st[("mm", u)]
+            nc.gpsimd.tensor_scalar(
+                out=m[:], in0=mm[:, 0:1], scalar1=mm[:, 1:2], scalar2=0.0, op0=ALU.min, op1=ALU.add
+            )
+            st[("m", u)] = m
 
         def exponent(u):
             h = u % H
@@ -273,30 +284,30 @@ def tile_groupedqueryattention_pa_t_kernel(tc, xq, xk_rep, kv, mask, Wv, out):
                 nc.tensor.transpose(et_ps[:, w, :], ew[:, w * P:(w + 1) * P], ident_f[:])
             st[("et", u)] = et_ps
 
-        def regroup(u):
-            et_grp = ring.tile([P, 2 * P * 4], BF16, tag="etg", bufs=4, name="et_grp", align_bytes=64)
+        def regroup(u, copy):
+            if u % 2 == 0:
+                st[("etg", u // 2)] = ring.tile([P, 2, 2 * P * 4], BF16, tag="etg", bufs=4, name="et_grp", align_bytes=64)
             src = st[("et", u)][:].rearrange("p (g u) q -> p g q u", u=2)
-            dst = et_grp[:].bitcast(F32).rearrange("p (g q u) -> p g q u", g=2, u=2)
-            nc.scalar.copy(out=dst, in_=src)
-            st[("etg", u)] = et_grp
+            dst = st[("etg", u // 2)][:, u % 2, :].bitcast(F32).rearrange("p (g q u) -> p g q u", g=2, u=2)
+            copy(out=dst, in_=src)
 
-        def quantise(u):
-            h = u % H
-            g = u // H
+        def quantise(pair):
+            h = 2 * pair % H
+            g = 2 * pair // H
             if h == 0:
                 st[("ec", g)] = ring.tile([P, H * 2 * P], U32, tag="ec", bufs=3, name="e_codes", align_bytes=64)
                 st[("es", g)] = ring.tile([P, H * 2 * P], U8, tag="es", bufs=3, name="e_scales", align_bytes=64)
-            cols = slice(h * 2 * P, (h + 1) * 2 * P)
+            cols = slice(h * 2 * P, (h + 2) * 2 * P)
             nc.vector.quantize_mx(
                 out=st[("ec", g)][:, cols].bitcast(FP8X4),
                 scales=st[("es", g)][:, cols],
-                in_=st[("etg", u)][:],
+                in_=st[("etg", pair)][:].rearrange("p k x -> p (k x)"),
             )
 
         def weighted_sum(g):
             qt, b = groups[g]
             vc, vs = st[("v", b)]
-            o_ps = psum.tile([P, H, HD], F32, tag="o", bufs=1, name="o_ps")
+            o_ps = et_bank(F32, [P, H, HD], "o_ps")
             for h in range(H):
                 for gg in range(2):
                     cols = slice((h * 2 + gg) * P, (h * 2 + gg + 1) * P)
@@ -317,61 +328,53 @@ def tile_groupedqueryattention_pa_t_kernel(tc, xq, xk_rep, kv, mask, Wv, out):
             nc.vector.reciprocal(rinv[:], st[("rs", g)][:])
             st[("ri", g)] = rinv
 
+        def o_leave(g):
+            own = st[("o", g)][:].rearrange("p h f -> p (h f)")[:, HD - DIST:HD - DIST + H * (HD - DIST)]
+            o_n = ring.tile([P, H, DIST], F32, tag="on", bufs=2, name="o_n")
+            nc.scalar.copy(out=o_n[:], in_=own.rearrange("p (h x) -> p h x", h=H)[:, :, 0:DIST])
+            st[("on", g)] = o_n
+
         def normalise(g):
             qt, b = groups[g]
-            o_ps = st[("o", g)]
-            rinv = st[("ri", g)]
-            own = o_ps[:].rearrange("p h f -> p (h f)")[:, HD - DIST:HD - DIST + H * (HD - DIST)]
-            o_n = ring.tile([P, H, DIST], F32, tag="on", bufs=2, name="o_n")
-            nc.vector.tensor_tensor(
-                out=o_n[:],
-                in0=own.rearrange("p (h x) -> p h x", h=H)[:, :, 0:DIST],
-                in1=rinv[:].unsqueeze(2).to_broadcast([P, H, DIST]),
-                op=ALU.mult,
-            )
-            o_sb = ring.tile([P, H * DIST, REP], F32, tag="osb", bufs=2, name="o_sb")
-            nc.gpsimd.tensor_scalar(
-                out=o_sb[:],
-                in0=o_n[:].rearrange("p h j -> p (h j)").unsqueeze(2).to_broadcast([P, H * DIST, REP]),
-                scalar1=1.0,
-                scalar2=0.0,
-                op0=ALU.mult,
-                op1=ALU.add,
-            )
-            nc.sync.dma_start(out=out[b, qt * P:(qt + 1) * P, :], in_=o_sb[:].rearrange("p j r -> p (j r)"))
+            o_sb = ring.tile([P, H, DIST, REP], F32, tag="osb", bufs=2, name="o_sb")
+            for h in range(H):
+                nc.gpsimd.tensor_scalar(
+                    out=o_sb[:, h],
+                    in0=st[("on", g)][:, h].unsqueeze(2).to_broadcast([P, DIST, REP]),
+                    scalar1=st[("ri", g)][:, h:h + 1],
+                    scalar2=0.0,
+                    op0=ALU.mult,
+                    op1=ALU.add,
+                )
+            nc.sync.dma_start(out=out[b, qt * P:(qt + 1) * P, :], in_=o_sb[:].rearrange("p h j r -> p (h j r)"))
 
-        load_mask(0)
-        load_mask(1)
-        load_mask(2)
-        load_mask(3)
-        load_xk(0)
-        load_mask(4)
-        load_mask(5)
-        load_xq(0)
-        load_xq(1)
-        for qt in range(6, MASK_BUFS):
+        for qt in range(3):
             load_mask(qt)
-        keep_clock(5)
-        for qt in range(4):
+        load_xk(0)
+        load_xq(0)
+        load_mask(3)
+        load_mask(4)
+        load_xq(1)
+        for qt in range(5, MASK_BUFS):
+            load_mask(qt)
+        for qt in range(2):
+            seed(qt)
+            square(qt, nc.vector)
+        seed(2)
+        keep_clock(6)
+        kT_transposes(0, 0)
+        kT_leave(0, 0)
+        qT_transposes(0)
+        qT_leave(0)
+        keep_clock(2)
+        seed(3)
+        kT_transposes(0, 1)
+        kT_leave(0, 1)
+        for qt in range(4, SEEDS_FIRST):
             seed(qt)
         kv_load(0)
-        for h in range(H):
-            keep_clock(2)
-            kT_transposes(0, h)
-            kT_leave(0, h)
-            seed(4 + h)
-            if h == 1:
-                load_xk(1)
         wv_load()
         kv_load(1)
-        for qt in range(2):
-            keep_clock(2)
-            qT_transposes(qt)
-            qT_leave(qt)
-            seed(4 + H + qt)
-        for qt in range(6 + H, SEEDS_FIRST):
-            keep_clock(1)
-            seed(qt)
 
         first_use = {}
         for u in range(NU):
@@ -383,59 +386,103 @@ def tile_groupedqueryattention_pa_t_kernel(tc, xq, xk_rep, kv, mask, Wv, out):
         def extra(tick, fill, leave, *args):
             extras.setdefault(tick, []).append((lambda: fill(*args), lambda: leave(*args)))
 
+        for h in (2, 3):
+            extra(h - 2, kT_transposes, kT_leave, 0, h)
+        extra(1, qT_transposes, qT_leave, 1)
         for h in range(H):
             extra(KT_AT + h, kT_transposes, kT_leave, 1, h)
         for qt in range(2, NQT):
             extra(first_use[qt] - 4, qT_transposes, qT_leave, qt)
         for c in range(4):
             for t in range(4):
-                extra(KV_AT + 4 * c + t, kv_transpose, kv_leave, c, t)
-            extra(KV_AT + 4 * c + 5, xv_matmul, xv_leave, c)
+                extra(KV_AT[c] + t, kv_transpose, kv_leave, c, t)
+            extra(KV_AT[c] + 5, xv_matmul, xv_leave, c)
 
-        for tk in range(NU + LAG_NORM + 1):
+        def exp_at(u):
+            return u + EXP_LAG_LAST + (EXP_LAG_FIRST - EXP_LAG_LAST) * (NU - 1 - u) // NU
+
+        def tr_at(u):
+            return exp_at(u) + TR_AFTER_EXP
+
+        def regroup_at(u):
+            return tr_at(u) + REGROUP_AFTER_TR
+
+        def quant_at(pair):
+            return regroup_at(2 * pair + 1) + QUANT_AFTER_REGROUP
+
+        def pv_at(g):
+            values_at = KV_AT[2 * groups[g][1] + 1] + 6
+            return max(quant_at(H // 2 * g + H // 2 - 1) + PV_AFTER_QUANT, values_at + 1)
+
+        def by_tick(at, n):
+            table = {}
+            for i in range(n):
+                table.setdefault(at(i), []).append(i)
+            return table
+
+        exp_in = by_tick(exp_at, NU)
+        tr_in = by_tick(tr_at, NU)
+        regroup_in = by_tick(regroup_at, NU)
+        quant_in = by_tick(quant_at, NU // 2)
+        pv_in = by_tick(pv_at, NG)
+
+        for tk in range(pv_at(NG - 1) + 2):
             for qt in range(2, NQT):
                 if tk == first_use[qt] - 10:
                     load_xq(qt)
+            if tk == 2:
+                load_xk(1)
             for c in (2, 3):
-                if tk == KV_AT + 4 * (c - 1):
+                if tk == KV_AT[c - 2] + 4:
                     kv_load(c)
-            if 0 <= tk - LAG_TR < NU:
-                transposes(tk - LAG_TR)
+            for u in exp_in.get(tk, []):
+                exponent(u)
+            if tk < NU:
+                for u in regroup_in.get(tk, []):
+                    regroup(u, nc.scalar.copy)
+            for g in pv_in.get(tk - 1, []):
+                o_leave(g)
+            for u in tr_in.get(tk, []):
+                transposes(u)
+            for qt in range(SEEDS_FIRST + SEEDS_A_TICK * tk, min(NQT, SEEDS_FIRST + SEEDS_A_TICK * (tk + 1))):
+                seed(qt)
             if tk < NU:
                 penalties(tk, 0)
                 penalties(tk, 1)
                 scores(tk, 0)
                 scores(tk, 1)
-            if tk >= LAG_PV and (tk - LAG_PV) % H == 0 and (tk - LAG_PV) // H < NG:
-                weighted_sum((tk - LAG_PV) // H)
-            if SEEDS_FIRST + tk < NQT:
-                seed(SEEDS_FIRST + tk)
-                keep_clock(1)
+            for g in pv_in.get(tk, []):
+                weighted_sum(g)
+            if tk < CLOCK_TICKS:
+                keep_clock(2 if tk < 4 else 1)
             for fill, leave in extras.get(tk, []):
                 fill()
+            for qt in range(2, NQT):
+                if tk == first_use[qt] - SQUARE_LAG:
+                    square(qt, nc.gpsimd)
+            if tk >= NU:
+                for u in regroup_in.get(tk, []):
+                    regroup(u, nc.vector.tensor_copy)
             if tk < NU:
                 leave_psum(tk, 0)
-            if 0 <= tk - LAG_QUANT < NU:
-                quantise(tk - LAG_QUANT)
+            for u in quant_in.get(tk, []):
+                quantise(u)
             if tk < NU:
                 leave_psum(tk, 1)
+                row_min(tk)
             for c in range(4):
-                if tk == KV_AT + 4 * c + 4:
+                if tk == KV_AT[c] + 4:
                     kv_quantise(c)
             for fill, leave in extras.get(tk, []):
                 leave()
-            if tk == KV_AT + 1:
+            if tk == KV_AT[0] + 1:
                 wv_regroup()
-            if tk == KV_AT + 2:
+            if tk == KV_AT[0] + 2:
                 wv_quantise()
-            for c in range(4):
-                if tk == KV_AT + 4 * c + 6 and c % 2 == 1:
-                    v_quantise(c // 2)
-            if tk >= LAG_NORM and (tk - LAG_NORM) % H == 0 and (tk - LAG_NORM) // H < NG:
-                normalise((tk - LAG_NORM) // H)
-            if tk >= LAG_RECIP and (tk - LAG_RECIP) % H == 0 and (tk - LAG_RECIP) // H < NG:
-                reciprocal((tk - LAG_RECIP) // H)
-            if 0 <= tk - LAG_EXP < NU:
-                exponent(tk - LAG_EXP)
-            if 0 <= tk - LAG_REGROUP < NU:
-                regroup(tk - LAG_REGROUP)
+            for b in range(B):
+                if tk == KV_AT[2 * b + 1] + 6:
+                    v_quantise(b)
+            for g in pv_in.get(tk, []):
+                reciprocal(g)
+            for g in pv_in.get(tk - 1, []):
+                normalise(g)

@@ -34,8 +34,12 @@ REGROUP_AFTER_TR = 1
 QUANT_AFTER_REGROUP = 2
 PV_AFTER_QUANT = 2
 T_BUFS = EXP_LAG_FIRST + 2
-SEEDS_FIRST = 5
-CLOCK_TICKS = 12
+SEEDS_FIRST = 3
+XK_AT = 3
+CLOCK_START = 4
+CLOCK_LOADS = 3
+CLOCK_KEYS = 2
+CLOCK_TICKS = 10
 SEEDS_A_TICK = 3
 SQUARE_LAG = 6
 KT_AT = 4
@@ -86,8 +90,11 @@ def tile_groupedqueryattention_pa_t_kernel(tc, xq, xk_rep, kv, mask, Wv, out):
 
         def load_xk(b):
             xk_sb = ring.tile([P, NKT, H * HD], BF16, tag="xk", bufs=1, name="xk_sb")
-            nc.sync.dma_start(out=xk_sb[:].rearrange("p (w e) c -> p w e c", e=2), in_=xk_v[:, b])
             st[("xk", b)] = xk_sb
+
+        def load_xk_half(b, i):
+            half = st[("xk", b)][:, 4 * i:4 * i + 4, :]
+            nc.sync.dma_start(out=half.rearrange("p (w e) c -> p w e c", e=2), in_=xk_v[:, b, 2 * i:2 * i + 2])
 
         def load_xq(qt):
             xq_sb = ring.tile([P, B, H * HD], BF16, tag="xq", bufs=2, name="xq_sb")
@@ -96,7 +103,7 @@ def tile_groupedqueryattention_pa_t_kernel(tc, xq, xk_rep, kv, mask, Wv, out):
 
         def seed(qt):
             m_sb = st[("mraw", qt)]
-            if qt < SEEDS_FIRST:
+            if qt < 2:
                 ps = s_bank(F32, [P, NKT // 2, P], "mt_ps")
             else:
                 ps = et_bank(F32, [P, NKT // 2, P], "mt_ps")
@@ -113,8 +120,8 @@ def tile_groupedqueryattention_pa_t_kernel(tc, xq, xk_rep, kv, mask, Wv, out):
                 load_mask(qt + MASK_BUFS)
 
         def square(qt, eng):
-            for i in range(4):
-                y = yT[:, qt, 2 * i:2 * i + 2, :]
+            for i in range(2):
+                y = yT[:, qt, 4 * i:4 * i + 4, :]
                 eng.tensor_tensor(out=y, in0=y, in1=y, op=ALU.mult)
 
         def kT_transposes(b, h):
@@ -228,6 +235,9 @@ def tile_groupedqueryattention_pa_t_kernel(tc, xq, xk_rep, kv, mask, Wv, out):
         def penalties(u, c):
             qt, b, h = units[u]
             s_ps = s_bank(F32, [P, 512], "s_ps")
+            if c == 0:
+                for i in range(2 if u < 4 else 1 if u < CLOCK_TICKS else 0):
+                    nc.tensor.matmul(s_ps[:], lhsT=zeros[:, 0:P], rhs=zeros[:], start=True, stop=True)
             for jj in range(4):
                 nc.tensor.matmul(
                     s_ps[:, jj * P:(jj + 1) * P], lhsT=yT[:, qt, 4 * c + jj, :], rhs=ident_f[:],
@@ -328,49 +338,52 @@ def tile_groupedqueryattention_pa_t_kernel(tc, xq, xk_rep, kv, mask, Wv, out):
             nc.vector.reciprocal(rinv[:], st[("rs", g)][:])
             st[("ri", g)] = rinv
 
-        def o_leave(g):
+        def normalise(g):
             own = st[("o", g)][:].rearrange("p h f -> p (h f)")[:, HD - DIST:HD - DIST + H * (HD - DIST)]
             o_n = ring.tile([P, H, DIST], F32, tag="on", bufs=2, name="o_n")
-            nc.scalar.copy(out=o_n[:], in_=own.rearrange("p (h x) -> p h x", h=H)[:, :, 0:DIST])
+            nc.vector.tensor_tensor(
+                out=o_n[:],
+                in0=own.rearrange("p (h x) -> p h x", h=H)[:, :, 0:DIST],
+                in1=st[("ri", g)][:].unsqueeze(2).to_broadcast([P, H, DIST]),
+                op=ALU.mult,
+            )
             st[("on", g)] = o_n
 
-        def normalise(g):
+        def repeat(g):
             qt, b = groups[g]
-            o_sb = ring.tile([P, H, DIST, REP], F32, tag="osb", bufs=2, name="o_sb")
-            for h in range(H):
-                nc.gpsimd.tensor_scalar(
-                    out=o_sb[:, h],
-                    in0=st[("on", g)][:, h].unsqueeze(2).to_broadcast([P, DIST, REP]),
-                    scalar1=st[("ri", g)][:, h:h + 1],
-                    scalar2=0.0,
-                    op0=ALU.mult,
-                    op1=ALU.add,
-                )
-            nc.sync.dma_start(out=out[b, qt * P:(qt + 1) * P, :], in_=o_sb[:].rearrange("p h j r -> p (h j r)"))
+            o_sb = ring.tile([P, H * DIST, REP], F32, tag="osb", bufs=2, name="o_sb")
+            nc.gpsimd.tensor_scalar(
+                out=o_sb[:],
+                in0=st[("on", g)][:].rearrange("p h j -> p (h j)").unsqueeze(2).to_broadcast([P, H * DIST, REP]),
+                scalar1=1.0,
+                scalar2=0.0,
+                op0=ALU.mult,
+                op1=ALU.add,
+            )
+            nc.sync.dma_start(out=out[b, qt * P:(qt + 1) * P, :], in_=o_sb[:].rearrange("p j r -> p (j r)"))
 
-        for qt in range(3):
-            load_mask(qt)
+        load_mask(0)
+        load_mask(1)
         load_xk(0)
+        load_xk_half(0, 0)
         load_xq(0)
-        load_mask(3)
-        load_mask(4)
+        load_xk_half(0, 1)
+        load_mask(2)
         load_xq(1)
-        for qt in range(5, MASK_BUFS):
+        for qt in range(3, MASK_BUFS):
             load_mask(qt)
+        keep_clock(CLOCK_START)
         for qt in range(2):
             seed(qt)
-            square(qt, nc.vector)
-        seed(2)
-        keep_clock(6)
+        square(0, nc.vector)
+        keep_clock(CLOCK_LOADS)
         kT_transposes(0, 0)
-        kT_leave(0, 0)
+        keep_clock(CLOCK_KEYS)
         qT_transposes(0)
+        kT_leave(0, 0)
         qT_leave(0)
-        keep_clock(2)
-        seed(3)
-        kT_transposes(0, 1)
-        kT_leave(0, 1)
-        for qt in range(4, SEEDS_FIRST):
+        square(1, nc.vector)
+        for qt in range(2, SEEDS_FIRST):
             seed(qt)
         kv_load(0)
         wv_load()
@@ -386,9 +399,9 @@ def tile_groupedqueryattention_pa_t_kernel(tc, xq, xk_rep, kv, mask, Wv, out):
         def extra(tick, fill, leave, *args):
             extras.setdefault(tick, []).append((lambda: fill(*args), lambda: leave(*args)))
 
-        for h in (2, 3):
-            extra(h - 2, kT_transposes, kT_leave, 0, h)
-        extra(1, qT_transposes, qT_leave, 1)
+        for h in (1, 2, 3):
+            extra(h - 1, kT_transposes, kT_leave, 0, h)
+        extra(2, qT_transposes, qT_leave, 1)
         for h in range(H):
             extra(KT_AT + h, kT_transposes, kT_leave, 1, h)
         for qt in range(2, NQT):
@@ -430,8 +443,10 @@ def tile_groupedqueryattention_pa_t_kernel(tc, xq, xk_rep, kv, mask, Wv, out):
             for qt in range(2, NQT):
                 if tk == first_use[qt] - 10:
                     load_xq(qt)
-            if tk == 2:
+            if tk == XK_AT:
                 load_xk(1)
+                for i in range(2):
+                    load_xk_half(1, i)
             for c in (2, 3):
                 if tk == KV_AT[c - 2] + 4:
                     kv_load(c)
@@ -440,23 +455,19 @@ def tile_groupedqueryattention_pa_t_kernel(tc, xq, xk_rep, kv, mask, Wv, out):
             if tk < NU:
                 for u in regroup_in.get(tk, []):
                     regroup(u, nc.scalar.copy)
-            for g in pv_in.get(tk - 1, []):
-                o_leave(g)
             for u in tr_in.get(tk, []):
                 transposes(u)
-            for qt in range(SEEDS_FIRST + SEEDS_A_TICK * tk, min(NQT, SEEDS_FIRST + SEEDS_A_TICK * (tk + 1))):
-                seed(qt)
             if tk < NU:
                 penalties(tk, 0)
                 penalties(tk, 1)
-                scores(tk, 0)
                 scores(tk, 1)
+                scores(tk, 0)
             for g in pv_in.get(tk, []):
                 weighted_sum(g)
-            if tk < CLOCK_TICKS:
-                keep_clock(2 if tk < 4 else 1)
             for fill, leave in extras.get(tk, []):
                 fill()
+            for qt in range(SEEDS_FIRST + SEEDS_A_TICK * tk, min(NQT, SEEDS_FIRST + SEEDS_A_TICK * (tk + 1))):
+                seed(qt)
             for qt in range(2, NQT):
                 if tk == first_use[qt] - SQUARE_LAG:
                     square(qt, nc.gpsimd)
@@ -483,6 +494,7 @@ def tile_groupedqueryattention_pa_t_kernel(tc, xq, xk_rep, kv, mask, Wv, out):
                 if tk == KV_AT[2 * b + 1] + 6:
                     v_quantise(b)
             for g in pv_in.get(tk, []):
-                reciprocal(g)
-            for g in pv_in.get(tk - 1, []):
                 normalise(g)
+                repeat(g)
+            for g in pv_in.get(tk + 1, []):
+                reciprocal(g)

@@ -27,13 +27,13 @@ FLOPS = 2 * B * SKV * DIN * HD + 2 * 2 * B * H * SQ * SKV * HD
 MASK_BUFS = 8
 S_BANKS = 5
 ET_BANKS = 3
-EXP_LAG_FIRST = 5
-EXP_LAG_LAST = 3
-TR_AFTER_EXP = 3
+EXP_LAG_FIRST = 6
+EXP_LAG_LAST = 5
+TR_AFTER_EXP = 2
 REGROUP_AFTER_TR = 1
 QUANT_AFTER_REGROUP = 2
 PV_AFTER_QUANT = 2
-T_BUFS = EXP_LAG_FIRST + 2
+T_BUFS = EXP_LAG_FIRST + 3
 SEEDS_FIRST = 3
 XK_AT = 3
 CLOCK_START = 4
@@ -42,6 +42,8 @@ CLOCK_KEYS = 2
 CLOCK_TICKS = 10
 SEEDS_A_TICK = 3
 SQUARE_LAG = 6
+SQUARES = 4
+REPEATS = 2
 KT_AT = 4
 KV_AT = (6, 10, 14, 18)
 
@@ -120,8 +122,8 @@ def tile_groupedqueryattention_pa_t_kernel(tc, xq, xk_rep, kv, mask, Wv, out):
                 load_mask(qt + MASK_BUFS)
 
         def square(qt, eng):
-            for i in range(2):
-                y = yT[:, qt, 4 * i:4 * i + 4, :]
+            for i in range(SQUARES):
+                y = yT[:, qt, NKT // SQUARES * i:NKT // SQUARES * (i + 1), :]
                 eng.tensor_tensor(out=y, in0=y, in1=y, op=ALU.mult)
 
         def kT_transposes(b, h):
@@ -277,9 +279,9 @@ def tile_groupedqueryattention_pa_t_kernel(tc, xq, xk_rep, kv, mask, Wv, out):
         def exponent(u):
             h = u % H
             g = u // H
-            if h == 0:
+            if h == 1:
                 st[("rs", g)] = ring.tile([P, H], F32, tag="rs", bufs=6, name="rowsum")
-            e = ring.tile([P, SKV], BF16, tag="e", bufs=5, name="e")
+            e = ring.tile([P, SKV], BF16, tag="e", bufs=6, name="e")
             nc.scalar.activation(
                 out=e[:], in_=st[("t", u)][:], func=ACT.Exp, bias=st[("m", u)][:, 0:1], scale=-1.0,
                 accum_out=st[("rs", g)][:, h:h + 1],
@@ -295,7 +297,7 @@ def tile_groupedqueryattention_pa_t_kernel(tc, xq, xk_rep, kv, mask, Wv, out):
             st[("et", u)] = et_ps
 
         def regroup(u, copy):
-            if u % 2 == 0:
+            if u % 2 == 1:
                 st[("etg", u // 2)] = ring.tile([P, 2, 2 * P * 4], BF16, tag="etg", bufs=4, name="et_grp", align_bytes=64)
             src = st[("et", u)][:].rearrange("p (g u) q -> p g q u", u=2)
             dst = st[("etg", u // 2)][:, u % 2, :].bitcast(F32).rearrange("p (g q u) -> p g q u", g=2, u=2)
@@ -341,25 +343,25 @@ def tile_groupedqueryattention_pa_t_kernel(tc, xq, xk_rep, kv, mask, Wv, out):
         def normalise(g):
             own = st[("o", g)][:].rearrange("p h f -> p (h f)")[:, HD - DIST:HD - DIST + H * (HD - DIST)]
             o_n = ring.tile([P, H, DIST], F32, tag="on", bufs=2, name="o_n")
-            nc.vector.tensor_tensor(
-                out=o_n[:],
-                in0=own.rearrange("p (h x) -> p h x", h=H)[:, :, 0:DIST],
-                in1=st[("ri", g)][:].unsqueeze(2).to_broadcast([P, H, DIST]),
-                op=ALU.mult,
-            )
+            for h in reversed(range(H)):
+                nc.scalar.activation(
+                    out=o_n[:, h], in_=own[:, h * (HD - DIST):h * (HD - DIST) + DIST], func=ACT.Copy, scale=st[("ri", g)][:, h:h + 1]
+                )
             st[("on", g)] = o_n
 
         def repeat(g):
             qt, b = groups[g]
             o_sb = ring.tile([P, H * DIST, REP], F32, tag="osb", bufs=2, name="o_sb")
-            nc.gpsimd.tensor_scalar(
-                out=o_sb[:],
-                in0=st[("on", g)][:].rearrange("p h j -> p (h j)").unsqueeze(2).to_broadcast([P, H * DIST, REP]),
-                scalar1=1.0,
-                scalar2=0.0,
-                op0=ALU.mult,
-                op1=ALU.add,
-            )
+            n = H * DIST // REPEATS
+            for i in range(REPEATS):
+                nc.gpsimd.tensor_scalar(
+                    out=o_sb[:, i * n:(i + 1) * n],
+                    in0=st[("on", g)][:].rearrange("p h j -> p (h j)")[:, i * n:(i + 1) * n].unsqueeze(2).to_broadcast([P, n, REP]),
+                    scalar1=1.0,
+                    scalar2=0.0,
+                    op0=ALU.mult,
+                    op1=ALU.add,
+                )
             nc.sync.dma_start(out=out[b, qt * P:(qt + 1) * P, :], in_=o_sb[:].rearrange("p j r -> p (j r)"))
 
         load_mask(0)
@@ -411,17 +413,18 @@ def tile_groupedqueryattention_pa_t_kernel(tc, xq, xk_rep, kv, mask, Wv, out):
                 extra(KV_AT[c] + t, kv_transpose, kv_leave, c, t)
             extra(KV_AT[c] + 5, xv_matmul, xv_leave, c)
 
-        def exp_at(u):
+        def exp_at(pair):
+            u = 2 * pair + 1
             return u + EXP_LAG_LAST + (EXP_LAG_FIRST - EXP_LAG_LAST) * (NU - 1 - u) // NU
 
-        def tr_at(u):
-            return exp_at(u) + TR_AFTER_EXP
+        def tr_at(pair):
+            return exp_at(pair) + TR_AFTER_EXP
 
-        def regroup_at(u):
-            return tr_at(u) + REGROUP_AFTER_TR
+        def regroup_at(pair):
+            return tr_at(pair) + REGROUP_AFTER_TR
 
         def quant_at(pair):
-            return regroup_at(2 * pair + 1) + QUANT_AFTER_REGROUP
+            return regroup_at(pair) + QUANT_AFTER_REGROUP
 
         def pv_at(g):
             values_at = KV_AT[2 * groups[g][1] + 1] + 6
@@ -433,9 +436,9 @@ def tile_groupedqueryattention_pa_t_kernel(tc, xq, xk_rep, kv, mask, Wv, out):
                 table.setdefault(at(i), []).append(i)
             return table
 
-        exp_in = by_tick(exp_at, NU)
-        tr_in = by_tick(tr_at, NU)
-        regroup_in = by_tick(regroup_at, NU)
+        exp_in = by_tick(exp_at, NU // 2)
+        tr_in = by_tick(tr_at, NU // 2)
+        regroup_in = by_tick(regroup_at, NU // 2)
         quant_in = by_tick(quant_at, NU // 2)
         pv_in = by_tick(pv_at, NG)
 
@@ -450,13 +453,18 @@ def tile_groupedqueryattention_pa_t_kernel(tc, xq, xk_rep, kv, mask, Wv, out):
             for c in (2, 3):
                 if tk == KV_AT[c - 2] + 4:
                     kv_load(c)
-            for u in exp_in.get(tk, []):
-                exponent(u)
+            for pair in exp_in.get(tk, []):
+                exponent(2 * pair + 1)
+                exponent(2 * pair)
             if tk < NU:
-                for u in regroup_in.get(tk, []):
-                    regroup(u, nc.scalar.copy)
-            for u in tr_in.get(tk, []):
-                transposes(u)
+                for pair in regroup_in.get(tk, []):
+                    regroup(2 * pair + 1, nc.scalar.copy)
+                    regroup(2 * pair, nc.scalar.copy)
+            for g in pv_in.get(tk - 1, []):
+                normalise(g)
+            for pair in tr_in.get(tk, []):
+                transposes(2 * pair)
+                transposes(2 * pair + 1)
             if tk < NU:
                 penalties(tk, 0)
                 penalties(tk, 1)
@@ -472,8 +480,9 @@ def tile_groupedqueryattention_pa_t_kernel(tc, xq, xk_rep, kv, mask, Wv, out):
                 if tk == first_use[qt] - SQUARE_LAG:
                     square(qt, nc.gpsimd)
             if tk >= NU:
-                for u in regroup_in.get(tk, []):
-                    regroup(u, nc.vector.tensor_copy)
+                for pair in regroup_in.get(tk, []):
+                    regroup(2 * pair + 1, nc.vector.tensor_copy)
+                    regroup(2 * pair, nc.vector.tensor_copy)
             if tk < NU:
                 leave_psum(tk, 0)
             for u in quant_in.get(tk, []):
@@ -493,8 +502,7 @@ def tile_groupedqueryattention_pa_t_kernel(tc, xq, xk_rep, kv, mask, Wv, out):
             for b in range(B):
                 if tk == KV_AT[2 * b + 1] + 6:
                     v_quantise(b)
-            for g in pv_in.get(tk, []):
-                normalise(g)
-                repeat(g)
             for g in pv_in.get(tk + 1, []):
                 reciprocal(g)
+            for g in pv_in.get(tk - 1, []):
+                repeat(g)

@@ -27,14 +27,15 @@ FLOPS = 2 * B * SKV * DIN * HD + 2 * 2 * B * H * SQ * SKV * HD
 MASK_BUFS = 8
 S_BANKS = 5
 ET_BANKS = 3
-EXP_LAG_FIRST = 6
+EXP_LAG_FIRST = 5
 EXP_LAG_LAST = 5
 TR_AFTER_EXP = 2
 REGROUP_AFTER_TR = 1
 QUANT_AFTER_REGROUP = 2
 PV_AFTER_QUANT = 2
+NORM_AFTER_PV = 2
 T_BUFS = EXP_LAG_FIRST + 3
-SEEDS_FIRST = 3
+SEEDS_FIRST = 4
 XK_AT = 3
 CLOCK_START = 4
 CLOCK_LOADS = 3
@@ -45,7 +46,7 @@ SQUARE_LAG = 6
 SQUARES = 4
 REPEATS = 2
 KT_AT = 4
-KV_AT = (6, 10, 14, 18)
+KV_AT = (3, 7, 12, 16)
 
 
 def tile_groupedqueryattention_pa_t_kernel(tc, xq, xk_rep, kv, mask, Wv, out):
@@ -105,7 +106,7 @@ def tile_groupedqueryattention_pa_t_kernel(tc, xq, xk_rep, kv, mask, Wv, out):
 
         def seed(qt):
             m_sb = st[("mraw", qt)]
-            if qt < 2:
+            if qt < SEEDS_FIRST:
                 ps = s_bank(F32, [P, NKT // 2, P], "mt_ps")
             else:
                 ps = et_bank(F32, [P, NKT // 2, P], "mt_ps")
@@ -370,9 +371,10 @@ def tile_groupedqueryattention_pa_t_kernel(tc, xq, xk_rep, kv, mask, Wv, out):
         load_xk_half(0, 0)
         load_xq(0)
         load_xk_half(0, 1)
-        load_mask(2)
+        for qt in range(2, 5):
+            load_mask(qt)
         load_xq(1)
-        for qt in range(3, MASK_BUFS):
+        for qt in range(5, MASK_BUFS):
             load_mask(qt)
         keep_clock(CLOCK_START)
         for qt in range(2):
@@ -380,13 +382,13 @@ def tile_groupedqueryattention_pa_t_kernel(tc, xq, xk_rep, kv, mask, Wv, out):
         square(0, nc.vector)
         keep_clock(CLOCK_LOADS)
         kT_transposes(0, 0)
+        seed(2)
         keep_clock(CLOCK_KEYS)
         qT_transposes(0)
+        seed(3)
         kT_leave(0, 0)
         qT_leave(0)
         square(1, nc.vector)
-        for qt in range(2, SEEDS_FIRST):
-            seed(qt)
         kv_load(0)
         wv_load()
         kv_load(1)
@@ -442,7 +444,7 @@ def tile_groupedqueryattention_pa_t_kernel(tc, xq, xk_rep, kv, mask, Wv, out):
         quant_in = by_tick(quant_at, NU // 2)
         pv_in = by_tick(pv_at, NG)
 
-        for tk in range(pv_at(NG - 1) + 2):
+        for tk in range(pv_at(NG - 1) + NORM_AFTER_PV + 1):
             for qt in range(2, NQT):
                 if tk == first_use[qt] - 10:
                     load_xq(qt)
@@ -460,7 +462,7 @@ def tile_groupedqueryattention_pa_t_kernel(tc, xq, xk_rep, kv, mask, Wv, out):
                 for pair in regroup_in.get(tk, []):
                     regroup(2 * pair + 1, nc.scalar.copy)
                     regroup(2 * pair, nc.scalar.copy)
-            for g in pv_in.get(tk - 1, []):
+            for g in pv_in.get(tk - NORM_AFTER_PV, []):
                 normalise(g)
             for pair in tr_in.get(tk, []):
                 transposes(2 * pair)
@@ -504,5 +506,5 @@ def tile_groupedqueryattention_pa_t_kernel(tc, xq, xk_rep, kv, mask, Wv, out):
                     v_quantise(b)
             for g in pv_in.get(tk + 1, []):
                 reciprocal(g)
-            for g in pv_in.get(tk - 1, []):
+            for g in pv_in.get(tk - NORM_AFTER_PV, []):
                 repeat(g)

@@ -37,10 +37,6 @@ NORM_AFTER_PV = 2
 T_BUFS = EXP_LAG_FIRST + 3
 SEEDS_FIRST = 4
 XK_AT = 3
-CLOCK_START = 4
-CLOCK_LOADS = 3
-CLOCK_KEYS = 2
-CLOCK_TICKS = 10
 SEEDS_A_TICK = 3
 SQUARE_LAG = 6
 SQUARES = 4
@@ -70,15 +66,7 @@ def tile_groupedqueryattention_pa_t_kernel(tc, xq, xk_rep, kv, mask, Wv, out):
         yT = keep.tile([P, NQT, NKT, P], F32, name="yT")
         kT = keep.tile([P, B, H, SKV], BF16, name="kT")
 
-        zeros = keep.tile([P, 512], BF16, name="zeros")
-        nc.vector.memset(zeros[:], 0.0)
-
         st = {}
-
-        def keep_clock(n):
-            for i in range(n):
-                nothing = s_bank(F32, [P, 512], "nothing")
-                nc.tensor.matmul(nothing[:], lhsT=zeros[:, 0:P], rhs=zeros[:], start=True, stop=True)
 
         def et_bank(dtype, shape, name):
             return psum.tile(shape, dtype, tag="et", bufs=ET_BANKS, name=name)
@@ -238,9 +226,6 @@ def tile_groupedqueryattention_pa_t_kernel(tc, xq, xk_rep, kv, mask, Wv, out):
         def penalties(u, c):
             qt, b, h = units[u]
             s_ps = s_bank(F32, [P, 512], "s_ps")
-            if c == 0:
-                for i in range(2 if u < 4 else 1 if u < CLOCK_TICKS else 0):
-                    nc.tensor.matmul(s_ps[:], lhsT=zeros[:, 0:P], rhs=zeros[:], start=True, stop=True)
             for jj in range(4):
                 nc.tensor.matmul(
                     s_ps[:, jj * P:(jj + 1) * P], lhsT=yT[:, qt, 4 * c + jj, :], rhs=ident_f[:],
@@ -350,6 +335,20 @@ def tile_groupedqueryattention_pa_t_kernel(tc, xq, xk_rep, kv, mask, Wv, out):
                 )
             st[("on", g)] = o_n
 
+        def finish(g):
+            own = st[("o", g)][:].rearrange("p h f -> p (h f)")[:, HD - DIST:HD - DIST + H * (HD - DIST)]
+            qt, b = groups[g]
+            for h in range(H):
+                o_sb = ring.tile([P, DIST, REP], F32, tag="ofin", bufs=4, name="o_fin")
+                src = own[:, h * (HD - DIST):h * (HD - DIST) + DIST].unsqueeze(2).to_broadcast([P, DIST, REP])
+                if h % 2 == 0:
+                    nc.scalar.activation(out=o_sb[:], in_=src, func=ACT.Copy, scale=st[("ri", g)][:, h:h + 1])
+                else:
+                    nc.vector.tensor_scalar(out=o_sb[:], in0=src, scalar1=st[("ri", g)][:, h:h + 1], scalar2=None, op0=ALU.mult)
+                nc.sync.dma_start(
+                    out=out[b, qt * P:(qt + 1) * P, h * HD:(h + 1) * HD], in_=o_sb[:].rearrange("p j r -> p (j r)")
+                )
+
         def repeat(g):
             qt, b = groups[g]
             o_sb = ring.tile([P, H * DIST, REP], F32, tag="osb", bufs=2, name="o_sb")
@@ -376,14 +375,11 @@ def tile_groupedqueryattention_pa_t_kernel(tc, xq, xk_rep, kv, mask, Wv, out):
         load_xq(1)
         for qt in range(5, MASK_BUFS):
             load_mask(qt)
-        keep_clock(CLOCK_START)
         for qt in range(2):
             seed(qt)
         square(0, nc.vector)
-        keep_clock(CLOCK_LOADS)
         kT_transposes(0, 0)
         seed(2)
-        keep_clock(CLOCK_KEYS)
         qT_transposes(0)
         seed(3)
         kT_leave(0, 0)
@@ -463,7 +459,10 @@ def tile_groupedqueryattention_pa_t_kernel(tc, xq, xk_rep, kv, mask, Wv, out):
                     regroup(2 * pair + 1, nc.scalar.copy)
                     regroup(2 * pair, nc.scalar.copy)
             for g in pv_in.get(tk - NORM_AFTER_PV, []):
-                normalise(g)
+                if g < NG - 1:
+                    normalise(g)
+                else:
+                    finish(g)
             for pair in tr_in.get(tk, []):
                 transposes(2 * pair)
                 transposes(2 * pair + 1)
@@ -483,8 +482,9 @@ def tile_groupedqueryattention_pa_t_kernel(tc, xq, xk_rep, kv, mask, Wv, out):
                     square(qt, nc.gpsimd)
             if tk >= NU:
                 for pair in regroup_in.get(tk, []):
+                    last = pair == NU // 2 - 1
                     regroup(2 * pair + 1, nc.vector.tensor_copy)
-                    regroup(2 * pair, nc.vector.tensor_copy)
+                    regroup(2 * pair, nc.scalar.copy if last else nc.vector.tensor_copy)
             if tk < NU:
                 leave_psum(tk, 0)
             for u in quant_in.get(tk, []):
@@ -507,4 +507,5 @@ def tile_groupedqueryattention_pa_t_kernel(tc, xq, xk_rep, kv, mask, Wv, out):
             for g in pv_in.get(tk + 1, []):
                 reciprocal(g)
             for g in pv_in.get(tk - NORM_AFTER_PV, []):
-                repeat(g)
+                if g < NG - 1:
+                    repeat(g)

@@ -27,22 +27,24 @@ FLOPS = 2 * B * SKV * DIN * HD + 2 * 2 * B * H * SQ * SKV * HD
 MASK_BUFS = 8
 S_BANKS = 5
 ET_BANKS = 3
-EXP_LAG_FIRST = 5
-EXP_LAG_LAST = 5
-TR_AFTER_EXP = 2
+EXP_LAG_FIRST = 6
+EXP_LAG_LAST = 6
+TR_AFTER_EXP = 1
 REGROUP_AFTER_TR = 1
 QUANT_AFTER_REGROUP = 2
 PV_AFTER_QUANT = 2
 NORM_AFTER_PV = 2
-T_BUFS = EXP_LAG_FIRST + 3
-SEEDS_FIRST = 4
-XK_AT = 3
-SEEDS_A_TICK = 3
+T_BUFS = EXP_LAG_FIRST + 2
+WARM_TICKS = 4
+SEEDS_FIRST = 6
 SQUARE_LAG = 6
 SQUARES = 4
 REPEATS = 2
-KT_AT = 4
-KV_AT = (3, 7, 12, 16)
+XK_AT = 10
+KT_AT = 24
+KT_STEP = 8
+KV_AT = (4, 8, 18, 38)
+KV_STEP = (1, 1, 4, 4)
 
 
 def tile_groupedqueryattention_pa_t_kernel(tc, xq, xk_rep, kv, mask, Wv, out):
@@ -87,17 +89,15 @@ def tile_groupedqueryattention_pa_t_kernel(tc, xq, xk_rep, kv, mask, Wv, out):
             half = st[("xk", b)][:, 4 * i:4 * i + 4, :]
             nc.sync.dma_start(out=half.rearrange("p (w e) c -> p w e c", e=2), in_=xk_v[:, b, 2 * i:2 * i + 2])
 
-        def load_xq(qt):
-            xq_sb = ring.tile([P, B, H * HD], BF16, tag="xq", bufs=2, name="xq_sb")
-            nc.sync.dma_start(out=xq_sb[:], in_=xq_v[:, :, qt, :])
-            st[("xq", qt)] = xq_sb
+        def load_xq(n):
+            b, tp = divmod(n, NQT // 2)
+            xq_sb = ring.tile([P, 2, H * HD], BF16, tag="xq", bufs=2, name="xq_sb")
+            nc.sync.dma_start(out=xq_sb[:], in_=xq_v[:, b, 2 * tp:2 * tp + 2, :])
+            st[("xq", n)] = xq_sb
 
         def seed(qt):
             m_sb = st[("mraw", qt)]
-            if qt < SEEDS_FIRST:
-                ps = s_bank(F32, [P, NKT // 2, P], "mt_ps")
-            else:
-                ps = et_bank(F32, [P, NKT // 2, P], "mt_ps")
+            ps = et_bank(F32, [P, NKT // 2, P], "mt_ps")
             words = m_sb[:].bitcast(F32)
             for w in range(NKT // 2):
                 nc.tensor.transpose(ps[:, w, :], words[:, w * P:(w + 1) * P], ident_f[:])
@@ -110,32 +110,39 @@ def tile_groupedqueryattention_pa_t_kernel(tc, xq, xk_rep, kv, mask, Wv, out):
             if qt + MASK_BUFS < NQT:
                 load_mask(qt + MASK_BUFS)
 
+        def warm(ps, n):
+            for i in range(n):
+                nc.tensor.matmul(ps[:], lhsT=ident_bf[:], rhs=zeros[:], start=True, stop=True)
+
         def square(qt, eng):
             for i in range(SQUARES):
                 y = yT[:, qt, NKT // SQUARES * i:NKT // SQUARES * (i + 1), :]
                 eng.tensor_tensor(out=y, in0=y, in1=y, op=ALU.mult)
 
-        def kT_transposes(b, h):
-            ps = s_bank(BF16, [P, NKT, P], "kt_ps")
-            for j in range(NKT):
-                nc.tensor.transpose(ps[:, j, :], st[("xk", b)][:, j, h * HD:(h + 1) * HD], ident_bf[:])
-            st[("ktps", b, h)] = ps
+        def kT_transposes(b, h, blocks=range(NKT)):
+            if 0 in blocks:
+                st[("ktps", b, h)] = s_bank(BF16, [P, NKT, P], "kt_ps")
+            for j in blocks:
+                nc.tensor.transpose(
+                    st[("ktps", b, h)][:, j, :], st[("xk", b)][:, j, h * HD:(h + 1) * HD], ident_bf[:]
+                )
 
-        def kT_leave(b, h):
-            src = st[("ktps", b, h)][:].rearrange("p j k -> p (j k)")
-            nc.vector.tensor_scalar(out=kT[:, b, h, :], in0=src, scalar1=-1.0, scalar2=None, op0=ALU.mult)
+        def kT_leave(b, h, blocks=range(NKT)):
+            keys = slice(blocks[0] * P, (blocks[-1] + 1) * P)
+            src = st[("ktps", b, h)][:].rearrange("p j k -> p (j k)")[:, keys]
+            nc.vector.tensor_scalar(out=kT[:, b, h, keys], in0=src, scalar1=-1.0, scalar2=None, op0=ALU.mult)
 
-        def qT_transposes(qt):
-            ps = s_bank(BF16, [P, B * H, P], "qt_ps")
-            for b in range(B):
+        def qT_transposes(n):
+            ps = s_bank(BF16, [P, 2 * H, P], "qt_ps")
+            for t in range(2):
                 for h in range(H):
-                    nc.tensor.transpose(ps[:, b * H + h, :], st[("xq", qt)][:, b, h * HD:(h + 1) * HD], ident_bf[:])
-            st[("qtps", qt)] = ps
+                    nc.tensor.transpose(ps[:, t * H + h, :], st[("xq", n)][:, t, h * HD:(h + 1) * HD], ident_bf[:])
+            st[("qtps", n)] = ps
 
-        def qT_leave(qt):
-            qT = ring.tile([P, B * H, P], BF16, tag="qT", bufs=2, name="qT")
-            nc.vector.tensor_copy(out=qT[:], in_=st[("qtps", qt)][:])
-            st[("qT", qt)] = qT
+        def qT_leave(n):
+            qT = ring.tile([P, 2 * H, P], BF16, tag="qT", bufs=2, name="qT")
+            nc.vector.tensor_copy(out=qT[:], in_=st[("qtps", n)][:])
+            st[("qT", n)] = qT
 
         wv_raw = keep.tile([P, 2, 2, 2, HD], BF16, name="wv_raw")
         wv_grp = keep.tile([P, 2, HD, 4], BF16, name="wv_grp", align_bytes=64)
@@ -169,7 +176,7 @@ def tile_groupedqueryattention_pa_t_kernel(tc, xq, xk_rep, kv, mask, Wv, out):
             st[("kv", c)] = kv_sb
 
         def kv_transpose(c, t):
-            xt = s_bank(F32, [P, 4, P], "xt")
+            xt = s_bank(F32, [P, 4, P], "xt") if c < 2 else et_bank(F32, [P, 4, P], "xt")
             kw = st[("kv", c)][:, t, :].bitcast(F32)
             for w in range(4):
                 nc.tensor.transpose(xt[:, w, :], kw[:, w * P:(w + 1) * P], ident_f[:])
@@ -179,7 +186,8 @@ def tile_groupedqueryattention_pa_t_kernel(tc, xq, xk_rep, kv, mask, Wv, out):
             if t == 0:
                 st[("kvg", c)] = ring.tile([P, 4 * 1024], BF16, tag="kvg", bufs=1, name="kv_grp", align_bytes=64)
             grp_w = st[("kvg", c)][:].bitcast(F32).rearrange("p (t g k u) -> p t g k u", t=4, g=2, u=2)
-            nc.vector.tensor_copy(out=grp_w[:, t], in_=st[("xt", c, t)][:].rearrange("p (g u) k -> p g k u", u=2))
+            copy = nc.vector.tensor_copy if c < 2 else nc.scalar.copy
+            copy(out=grp_w[:, t], in_=st[("xt", c, t)][:].rearrange("p (g u) k -> p g k u", u=2))
 
         def kv_quantise(c):
             kv_codes = ring.tile([P, 1024], U32, tag="kvc", bufs=1, name="kv_codes", align_bytes=64)
@@ -218,7 +226,7 @@ def tile_groupedqueryattention_pa_t_kernel(tc, xq, xk_rep, kv, mask, Wv, out):
             )
             st[("v", b)] = (vc, vs)
 
-        groups = [(0, 0), (1, 0), (0, 1), (1, 1)] + [(qt, b) for qt in range(2, NQT) for b in range(B)]
+        groups = [(qt, b) for b in range(B) for qt in range(NQT)]
         units = [(qt, b, h) for (qt, b) in groups for h in range(H)]
         NU = len(units)
         NG = len(groups)
@@ -226,6 +234,8 @@ def tile_groupedqueryattention_pa_t_kernel(tc, xq, xk_rep, kv, mask, Wv, out):
         def penalties(u, c):
             qt, b, h = units[u]
             s_ps = s_bank(F32, [P, 512], "s_ps")
+            if u < WARM_TICKS and c == 0:
+                warm(s_ps, 1)
             for jj in range(4):
                 nc.tensor.matmul(
                     s_ps[:, jj * P:(jj + 1) * P], lhsT=yT[:, qt, 4 * c + jj, :], rhs=ident_f[:],
@@ -236,7 +246,7 @@ def tile_groupedqueryattention_pa_t_kernel(tc, xq, xk_rep, kv, mask, Wv, out):
         def scores(u, c):
             qt, b, h = units[u]
             nc.tensor.matmul(
-                st[("s", u, c)][:], lhsT=st[("qT", qt)][:, b * H + h, :], rhs=kT[:, b, h, c * 512:(c + 1) * 512],
+                st[("s", u, c)][:], lhsT=st[("qT", u // (2 * H))][:, u % (2 * H), :], rhs=kT[:, b, h, c * 512:(c + 1) * 512],
                 start=False, stop=True,
             )
 
@@ -365,29 +375,50 @@ def tile_groupedqueryattention_pa_t_kernel(tc, xq, xk_rep, kv, mask, Wv, out):
             nc.sync.dma_start(out=out[b, qt * P:(qt + 1) * P, :], in_=o_sb[:].rearrange("p j r -> p (j r)"))
 
         load_mask(0)
-        load_mask(1)
         load_xk(0)
         load_xk_half(0, 0)
+        load_mask(1)
         load_xq(0)
+        load_mask(2)
         load_xk_half(0, 1)
-        for qt in range(2, 5):
+        for qt in range(3, MASK_BUFS):
             load_mask(qt)
         load_xq(1)
-        for qt in range(5, MASK_BUFS):
-            load_mask(qt)
-        for qt in range(2):
-            seed(qt)
-        square(0, nc.vector)
-        kT_transposes(0, 0)
-        seed(2)
+        zeros = keep.tile([P, 512], BF16, name="zeros")
+        nc.vector.memset(zeros[:], 0.0)
+        w_ps = s_bank(F32, [P, 512], "w_ps")
+        half = (range(NKT // 2), range(NKT // 2, NKT))
+        warm(w_ps, 5)
+        seed(0)
+        warm(w_ps, 2)
+        kT_transposes(0, 0, half[0])
+        seed(1)
+        warm(w_ps, 2)
         qT_transposes(0)
-        seed(3)
-        kT_leave(0, 0)
+        warm(w_ps, 2)
+        seed(2)
+        kT_transposes(0, 0, half[1])
+        kT_transposes(0, 1)
+        warm(w_ps, 2)
+        square(0, nc.vector)
+        kT_leave(0, 0, half[0])
         qT_leave(0)
-        square(1, nc.vector)
+        kT_leave(0, 0, half[1])
+        kT_leave(0, 1)
+        seed(3)
+        seed(4)
+        seed(5)
         kv_load(0)
         wv_load()
         kv_load(1)
+
+        def kvq_tick(c):
+            return KV_AT[c] + 3 * KV_STEP[c] + (1 if c < 2 else 2)
+
+        def xv_tick(c):
+            return kvq_tick(c) + 3
+
+        NQ = B * NQT // 2
 
         first_use = {}
         for u in range(NU):
@@ -395,21 +426,24 @@ def tile_groupedqueryattention_pa_t_kernel(tc, xq, xk_rep, kv, mask, Wv, out):
                 first_use[units[u][0]] = u
 
         extras = {}
+        kv_in = {}
 
         def extra(tick, fill, leave, *args):
             extras.setdefault(tick, []).append((lambda: fill(*args), lambda: leave(*args)))
 
-        for h in (1, 2, 3):
-            extra(h - 1, kT_transposes, kT_leave, 0, h)
-        extra(2, qT_transposes, qT_leave, 1)
+        for h in (2, 3):
+            extra(h - 2, kT_transposes, kT_leave, 0, h)
         for h in range(H):
-            extra(KT_AT + h, kT_transposes, kT_leave, 1, h)
-        for qt in range(2, NQT):
-            extra(first_use[qt] - 4, qT_transposes, qT_leave, qt)
+            extra(KT_AT + KT_STEP * h, kT_transposes, kT_leave, 1, h)
+        for n in range(1, NQ):
+            extra(2 * H * n - 4, qT_transposes, qT_leave, n)
         for c in range(4):
             for t in range(4):
-                extra(KV_AT[c] + t, kv_transpose, kv_leave, c, t)
-            extra(KV_AT[c] + 5, xv_matmul, xv_leave, c)
+                if c < 2:
+                    extra(KV_AT[c] + KV_STEP[c] * t, kv_transpose, kv_leave, c, t)
+                else:
+                    kv_in[KV_AT[c] + KV_STEP[c] * t] = (c, t)
+            extra(xv_tick(c), xv_matmul, xv_leave, c)
 
         def exp_at(pair):
             u = 2 * pair + 1
@@ -425,7 +459,7 @@ def tile_groupedqueryattention_pa_t_kernel(tc, xq, xk_rep, kv, mask, Wv, out):
             return regroup_at(pair) + QUANT_AFTER_REGROUP
 
         def pv_at(g):
-            values_at = KV_AT[2 * groups[g][1] + 1] + 6
+            values_at = xv_tick(2 * groups[g][1] + 1) + 1
             return max(quant_at(H // 2 * g + H // 2 - 1) + PV_AFTER_QUANT, values_at + 1)
 
         def by_tick(at, n):
@@ -434,6 +468,12 @@ def tile_groupedqueryattention_pa_t_kernel(tc, xq, xk_rep, kv, mask, Wv, out):
                 table.setdefault(at(i), []).append(i)
             return table
 
+        def seed_at(i):
+            return i // 2
+
+        seed_in = {}
+        for qt in range(SEEDS_FIRST, NQT):
+            seed_in.setdefault(seed_at(qt - SEEDS_FIRST), []).append(qt)
         exp_in = by_tick(exp_at, NU // 2)
         tr_in = by_tick(tr_at, NU // 2)
         regroup_in = by_tick(regroup_at, NU // 2)
@@ -441,15 +481,15 @@ def tile_groupedqueryattention_pa_t_kernel(tc, xq, xk_rep, kv, mask, Wv, out):
         pv_in = by_tick(pv_at, NG)
 
         for tk in range(pv_at(NG - 1) + NORM_AFTER_PV + 1):
-            for qt in range(2, NQT):
-                if tk == first_use[qt] - 10:
-                    load_xq(qt)
+            for n in range(2, NQ):
+                if tk == 2 * H * n - 10:
+                    load_xq(n)
             if tk == XK_AT:
                 load_xk(1)
                 for i in range(2):
                     load_xk_half(1, i)
             for c in (2, 3):
-                if tk == KV_AT[c - 2] + 4:
+                if tk == kvq_tick(c - 2) + 1:
                     kv_load(c)
             for pair in exp_in.get(tk, []):
                 exponent(2 * pair + 1)
@@ -458,6 +498,8 @@ def tile_groupedqueryattention_pa_t_kernel(tc, xq, xk_rep, kv, mask, Wv, out):
                 for pair in regroup_in.get(tk, []):
                     regroup(2 * pair + 1, nc.scalar.copy)
                     regroup(2 * pair, nc.scalar.copy)
+            if tk - 1 in kv_in:
+                kv_leave(*kv_in[tk - 1])
             for g in pv_in.get(tk - NORM_AFTER_PV, []):
                 if g < NG - 1:
                     normalise(g)
@@ -466,6 +508,8 @@ def tile_groupedqueryattention_pa_t_kernel(tc, xq, xk_rep, kv, mask, Wv, out):
             for pair in tr_in.get(tk, []):
                 transposes(2 * pair)
                 transposes(2 * pair + 1)
+            if tk in kv_in:
+                kv_transpose(*kv_in[tk])
             if tk < NU:
                 penalties(tk, 0)
                 penalties(tk, 1)
@@ -475,10 +519,10 @@ def tile_groupedqueryattention_pa_t_kernel(tc, xq, xk_rep, kv, mask, Wv, out):
                 weighted_sum(g)
             for fill, leave in extras.get(tk, []):
                 fill()
-            for qt in range(SEEDS_FIRST + SEEDS_A_TICK * tk, min(NQT, SEEDS_FIRST + SEEDS_A_TICK * (tk + 1))):
+            for qt in seed_in.get(tk, []):
                 seed(qt)
-            for qt in range(2, NQT):
-                if tk == first_use[qt] - SQUARE_LAG:
+            for qt in range(1, NQT):
+                if tk == max(0, first_use[qt] - SQUARE_LAG):
                     square(qt, nc.gpsimd)
             if tk >= NU:
                 for pair in regroup_in.get(tk, []):
@@ -493,7 +537,7 @@ def tile_groupedqueryattention_pa_t_kernel(tc, xq, xk_rep, kv, mask, Wv, out):
                 leave_psum(tk, 1)
                 row_min(tk)
             for c in range(4):
-                if tk == KV_AT[c] + 4:
+                if tk == kvq_tick(c):
                     kv_quantise(c)
             for fill, leave in extras.get(tk, []):
                 leave()
@@ -502,7 +546,7 @@ def tile_groupedqueryattention_pa_t_kernel(tc, xq, xk_rep, kv, mask, Wv, out):
             if tk == KV_AT[0] + 2:
                 wv_quantise()
             for b in range(B):
-                if tk == KV_AT[2 * b + 1] + 6:
+                if tk == xv_tick(2 * b + 1) + 1:
                     v_quantise(b)
             for g in pv_in.get(tk + 1, []):
                 reciprocal(g)

@@ -24,6 +24,9 @@ SCALE = 1.0 / math.sqrt(HD)
 ROOT = math.sqrt(HD)
 FLOPS = 2 * B * SKV * DIN * HD + 2 * 2 * B * H * SQ * SKV * HD
 
+NORM_EVERY = 2
+KV_ON_S = 2
+KV0_BEHIND = 5
 MASK_BUFS = 8
 S_BANKS = 5
 ET_BANKS = 3
@@ -43,7 +46,7 @@ REPEATS = 2
 XK_AT = 10
 KT_AT = 24
 KT_STEP = 8
-KV_AT = (4, 8, 18, 38)
+KV_AT = (1, 5, 18, 38)
 KV_STEP = (1, 1, 4, 4)
 
 
@@ -176,7 +179,7 @@ def tile_groupedqueryattention_pa_t_kernel(tc, xq, xk_rep, kv, mask, Wv, out):
             st[("kv", c)] = kv_sb
 
         def kv_transpose(c, t):
-            xt = s_bank(F32, [P, 4, P], "xt") if c < 2 else et_bank(F32, [P, 4, P], "xt")
+            xt = s_bank(F32, [P, 4, P], "xt") if c < KV_ON_S else et_bank(F32, [P, 4, P], "xt")
             kw = st[("kv", c)][:, t, :].bitcast(F32)
             for w in range(4):
                 nc.tensor.transpose(xt[:, w, :], kw[:, w * P:(w + 1) * P], ident_f[:])
@@ -186,7 +189,7 @@ def tile_groupedqueryattention_pa_t_kernel(tc, xq, xk_rep, kv, mask, Wv, out):
             if t == 0:
                 st[("kvg", c)] = ring.tile([P, 4 * 1024], BF16, tag="kvg", bufs=1, name="kv_grp", align_bytes=64)
             grp_w = st[("kvg", c)][:].bitcast(F32).rearrange("p (t g k u) -> p t g k u", t=4, g=2, u=2)
-            copy = nc.vector.tensor_copy if c < 2 else nc.scalar.copy
+            copy = nc.vector.tensor_copy if c < KV_ON_S else nc.scalar.copy
             copy(out=grp_w[:, t], in_=st[("xt", c, t)][:].rearrange("p (g u) k -> p g k u", u=2))
 
         def kv_quantise(c):
@@ -336,6 +339,20 @@ def tile_groupedqueryattention_pa_t_kernel(tc, xq, xk_rep, kv, mask, Wv, out):
             nc.vector.reciprocal(rinv[:], st[("rs", g)][:])
             st[("ri", g)] = rinv
 
+        def on_vector(g):
+            return g < NG - 1 and g % NORM_EVERY == NORM_EVERY - 1
+
+        def normalise_on_vector(g):
+            own = st[("o", g)][:].rearrange("p h f -> p (h f)")[:, HD - DIST:HD - DIST + H * (HD - DIST)]
+            o_n = ring.tile([P, H, DIST], F32, tag="on", bufs=2, name="o_n")
+            nc.vector.tensor_tensor(
+                out=o_n[:],
+                in0=own.rearrange("p (h f) -> p h f", h=H)[:, :, 0:DIST],
+                in1=st[("ri", g)][:].unsqueeze(2).to_broadcast([P, H, DIST]),
+                op=ALU.mult,
+            )
+            st[("on", g)] = o_n
+
         def normalise(g):
             own = st[("o", g)][:].rearrange("p h f -> p (h f)")[:, HD - DIST:HD - DIST + H * (HD - DIST)]
             o_n = ring.tile([P, H, DIST], F32, tag="on", bufs=2, name="o_n")
@@ -383,6 +400,8 @@ def tile_groupedqueryattention_pa_t_kernel(tc, xq, xk_rep, kv, mask, Wv, out):
         load_xk_half(0, 1)
         for qt in range(3, MASK_BUFS):
             load_mask(qt)
+            if qt == KV0_BEHIND:
+                kv_load(0)
         load_xq(1)
         zeros = keep.tile([P, 512], BF16, name="zeros")
         nc.vector.memset(zeros[:], 0.0)
@@ -408,12 +427,11 @@ def tile_groupedqueryattention_pa_t_kernel(tc, xq, xk_rep, kv, mask, Wv, out):
         seed(3)
         seed(4)
         seed(5)
-        kv_load(0)
         wv_load()
         kv_load(1)
 
         def kvq_tick(c):
-            return KV_AT[c] + 3 * KV_STEP[c] + (1 if c < 2 else 2)
+            return KV_AT[c] + 3 * KV_STEP[c] + (1 if c < KV_ON_S else 2)
 
         def xv_tick(c):
             return kvq_tick(c) + 3
@@ -439,7 +457,7 @@ def tile_groupedqueryattention_pa_t_kernel(tc, xq, xk_rep, kv, mask, Wv, out):
             extra(2 * H * n - 4, qT_transposes, qT_leave, n)
         for c in range(4):
             for t in range(4):
-                if c < 2:
+                if c < KV_ON_S:
                     extra(KV_AT[c] + KV_STEP[c] * t, kv_transpose, kv_leave, c, t)
                 else:
                     kv_in[KV_AT[c] + KV_STEP[c] * t] = (c, t)
@@ -501,10 +519,10 @@ def tile_groupedqueryattention_pa_t_kernel(tc, xq, xk_rep, kv, mask, Wv, out):
             if tk - 1 in kv_in:
                 kv_leave(*kv_in[tk - 1])
             for g in pv_in.get(tk - NORM_AFTER_PV, []):
-                if g < NG - 1:
-                    normalise(g)
-                else:
+                if g == NG - 1:
                     finish(g)
+                elif not on_vector(g):
+                    normalise(g)
             for pair in tr_in.get(tk, []):
                 transposes(2 * pair)
                 transposes(2 * pair + 1)
@@ -524,6 +542,9 @@ def tile_groupedqueryattention_pa_t_kernel(tc, xq, xk_rep, kv, mask, Wv, out):
             for qt in range(1, NQT):
                 if tk == max(0, first_use[qt] - SQUARE_LAG):
                     square(qt, nc.gpsimd)
+            for g in pv_in.get(tk - 1, []):
+                if on_vector(g):
+                    normalise_on_vector(g)
             if tk >= NU:
                 for pair in regroup_in.get(tk, []):
                     last = pair == NU // 2 - 1

@@ -26,7 +26,8 @@ FLOPS = 2 * B * SKV * DIN * HD + 2 * 2 * B * H * SQ * SKV * HD
 
 NORM_EVERY = 2
 KV_ON_S = 2
-KV0_BEHIND = 5
+XK_BEHIND = 4
+KV0_BEHIND = 7
 MASK_BUFS = 8
 S_BANKS = 5
 ET_BANKS = 3
@@ -38,16 +39,17 @@ QUANT_AFTER_REGROUP = 2
 PV_AFTER_QUANT = 2
 NORM_AFTER_PV = 2
 T_BUFS = EXP_LAG_FIRST + 2
-WARM_TICKS = 4
-SEEDS_FIRST = 6
+WARM_UNITS = 4
+SEEDS_FIRST = 12
 SQUARE_LAG = 6
 SQUARES = 4
 REPEATS = 2
 XK_AT = 10
 KT_AT = 24
 KT_STEP = 8
-KV_AT = (1, 5, 18, 38)
-KV_STEP = (1, 1, 4, 4)
+KV_AT = (4, 6, 18, 38)
+KV_STEP = 4
+KV_A_TICK = 2
 
 
 def tile_groupedqueryattention_pa_t_kernel(tc, xq, xk_rep, kv, mask, Wv, out):
@@ -122,18 +124,25 @@ def tile_groupedqueryattention_pa_t_kernel(tc, xq, xk_rep, kv, mask, Wv, out):
                 y = yT[:, qt, NKT // SQUARES * i:NKT // SQUARES * (i + 1), :]
                 eng.tensor_tensor(out=y, in0=y, in1=y, op=ALU.mult)
 
-        def kT_transposes(b, h, blocks=range(NKT)):
-            if 0 in blocks:
-                st[("ktps", b, h)] = s_bank(BF16, [P, NKT, P], "kt_ps")
-            for j in blocks:
-                nc.tensor.transpose(
-                    st[("ktps", b, h)][:, j, :], st[("xk", b)][:, j, h * HD:(h + 1) * HD], ident_bf[:]
-                )
+        def kT_transposes(b, hp, i):
+            ps = s_bank(BF16, [P, 2, NKT // 2, P], "kt_ps")
+            for h in range(2):
+                for j in range(NKT // 2):
+                    nc.tensor.transpose(
+                        ps[:, h, j, :],
+                        st[("xk", b)][:, NKT // 2 * i + j, (2 * hp + h) * HD:(2 * hp + h + 1) * HD],
+                        ident_bf[:],
+                    )
+            st[("ktps", b, hp, i)] = ps
 
-        def kT_leave(b, h, blocks=range(NKT)):
-            keys = slice(blocks[0] * P, (blocks[-1] + 1) * P)
-            src = st[("ktps", b, h)][:].rearrange("p j k -> p (j k)")[:, keys]
-            nc.vector.tensor_scalar(out=kT[:, b, h, keys], in0=src, scalar1=-1.0, scalar2=None, op0=ALU.mult)
+        def kT_leave(b, hp, i):
+            nc.vector.tensor_scalar(
+                out=kT[:, b, 2 * hp:2 * hp + 2, i * 512:(i + 1) * 512],
+                in0=st[("ktps", b, hp, i)][:].rearrange("p h j k -> p h (j k)"),
+                scalar1=-1.0,
+                scalar2=None,
+                op0=ALU.mult,
+            )
 
         def qT_transposes(n):
             ps = s_bank(BF16, [P, 2 * H, P], "qt_ps")
@@ -237,7 +246,7 @@ def tile_groupedqueryattention_pa_t_kernel(tc, xq, xk_rep, kv, mask, Wv, out):
         def penalties(u, c):
             qt, b, h = units[u]
             s_ps = s_bank(F32, [P, 512], "s_ps")
-            if u < WARM_TICKS and c == 0:
+            if u < WARM_UNITS:
                 warm(s_ps, 1)
             for jj in range(4):
                 nc.tensor.matmul(
@@ -289,30 +298,29 @@ def tile_groupedqueryattention_pa_t_kernel(tc, xq, xk_rep, kv, mask, Wv, out):
 
         def transposes(u):
             e = st[("e", u)]
-            et_ps = et_bank(F32, [P, 4, P], "et_ps")
+            et_ps = (et_bank if u < NU - 4 else s_bank)(F32, [P, 4, P], "et_ps")
             ew = e[:].bitcast(F32)
             for w in range(4):
                 nc.tensor.transpose(et_ps[:, w, :], ew[:, w * P:(w + 1) * P], ident_f[:])
             st[("et", u)] = et_ps
 
         def regroup(u, copy):
-            if u % 2 == 1:
-                st[("etg", u // 2)] = ring.tile([P, 2, 2 * P * 4], BF16, tag="etg", bufs=4, name="et_grp", align_bytes=64)
+            if u % H == 1:
+                st[("etg", u // H)] = ring.tile([P, H, 2 * P * 4], BF16, tag="etg", bufs=2, name="et_grp", align_bytes=64)
             src = st[("et", u)][:].rearrange("p (g u) q -> p g q u", u=2)
-            dst = st[("etg", u // 2)][:, u % 2, :].bitcast(F32).rearrange("p (g q u) -> p g q u", g=2, u=2)
+            dst = st[("etg", u // H)][:, u % H, :].bitcast(F32).rearrange("p (g q u) -> p g q u", g=2, u=2)
             copy(out=dst, in_=src)
 
         def quantise(pair):
-            h = 2 * pair % H
             g = 2 * pair // H
-            if h == 0:
-                st[("ec", g)] = ring.tile([P, H * 2 * P], U32, tag="ec", bufs=3, name="e_codes", align_bytes=64)
-                st[("es", g)] = ring.tile([P, H * 2 * P], U8, tag="es", bufs=3, name="e_scales", align_bytes=64)
-            cols = slice(h * 2 * P, (h + 2) * 2 * P)
+            if 2 * pair % H == 0:
+                return
+            st[("ec", g)] = ring.tile([P, H * 2 * P], U32, tag="ec", bufs=2, name="e_codes", align_bytes=64)
+            st[("es", g)] = ring.tile([P, H * 2 * P], U8, tag="es", bufs=2, name="e_scales", align_bytes=64)
             nc.vector.quantize_mx(
-                out=st[("ec", g)][:, cols].bitcast(FP8X4),
-                scales=st[("es", g)][:, cols],
-                in_=st[("etg", pair)][:].rearrange("p k x -> p (k x)"),
+                out=st[("ec", g)][:].bitcast(FP8X4),
+                scales=st[("es", g)][:],
+                in_=st[("etg", g)][:].rearrange("p k x -> p (k x)"),
             )
 
         def weighted_sum(g):
@@ -396,45 +404,57 @@ def tile_groupedqueryattention_pa_t_kernel(tc, xq, xk_rep, kv, mask, Wv, out):
         load_xk_half(0, 0)
         load_mask(1)
         load_xq(0)
-        load_mask(2)
-        load_xk_half(0, 1)
-        for qt in range(3, MASK_BUFS):
+        for qt in range(2, MASK_BUFS):
             load_mask(qt)
+            if qt == XK_BEHIND:
+                load_xk_half(0, 1)
             if qt == KV0_BEHIND:
                 kv_load(0)
-        load_xq(1)
         zeros = keep.tile([P, 512], BF16, name="zeros")
         nc.vector.memset(zeros[:], 0.0)
         w_ps = s_bank(F32, [P, 512], "w_ps")
-        half = (range(NKT // 2), range(NKT // 2, NKT))
         warm(w_ps, 5)
         seed(0)
         warm(w_ps, 2)
-        kT_transposes(0, 0, half[0])
+        kT_transposes(0, 0, 0)
         seed(1)
-        warm(w_ps, 2)
         qT_transposes(0)
-        warm(w_ps, 2)
+        kT_transposes(0, 1, 0)
         seed(2)
-        kT_transposes(0, 0, half[1])
-        kT_transposes(0, 1)
         warm(w_ps, 2)
         square(0, nc.vector)
-        kT_leave(0, 0, half[0])
+        kT_leave(0, 0, 0)
         qT_leave(0)
-        kT_leave(0, 0, half[1])
-        kT_leave(0, 1)
-        seed(3)
-        seed(4)
-        seed(5)
+        kT_leave(0, 1, 0)
+        for u in range(H):
+            penalties(u, 0)
+            scores(u, 0)
+            leave_psum(u, 0)
+            seed(3 + u)
+        square(1, nc.gpsimd)
+        kT_transposes(0, 0, 1)
+        kT_transposes(0, 1, 1)
+        kT_leave(0, 0, 1)
+        kT_leave(0, 1, 1)
+        seed(7)
+        for u in range(H):
+            penalties(u, 1)
+            scores(u, 1)
+            leave_psum(u, 1)
+            row_min(u)
+            seed(8 + u)
+        load_xq(1)
         wv_load()
         kv_load(1)
 
+        def kv_tick(c, t):
+            return KV_AT[c] + (t // KV_A_TICK if c < KV_ON_S else KV_STEP * t)
+
         def kvq_tick(c):
-            return KV_AT[c] + 3 * KV_STEP[c] + (1 if c < KV_ON_S else 2)
+            return kv_tick(c, 3) + (1 if c < KV_ON_S else 2)
 
         def xv_tick(c):
-            return kvq_tick(c) + 3
+            return kvq_tick(c) + 4
 
         NQ = B * NQT // 2
 
@@ -449,18 +469,16 @@ def tile_groupedqueryattention_pa_t_kernel(tc, xq, xk_rep, kv, mask, Wv, out):
         def extra(tick, fill, leave, *args):
             extras.setdefault(tick, []).append((lambda: fill(*args), lambda: leave(*args)))
 
-        for h in (2, 3):
-            extra(h - 2, kT_transposes, kT_leave, 0, h)
-        for h in range(H):
-            extra(KT_AT + KT_STEP * h, kT_transposes, kT_leave, 1, h)
+        for n in range(4):
+            extra(KT_AT + KT_STEP * n, kT_transposes, kT_leave, 1, n // 2, n % 2)
         for n in range(1, NQ):
             extra(2 * H * n - 4, qT_transposes, qT_leave, n)
         for c in range(4):
             for t in range(4):
                 if c < KV_ON_S:
-                    extra(KV_AT[c] + KV_STEP[c] * t, kv_transpose, kv_leave, c, t)
+                    extra(kv_tick(c, t), kv_transpose, kv_leave, c, t)
                 else:
-                    kv_in[KV_AT[c] + KV_STEP[c] * t] = (c, t)
+                    kv_in[kv_tick(c, t)] = (c, t)
             extra(xv_tick(c), xv_matmul, xv_leave, c)
 
         def exp_at(pair):
@@ -487,7 +505,7 @@ def tile_groupedqueryattention_pa_t_kernel(tc, xq, xk_rep, kv, mask, Wv, out):
             return table
 
         def seed_at(i):
-            return i // 2
+            return H + i // 2
 
         seed_in = {}
         for qt in range(SEEDS_FIRST, NQT):
@@ -524,11 +542,11 @@ def tile_groupedqueryattention_pa_t_kernel(tc, xq, xk_rep, kv, mask, Wv, out):
                 elif not on_vector(g):
                     normalise(g)
             for pair in tr_in.get(tk, []):
-                transposes(2 * pair)
-                transposes(2 * pair + 1)
+                for u in (2 * pair + 1, 2 * pair) if pair == NU // 2 - 1 else (2 * pair, 2 * pair + 1):
+                    transposes(u)
             if tk in kv_in:
                 kv_transpose(*kv_in[tk])
-            if tk < NU:
+            if H <= tk < NU:
                 penalties(tk, 0)
                 penalties(tk, 1)
                 scores(tk, 1)
@@ -539,8 +557,8 @@ def tile_groupedqueryattention_pa_t_kernel(tc, xq, xk_rep, kv, mask, Wv, out):
                 fill()
             for qt in seed_in.get(tk, []):
                 seed(qt)
-            for qt in range(1, NQT):
-                if tk == max(0, first_use[qt] - SQUARE_LAG):
+            for qt in range(2, NQT):
+                if tk == first_use[qt] - SQUARE_LAG:
                     square(qt, nc.gpsimd)
             for g in pv_in.get(tk - 1, []):
                 if on_vector(g):
@@ -550,11 +568,11 @@ def tile_groupedqueryattention_pa_t_kernel(tc, xq, xk_rep, kv, mask, Wv, out):
                     last = pair == NU // 2 - 1
                     regroup(2 * pair + 1, nc.vector.tensor_copy)
                     regroup(2 * pair, nc.scalar.copy if last else nc.vector.tensor_copy)
-            if tk < NU:
+            if H <= tk < NU:
                 leave_psum(tk, 0)
             for u in quant_in.get(tk, []):
                 quantise(u)
-            if tk < NU:
+            if H <= tk < NU:
                 leave_psum(tk, 1)
                 row_min(tk)
             for c in range(4):

@@ -31,14 +31,14 @@ KV0_BEHIND = 7
 MASK_BUFS = 8
 S_BANKS = 5
 ET_BANKS = 3
-EXP_LAG_FIRST = 6
-EXP_LAG_LAST = 6
+EXP_LAG = 6
+TAIL = 8
 TR_AFTER_EXP = 1
 REGROUP_AFTER_TR = 1
 QUANT_AFTER_REGROUP = 2
 PV_AFTER_QUANT = 2
 NORM_AFTER_PV = 2
-T_BUFS = EXP_LAG_FIRST + 2
+T_BUFS = EXP_LAG + 2
 WARM_UNITS = 4
 SEEDS_FIRST = 12
 SQUARE_LAG = 6
@@ -298,61 +298,68 @@ def tile_groupedqueryattention_pa_t_kernel(tc, xq, xk_rep, kv, mask, Wv, out):
 
         def transposes(u):
             e = st[("e", u)]
-            et_ps = (et_bank if u < NU - 4 else s_bank)(F32, [P, 4, P], "et_ps")
+            et_ps = (et_bank if u < NU - TAIL else s_bank)(F32, [P, 4, P], "et_ps")
             ew = e[:].bitcast(F32)
             for w in range(4):
                 nc.tensor.transpose(et_ps[:, w, :], ew[:, w * P:(w + 1) * P], ident_f[:])
             st[("et", u)] = et_ps
 
-        def regroup(u, copy):
+        def regroup(u, copy, halves=slice(0, 2)):
             if u % H == 1:
                 st[("etg", u // H)] = ring.tile([P, H, 2 * P * 4], BF16, tag="etg", bufs=2, name="et_grp", align_bytes=64)
-            src = st[("et", u)][:].rearrange("p (g u) q -> p g q u", u=2)
-            dst = st[("etg", u // H)][:, u % H, :].bitcast(F32).rearrange("p (g q u) -> p g q u", g=2, u=2)
+            src = st[("et", u)][:].rearrange("p (g u) q -> p g q u", u=2)[:, halves]
+            dst = st[("etg", u // H)][:, u % H, :].bitcast(F32).rearrange("p (g q u) -> p g q u", g=2, u=2)[:, halves]
             copy(out=dst, in_=src)
 
-        def quantise(pair):
-            g = 2 * pair // H
-            if 2 * pair % H == 0:
-                return
-            st[("ec", g)] = ring.tile([P, H * 2 * P], U32, tag="ec", bufs=2, name="e_codes", align_bytes=64)
-            st[("es", g)] = ring.tile([P, H * 2 * P], U8, tag="es", bufs=2, name="e_scales", align_bytes=64)
+        def quantise(g, heads=range(H)):
+            if heads[0] == 0:
+                st[("ec", g)] = ring.tile([P, H * 2 * P], U32, tag="ec", bufs=2, name="e_codes", align_bytes=64)
+                st[("es", g)] = ring.tile([P, H * 2 * P], U8, tag="es", bufs=2, name="e_scales", align_bytes=64)
+            cols = slice(heads[0] * 2 * P, (heads[-1] + 1) * 2 * P)
             nc.vector.quantize_mx(
-                out=st[("ec", g)][:].bitcast(FP8X4),
-                scales=st[("es", g)][:],
-                in_=st[("etg", g)][:].rearrange("p k x -> p (k x)"),
+                out=st[("ec", g)][:, cols].bitcast(FP8X4),
+                scales=st[("es", g)][:, cols],
+                in_=st[("etg", g)][:, heads[0]:heads[-1] + 1, :].rearrange("p k x -> p (k x)"),
             )
 
+        def head_sum(g, h, o):
+            vc, vs = st[("v", groups[g][1])]
+            for gg in range(2):
+                cols = slice((h * 2 + gg) * P, (h * 2 + gg + 1) * P)
+                vcols = slice(gg * HD, (gg + 1) * HD)
+                nc.tensor.matmul_mx(
+                    out=o,
+                    lhsT=st[("ec", g)][:, cols].bitcast(FP8X4),
+                    lhsT_scale=st[("es", g)][:, cols],
+                    rhs=vc[:, vcols].bitcast(FP8X4),
+                    rhs_scale=vs[:, vcols],
+                    start=(gg == 0),
+                    stop=(gg == 1),
+                )
+
         def weighted_sum(g):
-            qt, b = groups[g]
-            vc, vs = st[("v", b)]
             o_ps = et_bank(F32, [P, H, HD], "o_ps")
             for h in range(H):
-                for gg in range(2):
-                    cols = slice((h * 2 + gg) * P, (h * 2 + gg + 1) * P)
-                    vcols = slice(gg * HD, (gg + 1) * HD)
-                    nc.tensor.matmul_mx(
-                        out=o_ps[:, h, :],
-                        lhsT=st[("ec", g)][:, cols].bitcast(FP8X4),
-                        lhsT_scale=st[("es", g)][:, cols],
-                        rhs=vc[:, vcols].bitcast(FP8X4),
-                        rhs_scale=vs[:, vcols],
-                        start=(gg == 0),
-                        stop=(gg == 1),
-                    )
+                head_sum(g, h, o_ps[:, h, :])
             st[("o", g)] = o_ps
 
-        def reciprocal(g):
-            rinv = ring.tile([P, H], F32, tag="ri", bufs=3, name="rinv")
-            nc.vector.reciprocal(rinv[:], st[("rs", g)][:])
-            st[("ri", g)] = rinv
+        def last_sum(h):
+            o_ps = s_bank(F32, [P, HD], "o_last")
+            head_sum(NG - 1, h, o_ps[:])
+            st[("o", h, "last")] = o_ps
+
+        def reciprocal(g, heads=range(H)):
+            if heads[0] == 0:
+                st[("ri", g)] = ring.tile([P, H], F32, tag="ri", bufs=3, name="rinv")
+            cols = slice(heads[0], heads[-1] + 1)
+            nc.vector.reciprocal(st[("ri", g)][:, cols], st[("rs", g)][:, cols])
 
         def on_vector(g):
-            return g < NG - 1 and g % NORM_EVERY == NORM_EVERY - 1
+            return g % NORM_EVERY == NORM_EVERY - 1
 
         def normalise_on_vector(g):
             own = st[("o", g)][:].rearrange("p h f -> p (h f)")[:, HD - DIST:HD - DIST + H * (HD - DIST)]
-            o_n = ring.tile([P, H, DIST], F32, tag="on", bufs=2, name="o_n")
+            o_n = ring.tile([P, H, DIST], F32, tag="on", bufs=4, name="o_n")
             nc.vector.tensor_tensor(
                 out=o_n[:],
                 in0=own.rearrange("p (h f) -> p h f", h=H)[:, :, 0:DIST],
@@ -363,28 +370,29 @@ def tile_groupedqueryattention_pa_t_kernel(tc, xq, xk_rep, kv, mask, Wv, out):
 
         def normalise(g):
             own = st[("o", g)][:].rearrange("p h f -> p (h f)")[:, HD - DIST:HD - DIST + H * (HD - DIST)]
-            o_n = ring.tile([P, H, DIST], F32, tag="on", bufs=2, name="o_n")
+            o_n = ring.tile([P, H, DIST], F32, tag="on", bufs=4, name="o_n")
             for h in reversed(range(H)):
                 nc.scalar.activation(
                     out=o_n[:, h], in_=own[:, h * (HD - DIST):h * (HD - DIST) + DIST], func=ACT.Copy, scale=st[("ri", g)][:, h:h + 1]
                 )
             st[("on", g)] = o_n
 
-        def finish(g):
-            own = st[("o", g)][:].rearrange("p h f -> p (h f)")[:, HD - DIST:HD - DIST + H * (HD - DIST)]
-            qt, b = groups[g]
-            for h in range(H):
-                o_sb = ring.tile([P, DIST, REP], F32, tag="ofin", bufs=4, name="o_fin")
-                src = own[:, h * (HD - DIST):h * (HD - DIST) + DIST].unsqueeze(2).to_broadcast([P, DIST, REP])
-                if h % 2 == 0:
-                    nc.scalar.activation(out=o_sb[:], in_=src, func=ACT.Copy, scale=st[("ri", g)][:, h:h + 1])
-                else:
-                    nc.vector.tensor_scalar(out=o_sb[:], in0=src, scalar1=st[("ri", g)][:, h:h + 1], scalar2=None, op0=ALU.mult)
-                nc.sync.dma_start(
-                    out=out[b, qt * P:(qt + 1) * P, h * HD:(h + 1) * HD], in_=o_sb[:].rearrange("p j r -> p (j r)")
-                )
+        def finish(h, scale):
+            qt, b = groups[NG - 1]
+            o_sb = ring.tile([P, DIST, REP], F32, tag="ofin", bufs=4, name="o_fin")
+            own = st[("o", h, "last")][:, (H - 1 - h) * DIST:(H - h) * DIST]
+            scale(o_sb[:], own.unsqueeze(2).to_broadcast([P, DIST, REP]), st[("ri", NG - 1)][:, h:h + 1])
+            nc.sync.dma_start(
+                out=out[b, qt * P:(qt + 1) * P, h * HD:(h + 1) * HD], in_=o_sb[:].rearrange("p j r -> p (j r)")
+            )
 
-        def repeat(g):
+        def scale_on_scalar(o, i, s):
+            nc.scalar.activation(out=o, in_=i, func=ACT.Copy, scale=s)
+
+        def scale_on_vector(o, i, s):
+            nc.vector.tensor_scalar(out=o, in0=i, scalar1=s, scalar2=None, op0=ALU.mult)
+
+        def repeat(g, stores=1):
             qt, b = groups[g]
             o_sb = ring.tile([P, H * DIST, REP], F32, tag="osb", bufs=2, name="o_sb")
             n = H * DIST // REPEATS
@@ -397,7 +405,12 @@ def tile_groupedqueryattention_pa_t_kernel(tc, xq, xk_rep, kv, mask, Wv, out):
                     op0=ALU.mult,
                     op1=ALU.add,
                 )
-            nc.sync.dma_start(out=out[b, qt * P:(qt + 1) * P, :], in_=o_sb[:].rearrange("p j r -> p (j r)"))
+                if (i + 1) % (REPEATS // stores) == 0:
+                    cols = slice((i + 1 - REPEATS // stores) * n, (i + 1) * n)
+                    nc.sync.dma_start(
+                        out=out[b, qt * P:(qt + 1) * P, cols.start * REP:cols.stop * REP],
+                        in_=o_sb[:, cols].rearrange("p j r -> p (j r)"),
+                    )
 
         load_mask(0)
         load_xk(0)
@@ -482,8 +495,7 @@ def tile_groupedqueryattention_pa_t_kernel(tc, xq, xk_rep, kv, mask, Wv, out):
             extra(xv_tick(c), xv_matmul, xv_leave, c)
 
         def exp_at(pair):
-            u = 2 * pair + 1
-            return u + EXP_LAG_LAST + (EXP_LAG_FIRST - EXP_LAG_LAST) * (NU - 1 - u) // NU
+            return 2 * pair + 1 + EXP_LAG
 
         def tr_at(pair):
             return exp_at(pair) + TR_AFTER_EXP
@@ -491,12 +503,12 @@ def tile_groupedqueryattention_pa_t_kernel(tc, xq, xk_rep, kv, mask, Wv, out):
         def regroup_at(pair):
             return tr_at(pair) + REGROUP_AFTER_TR
 
-        def quant_at(pair):
-            return regroup_at(pair) + QUANT_AFTER_REGROUP
+        def quant_at(g):
+            return regroup_at(H // 2 * g + H // 2 - 1) + QUANT_AFTER_REGROUP
 
         def pv_at(g):
             values_at = xv_tick(2 * groups[g][1] + 1) + 1
-            return max(quant_at(H // 2 * g + H // 2 - 1) + PV_AFTER_QUANT, values_at + 1)
+            return max(quant_at(g) + PV_AFTER_QUANT, values_at + 1)
 
         def by_tick(at, n):
             table = {}
@@ -513,10 +525,10 @@ def tile_groupedqueryattention_pa_t_kernel(tc, xq, xk_rep, kv, mask, Wv, out):
         exp_in = by_tick(exp_at, NU // 2)
         tr_in = by_tick(tr_at, NU // 2)
         regroup_in = by_tick(regroup_at, NU // 2)
-        quant_in = by_tick(quant_at, NU // 2)
+        quant_in = by_tick(quant_at, NG)
         pv_in = by_tick(pv_at, NG)
 
-        for tk in range(pv_at(NG - 1) + NORM_AFTER_PV + 1):
+        for tk in range(NU):
             for n in range(2, NQ):
                 if tk == 2 * H * n - 10:
                     load_xq(n)
@@ -530,23 +542,20 @@ def tile_groupedqueryattention_pa_t_kernel(tc, xq, xk_rep, kv, mask, Wv, out):
             for pair in exp_in.get(tk, []):
                 exponent(2 * pair + 1)
                 exponent(2 * pair)
-            if tk < NU:
-                for pair in regroup_in.get(tk, []):
-                    regroup(2 * pair + 1, nc.scalar.copy)
-                    regroup(2 * pair, nc.scalar.copy)
+            for pair in regroup_in.get(tk, []):
+                regroup(2 * pair + 1, nc.scalar.copy)
+                regroup(2 * pair, nc.scalar.copy)
             if tk - 1 in kv_in:
                 kv_leave(*kv_in[tk - 1])
             for g in pv_in.get(tk - NORM_AFTER_PV, []):
-                if g == NG - 1:
-                    finish(g)
-                elif not on_vector(g):
+                if not on_vector(g):
                     normalise(g)
             for pair in tr_in.get(tk, []):
-                for u in (2 * pair + 1, 2 * pair) if pair == NU // 2 - 1 else (2 * pair, 2 * pair + 1):
-                    transposes(u)
+                transposes(2 * pair)
+                transposes(2 * pair + 1)
             if tk in kv_in:
                 kv_transpose(*kv_in[tk])
-            if H <= tk < NU:
+            if tk >= H:
                 penalties(tk, 0)
                 penalties(tk, 1)
                 scores(tk, 1)
@@ -563,16 +572,11 @@ def tile_groupedqueryattention_pa_t_kernel(tc, xq, xk_rep, kv, mask, Wv, out):
             for g in pv_in.get(tk - 1, []):
                 if on_vector(g):
                     normalise_on_vector(g)
-            if tk >= NU:
-                for pair in regroup_in.get(tk, []):
-                    last = pair == NU // 2 - 1
-                    regroup(2 * pair + 1, nc.vector.tensor_copy)
-                    regroup(2 * pair, nc.scalar.copy if last else nc.vector.tensor_copy)
-            if H <= tk < NU:
+            if tk >= H:
                 leave_psum(tk, 0)
-            for u in quant_in.get(tk, []):
-                quantise(u)
-            if H <= tk < NU:
+            for g in quant_in.get(tk, []):
+                quantise(g)
+            if tk >= H:
                 leave_psum(tk, 1)
                 row_min(tk)
             for c in range(4):
@@ -590,5 +594,55 @@ def tile_groupedqueryattention_pa_t_kernel(tc, xq, xk_rep, kv, mask, Wv, out):
             for g in pv_in.get(tk + 1, []):
                 reciprocal(g)
             for g in pv_in.get(tk - NORM_AFTER_PV, []):
-                if g < NG - 1:
-                    repeat(g)
+                repeat(g)
+
+        a = NU - 8
+        on_v = nc.vector.tensor_copy
+        transposes(a)
+        transposes(a + 1)
+        exponent(a + 3)
+        exponent(a + 2)
+        quantise(NG - 3)
+        normalise(NG - 4)
+        repeat(NG - 4)
+        regroup(a + 1, on_v)
+        regroup(a, on_v)
+        transposes(a + 2)
+        transposes(a + 3)
+        reciprocal(NG - 3)
+        weighted_sum(NG - 3)
+        exponent(a + 5)
+        exponent(a + 4)
+        regroup(a + 3, on_v)
+        regroup(a + 2, on_v)
+        quantise(NG - 2)
+        normalise_on_vector(NG - 3)
+        repeat(NG - 3)
+        transposes(a + 4)
+        transposes(a + 5)
+        exponent(a + 7)
+        exponent(a + 6)
+        transposes(a + 7)
+        transposes(a + 6)
+        weighted_sum(NG - 2)
+        regroup(a + 5, on_v)
+        reciprocal(NG - 2)
+        reciprocal(NG - 1, range(0, 2))
+        regroup(a + 4, nc.scalar.copy)
+        quantise(NG - 1, range(0, 2))
+        regroup(a + 7, nc.scalar.copy)
+        quantise(NG - 1, range(3, 4))
+        regroup(a + 6, nc.scalar.copy, slice(0, 1))
+        regroup(a + 6, on_v, slice(1, 2))
+        quantise(NG - 1, range(2, 3))
+        reciprocal(NG - 1, range(2, 4))
+        last_sum(0)
+        last_sum(1)
+        last_sum(3)
+        last_sum(2)
+        normalise(NG - 2)
+        repeat(NG - 2, 2)
+        finish(0, scale_on_scalar)
+        finish(1, scale_on_scalar)
+        finish(3, scale_on_scalar)
+        finish(2, scale_on_vector)

@@ -24,7 +24,6 @@ SCALE = 1.0 / math.sqrt(HD)
 ROOT = math.sqrt(HD)
 FLOPS = 2 * B * SKV * DIN * HD + 2 * 2 * B * H * SQ * SKV * HD
 
-NORM_EVERY = 2
 KV_ON_S = 2
 XK_BEHIND = 4
 KV0_BEHIND = 7
@@ -354,10 +353,7 @@ def tile_groupedqueryattention_pa_t_kernel(tc, xq, xk_rep, kv, mask, Wv, out):
             cols = slice(heads[0], heads[-1] + 1)
             nc.vector.reciprocal(st[("ri", g)][:, cols], st[("rs", g)][:, cols])
 
-        def on_vector(g):
-            return g % NORM_EVERY == NORM_EVERY - 1
-
-        def normalise_on_vector(g):
+        def normalise(g):
             own = st[("o", g)][:].rearrange("p h f -> p (h f)")[:, HD - DIST:HD - DIST + H * (HD - DIST)]
             o_n = ring.tile([P, H, DIST], F32, tag="on", bufs=4, name="o_n")
             nc.vector.tensor_tensor(
@@ -368,7 +364,7 @@ def tile_groupedqueryattention_pa_t_kernel(tc, xq, xk_rep, kv, mask, Wv, out):
             )
             st[("on", g)] = o_n
 
-        def normalise(g):
+        def normalise_on_scalar(g):
             own = st[("o", g)][:].rearrange("p h f -> p (h f)")[:, HD - DIST:HD - DIST + H * (HD - DIST)]
             o_n = ring.tile([P, H, DIST], F32, tag="on", bufs=4, name="o_n")
             for h in reversed(range(H)):
@@ -547,9 +543,6 @@ def tile_groupedqueryattention_pa_t_kernel(tc, xq, xk_rep, kv, mask, Wv, out):
                 regroup(2 * pair, nc.scalar.copy)
             if tk - 1 in kv_in:
                 kv_leave(*kv_in[tk - 1])
-            for g in pv_in.get(tk - NORM_AFTER_PV, []):
-                if not on_vector(g):
-                    normalise(g)
             for pair in tr_in.get(tk, []):
                 transposes(2 * pair)
                 transposes(2 * pair + 1)
@@ -569,11 +562,10 @@ def tile_groupedqueryattention_pa_t_kernel(tc, xq, xk_rep, kv, mask, Wv, out):
             for qt in range(2, NQT):
                 if tk == first_use[qt] - SQUARE_LAG:
                     square(qt, nc.gpsimd)
-            for g in pv_in.get(tk - 1, []):
-                if on_vector(g):
-                    normalise_on_vector(g)
             if tk >= H:
                 leave_psum(tk, 0)
+            for g in pv_in.get(tk - 1, []):
+                normalise(g)
             for g in quant_in.get(tk, []):
                 quantise(g)
             if tk >= H:
@@ -603,7 +595,7 @@ def tile_groupedqueryattention_pa_t_kernel(tc, xq, xk_rep, kv, mask, Wv, out):
         exponent(a + 3)
         exponent(a + 2)
         quantise(NG - 3)
-        normalise(NG - 4)
+        normalise_on_scalar(NG - 4)
         repeat(NG - 4)
         regroup(a + 1, on_v)
         regroup(a, on_v)
@@ -616,7 +608,7 @@ def tile_groupedqueryattention_pa_t_kernel(tc, xq, xk_rep, kv, mask, Wv, out):
         regroup(a + 3, on_v)
         regroup(a + 2, on_v)
         quantise(NG - 2)
-        normalise_on_vector(NG - 3)
+        normalise(NG - 3)
         repeat(NG - 3)
         transposes(a + 4)
         transposes(a + 5)
@@ -640,7 +632,7 @@ def tile_groupedqueryattention_pa_t_kernel(tc, xq, xk_rep, kv, mask, Wv, out):
         last_sum(1)
         last_sum(3)
         last_sum(2)
-        normalise(NG - 2)
+        normalise_on_scalar(NG - 2)
         repeat(NG - 2, 2)
         finish(0, scale_on_scalar)
         finish(1, scale_on_scalar)

@@ -41,8 +41,7 @@ T_BUFS = EXP_LAG + 2
 WARM_UNITS = 4
 SEEDS_FIRST = 12
 SQUARE_LAG = 6
-SQUARES = 4
-REPEATS = 2
+SQUARES = 2
 XK_AT = 10
 KT_AT = 24
 KT_STEP = 8
@@ -388,25 +387,24 @@ def tile_groupedqueryattention_pa_t_kernel(tc, xq, xk_rep, kv, mask, Wv, out):
         def scale_on_vector(o, i, s):
             nc.vector.tensor_scalar(out=o, in0=i, scalar1=s, scalar2=None, op0=ALU.mult)
 
-        def repeat(g, stores=1):
+        def repeat(g, pieces=1):
             qt, b = groups[g]
             o_sb = ring.tile([P, H * DIST, REP], F32, tag="osb", bufs=2, name="o_sb")
-            n = H * DIST // REPEATS
-            for i in range(REPEATS):
+            n = H * DIST // pieces
+            for i in range(pieces):
+                cols = slice(i * n, (i + 1) * n)
                 nc.gpsimd.tensor_scalar(
-                    out=o_sb[:, i * n:(i + 1) * n],
-                    in0=st[("on", g)][:].rearrange("p h j -> p (h j)")[:, i * n:(i + 1) * n].unsqueeze(2).to_broadcast([P, n, REP]),
+                    out=o_sb[:, cols],
+                    in0=st[("on", g)][:].rearrange("p h j -> p (h j)")[:, cols].unsqueeze(2).to_broadcast([P, n, REP]),
                     scalar1=1.0,
                     scalar2=0.0,
                     op0=ALU.mult,
                     op1=ALU.add,
                 )
-                if (i + 1) % (REPEATS // stores) == 0:
-                    cols = slice((i + 1 - REPEATS // stores) * n, (i + 1) * n)
-                    nc.sync.dma_start(
-                        out=out[b, qt * P:(qt + 1) * P, cols.start * REP:cols.stop * REP],
-                        in_=o_sb[:, cols].rearrange("p j r -> p (j r)"),
-                    )
+                nc.sync.dma_start(
+                    out=out[b, qt * P:(qt + 1) * P, i * n * REP:(i + 1) * n * REP],
+                    in_=o_sb[:, cols].rearrange("p j r -> p (j r)"),
+                )
 
         load_mask(0)
         load_xk(0)

@@ -38,7 +38,7 @@ QUANT_AFTER_REGROUP = 2
 PV_AFTER_QUANT = 2
 NORM_AFTER_PV = 2
 T_BUFS = EXP_LAG + 2
-WARM_UNITS = 4
+WARM_UNITS = 8
 SEEDS_FIRST = 12
 SQUARE_LAG = 6
 SQUARES = 2
@@ -424,7 +424,9 @@ def tile_groupedqueryattention_pa_t_kernel(tc, xq, xk_rep, kv, mask, Wv, out):
         seed(0)
         warm(w_ps, 2)
         kT_transposes(0, 0, 0)
+        warm(w_ps, 2)
         seed(1)
+        warm(w_ps, 0)
         qT_transposes(0)
         kT_transposes(0, 1, 0)
         seed(2)
@@ -439,8 +441,11 @@ def tile_groupedqueryattention_pa_t_kernel(tc, xq, xk_rep, kv, mask, Wv, out):
             leave_psum(u, 0)
             seed(3 + u)
         square(1, nc.gpsimd)
+        w_ps = s_bank(F32, [P, 512], "w_ps")
         kT_transposes(0, 0, 1)
+        warm(w_ps, 1)
         kT_transposes(0, 1, 1)
+        warm(w_ps, 1)
         kT_leave(0, 0, 1)
         kT_leave(0, 1, 1)
         seed(7)

from contextlib import ExitStack
import math

import concourse.bass as bass
import concourse.mybir as mybir
import concourse.tile as tile
from concourse.masks import make_identity

F32 = mybir.dt.float32
BF16 = mybir.dt.bfloat16
U32 = mybir.dt.uint32
U8 = mybir.dt.uint8
FP8X4 = mybir.dt.float8_e4m3fn_x4
ALU = mybir.AluOpType
ACT = mybir.ActivationFunctionType

B, SQ, SKV, DIN, H, HD = 2, 2048, 1024, 1024, 4, 128
P = 128
NQT = SQ // P
NKT = SKV // P
REP = 4
DIST = HD // REP
SCALE = 1.0 / math.sqrt(HD)
ROOT = math.sqrt(HD)
FLOPS = 2 * B * SKV * DIN * HD + 2 * 2 * B * H * SQ * SKV * HD

KV_ON_S = 2
XK_BEHIND = 4
KV0_BEHIND = 7
MASK_BUFS = 8
S_BANKS = 5
ET_BANKS = 3
EXP_LAG = 6
TAIL = 8
TR_AFTER_EXP = 1
REGROUP_AFTER_TR = 1
QUANT_AFTER_REGROUP = 2
PV_AFTER_QUANT = 2
NORM_AFTER_PV = 2
T_BUFS = EXP_LAG + 2
WARM_UNITS = 8
SEEDS_FIRST = 12
SQUARE_LAG = 6
SQUARES = 2
XK_AT = 10
KT_AT = 24
KT_STEP = 8
KV_AT = (4, 6, 18, 38)
KV_STEP = 4
KV_A_TICK = 2


def tile_groupedqueryattention_pa_t_kernel(tc, xq, xk_rep, kv, mask, Wv, out):
    nc = tc.nc
    with ExitStack() as ctx:
        keep = ctx.enter_context(tc.tile_pool(name="keep", bufs=1))
        ring = ctx.enter_context(tc.tile_pool(name="ring", bufs=2))
        psum = ctx.enter_context(tc.psum_pool(name="psum", bufs=1))
        ctx.enter_context(tc.manual_schedule())

        mask_v = mask.rearrange("a c (t p) k -> p (a c t) k", p=P)
        xq_v = xq.rearrange("b (t p) c -> p b t c", p=P)
        xk_v = xk_rep.rearrange("b (w p e) c -> p b w e c", p=P, e=2)
        kv_v = kv.rearrange("b (g u q i h) c -> h q b g u i c", g=2, u=2, i=2, h=2)

        ident_bf = keep.tile([P, P], BF16, name="ident_bf")
        make_identity(nc, ident_bf[:])
        ident_f = keep.tile([P, P], F32, name="ident_f")
        make_identity(nc, ident_f[:])

        yT = keep.tile([P, NQT, NKT, P], F32, name="yT")
        kT = keep.tile([P, B, H, SKV], BF16, name="kT")

        st = {}

        def et_bank(dtype, shape, name):
            return psum.tile(shape, dtype, tag="et", bufs=ET_BANKS, name=name)

        def s_bank(dtype, shape, name):
            return psum.tile(shape, dtype, tag="s", bufs=S_BANKS, name=name)

        def load_mask(qt):
            m_sb = ring.tile([P, SKV], BF16, tag="mraw", bufs=MASK_BUFS, name="m_sb")
            nc.sync.dma_start(out=m_sb[:], in_=mask_v[:, qt, :])
            st[("mraw", qt)] = m_sb

        def load_xk(b):
            xk_sb = ring.tile([P, NKT, H * HD], BF16, tag="xk", bufs=1, name="xk_sb")
            st[("xk", b)] = xk_sb

        def load_xk_half(b, i):
            half = st[("xk", b)][:, 4 * i:4 * i + 4, :]
            nc.sync.dma_start(out=half.rearrange("p (w e) c -> p w e c", e=2), in_=xk_v[:, b, 2 * i:2 * i + 2])

        def load_xq(n):
            b, tp = divmod(n, NQT // 2)
            xq_sb = ring.tile([P, 2, H * HD], BF16, tag="xq", bufs=2, name="xq_sb")
            nc.sync.dma_start(out=xq_sb[:], in_=xq_v[:, b, 2 * tp:2 * tp + 2, :])
            st[("xq", n)] = xq_sb

        def seed(qt):
            m_sb = st[("mraw", qt)]
            ps = et_bank(F32, [P, NKT // 2, P], "mt_ps")
            words = m_sb[:].bitcast(F32)
            for w in range(NKT // 2):
                nc.tensor.transpose(ps[:, w, :], words[:, w * P:(w + 1) * P], ident_f[:])
            nc.scalar.activation(
                out=yT[:, qt].rearrange("p (w e) q -> p w e q", e=2),
                in_=ps[:].rearrange("p w q -> p (w q)").bitcast(BF16).rearrange("p (w q e) -> p w e q", e=2, q=P),
                func=ACT.Abs_reciprocal_sqrt,
                scale=1.0 / ROOT,
            )
            if qt + MASK_BUFS < NQT:
                load_mask(qt + MASK_BUFS)

        def warm(ps, n):
            for i in range(n):
                nc.tensor.matmul(ps[:], lhsT=ident_bf[:], rhs=zeros[:], start=True, stop=True)

        def square(qt, eng):
            for i in range(SQUARES):
                y = yT[:, qt, NKT // SQUARES * i:NKT // SQUARES * (i + 1), :]
                eng.tensor_tensor(out=y, in0=y, in1=y, op=ALU.mult)

        def kT_transposes(b, hp, i):
            ps = s_bank(BF16, [P, 2, NKT // 2, P], "kt_ps")
            for h in range(2):
                for j in range(NKT // 2):
                    nc.tensor.transpose(
                        ps[:, h, j, :],
                        st[("xk", b)][:, NKT // 2 * i + j, (2 * hp + h) * HD:(2 * hp + h + 1) * HD],
                        ident_bf[:],
                    )
            st[("ktps", b, hp, i)] = ps

        def kT_leave(b, hp, i):
            nc.vector.tensor_scalar(
                out=kT[:, b, 2 * hp:2 * hp + 2, i * 512:(i + 1) * 512],
                in0=st[("ktps", b, hp, i)][:].rearrange("p h j k -> p h (j k)"),
                scalar1=-1.0,
                scalar2=None,
                op0=ALU.mult,
            )

        def qT_transposes(n):
            ps = s_bank(BF16, [P, 2 * H, P], "qt_ps")
            for t in range(2):
                for h in range(H):
                    nc.tensor.transpose(ps[:, t * H + h, :], st[("xq", n)][:, t, h * HD:(h + 1) * HD], ident_bf[:])
            st[("qtps", n)] = ps

        def qT_leave(n):
            qT = ring.tile([P, 2 * H, P], BF16, tag="qT", bufs=2, name="qT")
            nc.vector.tensor_copy(out=qT[:], in_=st[("qtps", n)][:])
            st[("qT", n)] = qT

        wv_raw = keep.tile([P, 2, 2, 2, HD], BF16, name="wv_raw")
        wv_grp = keep.tile([P, 2, HD, 4], BF16, name="wv_grp", align_bytes=64)
        wv_codes = keep.tile([P, 2 * HD], U32, name="wv_codes", align_bytes=64)
        wv_scales = keep.tile([P, 2 * HD], U8, name="wv_scales", align_bytes=64)

        def wv_load():
            nc.sync.dma_start(out=wv_raw[:], in_=Wv.rearrange("(g u p e) f -> p g u e f", g=2, u=2, e=2))

        def wv_regroup():
            for h in range(H):
                nc.vector.tensor_copy(
                    out=wv_grp[:, :, (H - 1 - h) * DIST:(H - h) * DIST, :],
                    in_=wv_raw[:, :, :, :, h * DIST:(h + 1) * DIST].rearrange("p g u e f -> p g f (u e)"),
                )

        def wv_quantise():
            nc.vector.quantize_mx(
                out=wv_codes[:].bitcast(FP8X4),
                scales=wv_scales[:],
                in_=wv_grp[:].rearrange("p g f t -> p (g f t)"),
            )

        def kv_load(c):
            kv_sb = ring.tile([P, 4, DIN], BF16, tag="kv", bufs=2, name="kv_sb")
            for h in range(2):
                for u in range(2):
                    nc.sync.dma_start(
                        out=kv_sb[h * P // 2:(h + 1) * P // 2, 2 * u:2 * u + 2, :], in_=kv_v[h, :, c // 2, c % 2, u]
                    )
            st[("kv", c)] = kv_sb

        def kv_transpose(c, t):
            xt = s_bank(F32, [P, 4, P], "xt") if c < KV_ON_S else et_bank(F32, [P, 4, P], "xt")
            kw = st[("kv", c)][:, t, :].bitcast(F32)
            for w in range(4):
                nc.tensor.transpose(xt[:, w, :], kw[:, w * P:(w + 1) * P], ident_f[:])
            st[("xt", c, t)] = xt

        def kv_leave(c, t):
            if t == 0:
                st[("kvg", c)] = ring.tile([P, 4 * 1024], BF16, tag="kvg", bufs=1, name="kv_grp", align_bytes=64)
            grp_w = st[("kvg", c)][:].bitcast(F32).rearrange("p (t g k u) -> p t g k u", t=4, g=2, u=2)
            copy = nc.vector.tensor_copy if c < KV_ON_S else nc.scalar.copy
            copy(out=grp_w[:, t], in_=st[("xt", c, t)][:].rearrange("p (g u) k -> p g k u", u=2))

        def kv_quantise(c):
            kv_codes = ring.tile([P, 1024], U32, tag="kvc", bufs=1, name="kv_codes", align_bytes=64)
            kv_scales = ring.tile([P, 1024], U8, tag="kvs", bufs=1, name="kv_scales", align_bytes=64)
            nc.vector.quantize_mx(out=kv_codes[:].bitcast(FP8X4), scales=kv_scales[:], in_=st[("kvg", c)][:])
            st[("kvc", c)] = (kv_codes, kv_scales)

        def xv_matmul(c):
            kv_codes, kv_scales = st[("kvc", c)]
            xv_ps = s_bank(F32, [P, 4, HD], "xv_ps")
            for t in range(4):
                for gg in range(2):
                    cols = slice((t * 2 + gg) * P, (t * 2 + gg + 1) * P)
                    wcols = slice(gg * HD, (gg + 1) * HD)
                    nc.tensor.matmul_mx(
                        out=xv_ps[:, t, :],
                        lhsT=kv_codes[:, cols].bitcast(FP8X4),
                        lhsT_scale=kv_scales[:, cols],
                        rhs=wv_codes[:, wcols].bitcast(FP8X4),
                        rhs_scale=wv_scales[:, wcols],
                        start=(gg == 0),
                        stop=(gg == 1),
                    )
            st[("xv", c)] = xv_ps

        def xv_leave(c):
            if c % 2 == 0:
                st[("vg", c // 2)] = ring.tile([P, 2, HD, 4], BF16, tag="vg", bufs=1, name="v_grp", align_bytes=64)
            nc.vector.tensor_copy(out=st[("vg", c // 2)][:, c % 2], in_=st[("xv", c)][:].rearrange("p t f -> p f t"))

        def v_quantise(b):
            vc = keep.tile([P, 2 * HD], U32, name="v_codes%d" % b, align_bytes=64)
            vs = keep.tile([P, 2 * HD], U8, name="v_scales%d" % b, align_bytes=64)
            nc.vector.quantize_mx(
                out=vc[:].bitcast(FP8X4), scales=vs[:], in_=st[("vg", b)][:].rearrange("p g f t -> p (g f t)")
            )
            st[("v", b)] = (vc, vs)

        groups = [(qt, b) for b in range(B) for qt in range(NQT)]
        units = [(qt, b, h) for (qt, b) in groups for h in range(H)]
        NU = len(units)
        NG = len(groups)

        def penalties(u, c):
            qt, b, h = units[u]
            s_ps = s_bank(F32, [P, 512], "s_ps")
            if u < WARM_UNITS:
                warm(s_ps, 1)
            for jj in range(4):
                nc.tensor.matmul(
                    s_ps[:, jj * P:(jj + 1) * P], lhsT=yT[:, qt, 4 * c + jj, :], rhs=ident_f[:],
                    is_transpose=True, start=(jj == 0), stop=False,
                )
            st[("s", u, c)] = s_ps

        def scores(u, c):
            qt, b, h = units[u]
            nc.tensor.matmul(
                st[("s", u, c)][:], lhsT=st[("qT", u // (2 * H))][:, u % (2 * H), :], rhs=kT[:, b, h, c * 512:(c + 1) * 512],
                start=False, stop=True,
            )

        def leave_psum(u, c):
            if c == 0:
                st[("t", u)] = ring.tile([P, SKV], F32, tag="t", bufs=T_BUFS, name="t")
                st[("mm", u)] = ring.tile([P, 2], F32, tag="mm", bufs=T_BUFS, name="mm")
            nc.vector.tensor_scalar(
                out=st[("t", u)][:, c * 512:(c + 1) * 512],
                in0=st[("s", u, c)][:],
                scalar1=SCALE,
                scalar2=None,
                op0=ALU.mult,
                op1=ALU.min,
                accum_out=st[("mm", u)][:, c:c + 1],
            )

        def row_min(u):
            m = ring.tile([P, 1], F32, tag="m", bufs=T_BUFS, name="m")
            mm = st[("mm", u)]
            nc.gpsimd.tensor_scalar(
                out=m[:], in0=mm[:, 0:1], scalar1=mm[:, 1:2], scalar2=0.0, op0=ALU.min, op1=ALU.add
            )
            st[("m", u)] = m

        def exponent(u):
            h = u % H
            g = u // H
            if h == 1:
                st[("rs", g)] = ring.tile([P, H], F32, tag="rs", bufs=6, name="rowsum")
            e = ring.tile([P, SKV], BF16, tag="e", bufs=6, name="e")
            nc.scalar.activation(
                out=e[:], in_=st[("t", u)][:], func=ACT.Exp, bias=st[("m", u)][:, 0:1], scale=-1.0,
                accum_out=st[("rs", g)][:, h:h + 1],
            )
            st[("e", u)] = e

        def transposes(u):
            e = st[("e", u)]
            et_ps = (et_bank if u < NU - TAIL else s_bank)(F32, [P, 4, P], "et_ps")
            ew = e[:].bitcast(F32)
            for w in range(4):
                nc.tensor.transpose(et_ps[:, w, :], ew[:, w * P:(w + 1) * P], ident_f[:])
            st[("et", u)] = et_ps

        def regroup(u, copy, halves=slice(0, 2)):
            if u % H == 1:
                st[("etg", u // H)] = ring.tile([P, H, 2 * P * 4], BF16, tag="etg", bufs=2, name="et_grp", align_bytes=64)
            src = st[("et", u)][:].rearrange("p (g u) q -> p g q u", u=2)[:, halves]
            dst = st[("etg", u // H)][:, u % H, :].bitcast(F32).rearrange("p (g q u) -> p g q u", g=2, u=2)[:, halves]
            copy(out=dst, in_=src)

        def quantise(g, heads=range(H)):
            if heads[0] == 0:
                st[("ec", g)] = ring.tile([P, H * 2 * P], U32, tag="ec", bufs=2, name="e_codes", align_bytes=64)
                st[("es", g)] = ring.tile([P, H * 2 * P], U8, tag="es", bufs=2, name="e_scales", align_bytes=64)
            cols = slice(heads[0] * 2 * P, (heads[-1] + 1) * 2 * P)
            nc.vector.quantize_mx(
                out=st[("ec", g)][:, cols].bitcast(FP8X4),
                scales=st[("es", g)][:, cols],
                in_=st[("etg", g)][:, heads[0]:heads[-1] + 1, :].rearrange("p k x -> p (k x)"),
            )

        def head_sum(g, h, o):
            vc, vs = st[("v", groups[g][1])]
            for gg in range(2):
                cols = slice((h * 2 + gg) * P, (h * 2 + gg + 1) * P)
                vcols = slice(gg * HD, (gg + 1) * HD)
                nc.tensor.matmul_mx(
                    out=o,
                    lhsT=st[("ec", g)][:, cols].bitcast(FP8X4),
                    lhsT_scale=st[("es", g)][:, cols],
                    rhs=vc[:, vcols].bitcast(FP8X4),
                    rhs_scale=vs[:, vcols],
                    start=(gg == 0),
                    stop=(gg == 1),
                )

        def weighted_sum(g):
            o_ps = et_bank(F32, [P, H, HD], "o_ps")
            for h in range(H):
                head_sum(g, h, o_ps[:, h, :])
            st[("o", g)] = o_ps

        def last_sum(h):
            o_ps = s_bank(F32, [P, HD], "o_last")
            head_sum(NG - 1, h, o_ps[:])
            st[("o", h, "last")] = o_ps

        def reciprocal(g, heads=range(H)):
            if heads[0] == 0:
                st[("ri", g)] = ring.tile([P, H], F32, tag="ri", bufs=3, name="rinv")
            cols = slice(heads[0], heads[-1] + 1)
            nc.vector.reciprocal(st[("ri", g)][:, cols], st[("rs", g)][:, cols])

        def normalise(g):
            own = st[("o", g)][:].rearrange("p h f -> p (h f)")[:, HD - DIST:HD - DIST + H * (HD - DIST)]
            o_n = ring.tile([P, H, DIST], F32, tag="on", bufs=4, name="o_n")
            nc.vector.tensor_tensor(
                out=o_n[:],
                in0=own.rearrange("p (h f) -> p h f", h=H)[:, :, 0:DIST],
                in1=st[("ri", g)][:].unsqueeze(2).to_broadcast([P, H, DIST]),
                op=ALU.mult,
            )
            st[("on", g)] = o_n

        def normalise_on_scalar(g):
            own = st[("o", g)][:].rearrange("p h f -> p (h f)")[:, HD - DIST:HD - DIST + H * (HD - DIST)]
            o_n = ring.tile([P, H, DIST], F32, tag="on", bufs=4, name="o_n")
            for h in reversed(range(H)):
                nc.scalar.activation(
                    out=o_n[:, h], in_=own[:, h * (HD - DIST):h * (HD - DIST) + DIST], func=ACT.Copy, scale=st[("ri", g)][:, h:h + 1]
                )
            st[("on", g)] = o_n

        def finish(h, scale):
            qt, b = groups[NG - 1]
            o_sb = ring.tile([P, DIST, REP], F32, tag="ofin", bufs=4, name="o_fin")
            own = st[("o", h, "last")][:, (H - 1 - h) * DIST:(H - h) * DIST]
            scale(o_sb[:], own.unsqueeze(2).to_broadcast([P, DIST, REP]), st[("ri", NG - 1)][:, h:h + 1])
            nc.sync.dma_start(
                out=out[b, qt * P:(qt + 1) * P, h * HD:(h + 1) * HD], in_=o_sb[:].rearrange("p j r -> p (j r)")
            )

        def scale_on_scalar(o, i, s):
            nc.scalar.activation(out=o, in_=i, func=ACT.Copy, scale=s)

        def scale_on_vector(o, i, s):
            nc.vector.tensor_scalar(out=o, in0=i, scalar1=s, scalar2=None, op0=ALU.mult)

        def repeat(g, pieces=1):
            qt, b = groups[g]
            o_sb = ring.tile([P, H * DIST, REP], F32, tag="osb", bufs=2, name="o_sb")
            n = H * DIST // pieces
            for i in range(pieces):
                cols = slice(i * n, (i + 1) * n)
                nc.gpsimd.tensor_scalar(
                    out=o_sb[:, cols],
                    in0=st[("on", g)][:].rearrange("p h j -> p (h j)")[:, cols].unsqueeze(2).to_broadcast([P, n, REP]),
                    scalar1=1.0,
                    scalar2=0.0,
                    op0=ALU.mult,
                    op1=ALU.add,
                )
                nc.sync.dma_start(
                    out=out[b, qt * P:(qt + 1) * P, i * n * REP:(i + 1) * n * REP],
                    in_=o_sb[:, cols].rearrange("p j r -> p (j r)"),
                )

        load_mask(0)
        load_xk(0)
        load_xk_half(0, 0)
        load_mask(1)
        load_xq(0)
        for qt in range(2, MASK_BUFS):
            load_mask(qt)
            if qt == XK_BEHIND:
                load_xk_half(0, 1)
            if qt == KV0_BEHIND:
                kv_load(0)
        zeros = keep.tile([P, 512], BF16, name="zeros")
        nc.vector.memset(zeros[:], 0.0)
        w_ps = s_bank(F32, [P, 512], "w_ps")
        warm(w_ps, 5)
        seed(0)
        warm(w_ps, 2)
        kT_transposes(0, 0, 0)
        warm(w_ps, 2)
        seed(1)
        warm(w_ps, 0)
        qT_transposes(0)
        kT_transposes(0, 1, 0)
        seed(2)
        warm(w_ps, 2)
        square(0, nc.vector)
        kT_leave(0, 0, 0)
        qT_leave(0)
        kT_leave(0, 1, 0)
        for u in range(H):
            penalties(u, 0)
            scores(u, 0)
            leave_psum(u, 0)
            seed(3 + u)
        square(1, nc.gpsimd)
        w_ps = s_bank(F32, [P, 512], "w_ps")
        kT_transposes(0, 0, 1)
        warm(w_ps, 1)
        kT_transposes(0, 1, 1)
        warm(w_ps, 1)
        kT_leave(0, 0, 1)
        kT_leave(0, 1, 1)
        seed(7)
        for u in range(H):
            penalties(u, 1)
            scores(u, 1)
            leave_psum(u, 1)
            row_min(u)
            seed(8 + u)
        load_xq(1)
        wv_load()
        kv_load(1)

        def kv_tick(c, t):
            return KV_AT[c] + (t // KV_A_TICK if c < KV_ON_S else KV_STEP * t)

        def kvq_tick(c):
            return kv_tick(c, 3) + (1 if c < KV_ON_S else 2)

        def xv_tick(c):
            return kvq_tick(c) + 4

        NQ = B * NQT // 2

        first_use = {}
        for u in range(NU):
            if units[u][0] not in first_use:
                first_use[units[u][0]] = u

        extras = {}
        kv_in = {}

        def extra(tick, fill, leave, *args):
            extras.setdefault(tick, []).append((lambda: fill(*args), lambda: leave(*args)))

        for n in range(4):
            extra(KT_AT + KT_STEP * n, kT_transposes, kT_leave, 1, n // 2, n % 2)
        for n in range(1, NQ):
            extra(2 * H * n - 4, qT_transposes, qT_leave, n)
        for c in range(4):
            for t in range(4):
                if c < KV_ON_S:
                    extra(kv_tick(c, t), kv_transpose, kv_leave, c, t)
                else:
                    kv_in[kv_tick(c, t)] = (c, t)
            extra(xv_tick(c), xv_matmul, xv_leave, c)

        def exp_at(pair):
            return 2 * pair + 1 + EXP_LAG

        def tr_at(pair):
            return exp_at(pair) + TR_AFTER_EXP

        def regroup_at(pair):
            return tr_at(pair) + REGROUP_AFTER_TR

        def quant_at(g):
            return regroup_at(H // 2 * g + H // 2 - 1) + QUANT_AFTER_REGROUP

        def pv_at(g):
            values_at = xv_tick(2 * groups[g][1] + 1) + 1
            return max(quant_at(g) + PV_AFTER_QUANT, values_at + 1)

        def by_tick(at, n):
            table = {}
            for i in range(n):
                table.setdefault(at(i), []).append(i)
            return table

        def seed_at(i):
            return H + i // 2

        seed_in = {}
        for qt in range(SEEDS_FIRST, NQT):
            seed_in.setdefault(seed_at(qt - SEEDS_FIRST), []).append(qt)
        exp_in = by_tick(exp_at, NU // 2)
        tr_in = by_tick(tr_at, NU // 2)
        regroup_in = by_tick(regroup_at, NU // 2)
        quant_in = by_tick(quant_at, NG)
        pv_in = by_tick(pv_at, NG)

        for tk in range(NU):
            for n in range(2, NQ):
                if tk == 2 * H * n - 10:
                    load_xq(n)
            if tk == XK_AT:
                load_xk(1)
                for i in range(2):
                    load_xk_half(1, i)
            for c in (2, 3):
                if tk == kvq_tick(c - 2) + 1:
                    kv_load(c)
            for pair in exp_in.get(tk, []):
                exponent(2 * pair + 1)
                exponent(2 * pair)
            for pair in regroup_in.get(tk, []):
                regroup(2 * pair + 1, nc.scalar.copy)
                regroup(2 * pair, nc.scalar.copy)
            if tk - 1 in kv_in:
                kv_leave(*kv_in[tk - 1])
            for pair in tr_in.get(tk, []):
                transposes(2 * pair)
                transposes(2 * pair + 1)
            if tk in kv_in:
                kv_transpose(*kv_in[tk])
            if tk >= H:
                penalties(tk, 0)
                penalties(tk, 1)
                scores(tk, 1)
                scores(tk, 0)
            for g in pv_in.get(tk, []):
                weighted_sum(g)
            for fill, leave in extras.get(tk, []):
                fill()
            for qt in seed_in.get(tk, []):
                seed(qt)
            for qt in range(2, NQT):
                if tk == first_use[qt] - SQUARE_LAG:
                    square(qt, nc.gpsimd)
            if tk >= H:
                leave_psum(tk, 0)
            for g in pv_in.get(tk - 1, []):
                normalise(g)
            for g in quant_in.get(tk, []):
                quantise(g)
            if tk >= H:
                leave_psum(tk, 1)
                row_min(tk)
            for c in range(4):
                if tk == kvq_tick(c):
                    kv_quantise(c)
            for fill, leave in extras.get(tk, []):
                leave()
            if tk == KV_AT[0] + 1:
                wv_regroup()
            if tk == KV_AT[0] + 2:
                wv_quantise()
            for b in range(B):
                if tk == xv_tick(2 * b + 1) + 1:
                    v_quantise(b)
            for g in pv_in.get(tk + 1, []):
                reciprocal(g)
            for g in pv_in.get(tk - NORM_AFTER_PV, []):
                repeat(g)

        a = NU - 8
        on_v = nc.vector.tensor_copy
        transposes(a)
        transposes(a + 1)
        exponent(a + 3)
        exponent(a + 2)
        quantise(NG - 3)
        normalise_on_scalar(NG - 4)
        repeat(NG - 4)
        regroup(a + 1, on_v)
        regroup(a, on_v)
        transposes(a + 2)
        transposes(a + 3)
        reciprocal(NG - 3)
        weighted_sum(NG - 3)
        exponent(a + 5)
        exponent(a + 4)
        regroup(a + 3, on_v)
        regroup(a + 2, on_v)
        quantise(NG - 2)
        normalise(NG - 3)
        repeat(NG - 3)
        transposes(a + 4)
        transposes(a + 5)
        exponent(a + 7)
        exponent(a + 6)
        transposes(a + 7)
        transposes(a + 6)
        weighted_sum(NG - 2)
        regroup(a + 5, on_v)
        reciprocal(NG - 2)
        reciprocal(NG - 1, range(0, 2))
        regroup(a + 4, nc.scalar.copy)
        quantise(NG - 1, range(0, 2))
        regroup(a + 7, nc.scalar.copy)
        quantise(NG - 1, range(3, 4))
        regroup(a + 6, nc.scalar.copy, slice(0, 1))
        regroup(a + 6, on_v, slice(1, 2))
        quantise(NG - 1, range(2, 3))
        reciprocal(NG - 1, range(2, 4))
        last_sum(0)
        last_sum(1)
        last_sum(3)
        last_sum(2)
        normalise_on_scalar(NG - 2)
        repeat(NG - 2, 2)
        finish(0, scale_on_scalar)
        finish(1, scale_on_scalar)
        finish(3, scale_on_scalar)
        finish(2, scale_on_vector)
